import numpy as np
import ml_dtypes


def mxq(x, axis, fmt="e4m3"):
    dtype, down = {"e4m3": (ml_dtypes.float8_e4m3fn, 7), "e5m2": (ml_dtypes.float8_e5m2, 14)}[fmt]
    v = np.moveaxis(np.asarray(x, np.float32).astype(ml_dtypes.bfloat16).astype(np.float64), axis, -1)
    blocks = v.reshape(v.shape[:-1] + (-1, 32))
    amax = np.abs(blocks).max(-1, keepdims=True)
    byte = np.maximum(np.where(amax > 0, np.frexp(amax)[1] - 1 + 127, 0) - down, 1)
    scale = np.exp2(byte - 127.0)
    codes = (blocks / scale).astype(np.float32).astype(dtype).astype(np.float64)
    return np.moveaxis((codes * scale).reshape(v.shape), -1, axis)


WIDE = False


def mx_kscale(k):
    if not WIDE:
        return np.ones(k)
    levels = np.array([10, -10, 5, -5, 0])
    a = np.random.permutation(np.resize(levels, k // 512 * 4)).reshape(k // 512, 4)
    idx = np.arange(k)
    return np.exp2(a[idx // 512, idx % 128 // 32])


BF16 = ml_dtypes.bfloat16


def bf(x):
    return np.asarray(x, np.float32).astype(BF16)


def f64(x):
    return np.asarray(x).astype(np.float64)


B, CIN, CK, CV, COUT, H, W, KS, DA, DB, DC = 4, 512, 512, 512, 128, 64, 64, 3, 1, 2, 4
DILS = (DA, DB, DC)
NN = KS * KS * len(DILS)
P = H * W


def rn(*shape):
    return np.random.standard_normal(shape)


def shifted(a, d, i, j):
    ap = np.pad(a, ((0, 0), (0, 0), (d, d), (d, d)))
    return ap[:, :, i * d:i * d + H, j * d:j * d + W]


def setup_inputs():
    s, t = mx_kscale(CIN), mx_kscale(CV)
    z = 1.2 * rn(B, NN, H, W)
    e = np.exp(z - z.max(axis=1, keepdims=True))
    return {"x": bf(rn(B, CIN, H, W) * s[None, :, None, None]),
            "attn": bf(e / e.sum(axis=1, keepdims=True)),
            "v_w": bf(rn(CV, CIN) / np.sqrt(CIN) / s[None, :] * t[:, None]),
            "v_b": bf(0.2 * rn(CV) * t),
            "w_w": bf(rn(COUT, CV) * 1.5 / np.sqrt(CV) / t[None, :]),
            "w_b": bf(0.3 * rn(COUT))}


def reference(x, attn, v_w, v_b, w_w, w_b):
    value = (mxq(f64(v_w), 1, "e4m3") @ mxq(f64(x).reshape(B, CIN, P), 1, "e4m3")) + f64(v_b)[None, :, None]
    vf = value.reshape(B, CV, H, W)
    a = f64(attn)
    offs = [(d, i, j) for d in DILS for i in range(KS) for j in range(KS)]
    context = sum(a[:, n:n + 1] * shifted(vf, d, i, j) for n, (d, i, j) in enumerate(offs))
    out = (mxq(f64(w_w), 1, "e4m3") @ mxq(context.reshape(B, CV, P), 1, "e4m3")) + f64(w_b)[None, :, None]
    return out.reshape(B, COUT, H, W)

@@ -1,0 +1,239 @@
+from contextlib import ExitStack
+
+import concourse.mybir as mybir
+from concourse.masks import make_identity
+
+FP8X4 = mybir.dt.float8_e4m3fn_x4
+BF16 = mybir.dt.bfloat16
+F32 = mybir.dt.float32
+U32 = mybir.dt.uint32
+U8 = mybir.dt.uint8
+ALU = mybir.AluOpType
+ACT = mybir.ActivationFunctionType
+AX = mybir.AxisListType
+
+B, CIN, CV, COUT, H, W = 4, 512, 512, 128, 64, 64
+P = 128
+DILS = (1, 2, 4)
+PADA = 16
+FLOPS = 2 * B * H * W * (CIN * CV + CV * COUT + 27 * CV)
+
+
+def chains_for(r):
+    side = []
+    for l, d in enumerate(DILS):
+        for j in (0, 2):
+            leaves = [((i - 1) * d, 9 * l + 3 * i + j) for i in range(3) if 0 <= r + (i - 1) * d < H]
+            side.append(((j - 1) * d, leaves[:2], True))
+            if len(leaves) > 2:
+                side.append(((j - 1) * d, leaves[2:], False))
+    mids = [(0, 4)]
+    for l, d in enumerate(DILS):
+        for i in (0, 2):
+            if 0 <= r + (i - 1) * d < H:
+                mids.append(((i - 1) * d, 9 * l + 3 * i + 1))
+    mid = [(0, [leaf], k % 2 == 1) for k, leaf in enumerate(mids)]
+    return mid + side
+
+
+def tile_selfattentionmodulev2_pb_t_kernel(tc, x, attn, v_w, v_b, w_w, w_b, out):
+    nc = tc.nc
+    with ExitStack() as ctx:
+        const = ctx.enter_context(tc.tile_pool(name="const", bufs=1))
+        xraw = ctx.enter_context(tc.tile_pool(name="xraw", bufs=2))
+        xgrp = ctx.enter_context(tc.tile_pool(name="xgrp", bufs=2))
+        xq = ctx.enter_context(tc.tile_pool(name="xq", bufs=2))
+        vpool = ctx.enter_context(tc.tile_pool(name="vpool", bufs=20))
+        ppool = ctx.enter_context(tc.tile_pool(name="ppool", bufs=8))
+        cgrp = ctx.enter_context(tc.tile_pool(name="cgrp", bufs=2))
+        cq = ctx.enter_context(tc.tile_pool(name="cq", bufs=2))
+        opool = ctx.enter_context(tc.tile_pool(name="opool", bufs=2))
+        ps_set = ctx.enter_context(tc.psum_pool(name="ps_set", bufs=2))
+        ps_v = ctx.enter_context(tc.psum_pool(name="ps_v", bufs=2))
+        ps_c = ctx.enter_context(tc.psum_pool(name="ps_c", bufs=2))
+        ps_o = ctx.enter_context(tc.psum_pool(name="ps_o", bufs=1))
+
+        a_raw = const.tile([P, PADA + 4096 + PADA], BF16)
+        nc.vector.memset(a_raw[:], 0.0)
+        a_view = a_raw[:, PADA:PADA + 4096].rearrange("p (q b c) -> p q b c", q=16, b=4)
+        a_src = attn.rearrange("b n (q s) c -> b n q s c", s=4)
+        vw_sb = const.tile([P, 4, CIN], BF16)
+        nc.sync.dma_start(out=vw_sb[:], in_=v_w.rearrange("(p t) k -> p t k", t=4))
+        for b in range(B):
+            for s in range(4):
+                eng = nc.sync if (b * 4 + s) % 2 == 0 else nc.scalar
+                eng.dma_start(out=a_view[s * 32:s * 32 + 27, :, b, :], in_=a_src[b, :, :, s, :])
+        vb_raw = const.tile([P, CV], BF16)
+        nc.scalar.dma_start(out=vb_raw[:], in_=v_b.partition_broadcast(P))
+        w_sb = const.tile([P, CV], BF16)
+        nc.scalar.dma_start(out=w_sb[:], in_=w_w)
+        wb_raw = const.tile([P, 1], BF16)
+        with nc.allow_non_contiguous_dma(reason="one bias value to a partition"):
+            nc.scalar.dma_start(out=wb_raw[:], in_=w_b.rearrange("(p o) -> p o", o=1))
+
+        ident_f = const.tile([P, P], F32)
+        make_identity(nc, ident_f[:])
+        ident_b = const.tile([P, P], BF16)
+        nc.vector.tensor_copy(out=ident_b[:], in_=ident_f[:])
+        i3 = ident_f[:].rearrange("p (b c) -> p b c", b=2)
+        msk = const.tile([P, 16], F32)
+        perm = {0: ident_f[:]}
+        for dc in (-4, -2, -1, 1, 2, 4):
+            pm = const.tile([P, 2, W], F32, name="perm%d" % (dc + 4))
+            e = abs(dc)
+            if dc > 0:
+                nc.vector.tensor_copy(out=pm[:, :, 0:W - e], in_=i3[:, :, e:W])
+                nc.vector.tensor_copy(out=pm[:, :, W - e:W], in_=i3[:, :, 0:e])
+                nc.vector.tensor_reduce(out=msk[:, dc + 4:dc + 5], in_=i3[:, :, e:W], axis=AX.XY, op=ALU.add)
+            else:
+                nc.vector.tensor_copy(out=pm[:, :, e:W], in_=i3[:, :, 0:W - e])
+                nc.vector.tensor_copy(out=pm[:, :, 0:e], in_=i3[:, :, W - e:W])
+                nc.vector.tensor_reduce(out=msk[:, dc + 4:dc + 5], in_=i3[:, :, 0:W - e], axis=AX.XY, op=ALU.add)
+            perm[dc] = pm[:].rearrange("p b c -> p (b c)")
+
+        vw_perm = const.tile([P, 4, 4, P], BF16)
+        nc.vector.tensor_copy(out=vw_perm[:], in_=vw_sb[:].rearrange("a t (p j) -> a t j p", j=4))
+        vw_grp = const.tile([P, 4, P, 4], BF16, align_bytes=64)
+        for t in range(4):
+            tp = ps_set.tile([P, 8, P], BF16, tag="setup")
+            for j in range(4):
+                nc.tensor.transpose(out=tp[:, j, :], in_=vw_perm[:, t, j, :], identity=ident_b[:])
+            nc.vector.tensor_copy(out=vw_grp[:, t], in_=tp[:, 0:4, :].rearrange("p j a -> p a j"))
+        vwc = const.tile([P, CV], U32, align_bytes=64)
+        vws = const.tile([P, CV], U8, align_bytes=64)
+        nc.vector.quantize_mx(out=vwc[:].bitcast(FP8X4), scales=vws[:], in_=vw_grp[:].rearrange("p t a j -> p (t a j)"))
+        vb_bc = const.tile([P, CV], F32)
+        nc.vector.tensor_copy(out=vb_bc[:].rearrange("p (t a) -> p t a", t=4), in_=vb_raw[:].rearrange("p (a t) -> p t a", t=4))
+
+        w_perm = const.tile([P, 4, P], BF16)
+        nc.vector.tensor_copy(out=w_perm[:], in_=w_sb[:].rearrange("a (p j) -> a j p", j=4))
+        w_grp = const.tile([P, P, 4], BF16, align_bytes=64)
+        tpw = ps_set.tile([P, 8, P], BF16, tag="setup")
+        for j in range(4):
+            nc.tensor.transpose(out=tpw[:, j, :], in_=w_perm[:, j, :], identity=ident_b[:])
+        nc.vector.tensor_copy(out=w_grp[:], in_=tpw[:, 0:4, :].rearrange("p j a -> p a j"))
+        wc = const.tile([P, COUT], U32, align_bytes=64)
+        ws = const.tile([P, COUT], U8, align_bytes=64)
+        nc.vector.quantize_mx(out=wc[:].bitcast(FP8X4), scales=ws[:], in_=w_grp[:].rearrange("p a j -> p (a j)"))
+        wb = const.tile([P, 1], F32)
+        nc.vector.tensor_copy(out=wb[:], in_=wb_raw[:])
+
+        a_t = const.tile([P, 2, H, 32], F32)
+        classes = [(0, 1, 9)]
+        for l, d in enumerate(DILS):
+            for j in (0, 2):
+                classes.append(((j - 1) * d, 9 * l + j, 3))
+
+        def prep_attn(bp, h):
+            for dc, n0, cnt in classes:
+                at_ps = ps_set.tile([P, 8, P], BF16, tag="setup")
+                for q in range(8):
+                    s0 = PADA + ((h * 8 + q) * 4 + 2 * bp) * W - dc
+                    nc.tensor.transpose(out=at_ps[:, q, :], in_=a_raw[:, s0:s0 + P], identity=ident_b[:])
+                src = at_ps[:].rearrange("p q (s n) -> p (q s) n", n=32)[:, :, n0:n0 + 3 * cnt - 2:3]
+                dst = a_t[:, bp, h * 32:(h + 1) * 32, n0:n0 + 3 * cnt - 2:3]
+                if dc == 0:
+                    nc.vector.tensor_copy(out=dst, in_=src)
+                else:
+                    nc.vector.tensor_scalar_mul(out=dst, in0=src, scalar1=msk[:, dc + 4:dc + 5])
+            rows = slice(h * 32, (h + 1) * 32)
+            nc.vector.tensor_tensor(out=a_t[:, bp, rows, 4], in0=a_t[:, bp, rows, 4], in1=a_t[:, bp, rows, 13], op=ALU.add)
+            nc.vector.tensor_tensor(out=a_t[:, bp, rows, 4], in0=a_t[:, bp, rows, 4], in1=a_t[:, bp, rows, 22], op=ALU.add)
+
+        for bp in range(2):
+            for h in range(2):
+                prep_attn(bp, h)
+
+        raws = {}
+        vrow = {}
+
+        def produce(kk):
+            bp, k4 = kk // 16, kk % 16
+            if k4 % 2 == 0:
+                raw = xraw.tile([P, 4, 2, 512], BF16)
+                for be in range(2):
+                    nc.sync.dma_start(
+                        out=raw[:, :, be, :],
+                        in_=x[2 * bp + be].rearrange("(p j) r c -> p j (r c)", j=4)[:, :, k4 * 256:k4 * 256 + 512],
+                    )
+                raws[kk // 2] = raw
+            raw = raws[kk // 2]
+            grp = xgrp.tile([P, 4, P, 4], BF16, align_bytes=64)
+            for i in range(4):
+                rl = (k4 % 2) * 4 + i
+                nc.scalar.copy(
+                    out=grp[:, i].rearrange("p (b c) j -> p b c j", b=2),
+                    in_=raw[:, :, :, rl * W:(rl + 1) * W].rearrange("p j b c -> p b c j"),
+                )
+            xc = xq.tile([P, 512], U32, align_bytes=64)
+            xs = xq.tile([P, 512], U8, align_bytes=64)
+            nc.vector.quantize_mx(out=xc[:].bitcast(FP8X4), scales=xs[:], in_=grp[:].rearrange("p i u j -> p (i u j)"))
+            for i in range(4):
+                v_ps = ps_v.tile([P, CV], F32)
+                nc.tensor.matmul_mx(
+                    out=v_ps[:],
+                    lhsT=xc[:, i * P:(i + 1) * P].bitcast(FP8X4),
+                    lhsT_scale=xs[:, i * P:(i + 1) * P],
+                    rhs=vwc[:].bitcast(FP8X4),
+                    rhs_scale=vws[:],
+                    start=True,
+                    stop=True,
+                )
+                vp = vpool.tile([P, CV], F32)
+                nc.vector.tensor_tensor(out=vp[:], in0=v_ps[:], in1=vb_bc[:], op=ALU.add)
+                vrow[(bp, k4 * 4 + i)] = vp
+
+        def dest(bp, r, grp_c):
+            ctx_ps = ps_c.tile([P, 4, P], F32)
+            chains = chains_for(r)
+            last = len(chains) - 1
+            for ci, (dc, leaves, on_scalar) in enumerate(chains):
+                pt = ppool.tile([P, CV], F32)
+                dr0, n0 = leaves[0]
+                if on_scalar:
+                    nc.scalar.activation(out=pt[:], in_=vrow[(bp, r + dr0)][:], func=ACT.Copy, scale=a_t[:, bp, r, n0:n0 + 1])
+                else:
+                    nc.vector.tensor_scalar_mul(out=pt[:], in0=vrow[(bp, r + dr0)][:], scalar1=a_t[:, bp, r, n0:n0 + 1])
+                for dr, n in leaves[1:]:
+                    nc.vector.scalar_tensor_tensor(
+                        out=pt[:], in0=vrow[(bp, r + dr)][:], scalar=a_t[:, bp, r, n:n + 1], in1=pt[:],
+                        op0=ALU.mult, op1=ALU.add,
+                    )
+                for t in range(4):
+                    nc.tensor.matmul(
+                        out=ctx_ps[:, t, :], lhsT=pt[:, t * P:(t + 1) * P], rhs=perm[dc],
+                        start=(ci == 0 and t == 0), stop=(ci == last and t == 3), is_transpose=True,
+                    )
+            nc.scalar.copy(out=grp_c[:, r % 4], in_=ctx_ps[:].rearrange("p t u -> p u t"))
+
+        def finish(bp, r0, grp_c):
+            cc = cq.tile([P, 512], U32, align_bytes=64)
+            cs = cq.tile([P, 512], U8, align_bytes=64)
+            nc.vector.quantize_mx(out=cc[:].bitcast(FP8X4), scales=cs[:], in_=grp_c[:].rearrange("p i u t -> p (i u t)"))
+            o_ps = ps_o.tile([P, 512], F32)
+            nc.tensor.matmul_mx(
+                out=o_ps[:], lhsT=wc[:].bitcast(FP8X4), lhsT_scale=ws[:], rhs=cc[:].bitcast(FP8X4), rhs_scale=cs[:],
+                start=True, stop=True,
+            )
+            o_sb = opool.tile([P, 2, 4, W], F32)
+            nc.scalar.activation(
+                out=o_sb[:].rearrange("p b r c -> p r b c"),
+                in_=o_ps[:].rearrange("p (r b c) -> p r b c", r=4, b=2),
+                func=ACT.Identity, bias=wb[:, 0:1],
+            )
+            nc.sync.dma_start(
+                out=out[2 * bp:2 * bp + 2, :, r0:r0 + 4, :].rearrange("b o r c -> o b (r c)"),
+                in_=o_sb[:].rearrange("p b r c -> p b (r c)"),
+            )
+
+        produce(0)
+        produce(1)
+        for g in range(2 * H):
+            bp, r = g // H, g % H
+            if g % 4 == 0:
+                if g // 4 + 2 < 32:
+                    produce(g // 4 + 2)
+                grp_c = cgrp.tile([P, 4, P, 4], BF16, align_bytes=64)
+            dest(bp, r, grp_c)
+            if g % 4 == 3:
+                finish(bp, r - 3, grp_c)

@@ -20,20 +20,17 @@ FLOPS = 2 * B * H * W * (CIN * CV + CV * COUT + 27 * CV)
 
 
 def chains_for(r):
-    side = []
+    def rows(l, j, picks):
+        d = DILS[l]
+        return [((i - 1) * d, 9 * l + 3 * i + j) for i in picks if 0 <= r + (i - 1) * d < H]
+
+    chains = []
     for l, d in enumerate(DILS):
+        chains.append((0, ([(0, 4)] if l == 0 else []) + rows(l, 1, (0, 2)), l > 0))
         for j in (0, 2):
-            leaves = [((i - 1) * d, 9 * l + 3 * i + j) for i in range(3) if 0 <= r + (i - 1) * d < H]
-            side.append(((j - 1) * d, leaves[:2], True))
-            if len(leaves) > 2:
-                side.append(((j - 1) * d, leaves[2:], False))
-    mids = [(0, 4)]
-    for l, d in enumerate(DILS):
-        for i in (0, 2):
-            if 0 <= r + (i - 1) * d < H:
-                mids.append(((i - 1) * d, 9 * l + 3 * i + 1))
-    mid = [(0, [leaf], k % 2 == 1) for k, leaf in enumerate(mids)]
-    return mid + side
+            chains.append(((j - 1) * d, rows(l, j, (1, 0)), True))
+            chains.append(((j - 1) * d, rows(l, j, (2,)), j == 0))
+    return [c for c in chains if c[1]]
 
 
 def tile_selfattentionmodulev2_pb_t_kernel(tc, x, attn, v_w, v_b, w_w, w_b, out):
@@ -140,9 +137,7 @@ def tile_selfattentionmodulev2_pb_t_kernel(tc, x, attn, v_w, v_b, w_w, w_b, out)
             nc.vector.tensor_tensor(out=a_t[:, bp, rows, 4], in0=a_t[:, bp, rows, 4], in1=a_t[:, bp, rows, 13], op=ALU.add)
             nc.vector.tensor_tensor(out=a_t[:, bp, rows, 4], in0=a_t[:, bp, rows, 4], in1=a_t[:, bp, rows, 22], op=ALU.add)
 
-        for bp in range(2):
-            for h in range(2):
-                prep_attn(bp, h)
+        prep_attn(0, 0)
 
         raws = {}
         vrow = {}
@@ -234,6 +229,8 @@ def tile_selfattentionmodulev2_pb_t_kernel(tc, x, attn, v_w, v_b, w_w, w_b, out)
                 if g // 4 + 2 < 32:
                     produce(g // 4 + 2)
                 grp_c = cgrp.tile([P, 4, P, 4], BF16, align_bytes=64)
+            if g % 32 == 8 and g < 96:
+                prep_attn((g // 32 + 1) // 2, (g // 32 + 1) % 2)
             dest(bp, r, grp_c)
             if g % 4 == 3:
                 finish(bp, r - 3, grp_c)

@@ -16,21 +16,32 @@ B, CIN, CV, COUT, H, W = 4, 512, 512, 128, 64, 64
 P = 128
 DILS = (1, 2, 4)
 PADA = 16
+LEVEL = {1: 0, 2: 1, 4: 2}
+VECTOR_ROWS = (0, -1)
+SCALAR_ROWS = (1, 4)
+BIAS = (None, None)
+LEAD_LOAD, LEAD_GROUP, LEAD_QUANT, LEAD_VALUE = 16, 10, 6, 4
 FLOPS = 2 * B * H * W * (CIN * CV + CV * COUT + 27 * CV)
 
 
 def chains_for(r):
-    def rows(l, j, picks):
-        d = DILS[l]
-        return [((i - 1) * d, 9 * l + 3 * i + j) for i in picks if 0 <= r + (i - 1) * d < H]
-
     chains = []
-    for l, d in enumerate(DILS):
-        chains.append((0, ([(0, 4)] if l == 0 else []) + rows(l, 1, (0, 2)), l > 0))
-        for j in (0, 2):
-            chains.append(((j - 1) * d, rows(l, j, (1, 0)), True))
-            chains.append(((j - 1) * d, rows(l, j, (2,)), j == 0))
-    return [c for c in chains if c[1]]
+    for dc in (0, -1, 1, -2, 2, -4, 4):
+        if dc == 0:
+            terms = [(0, 4)] + [((i - 1) * d, 9 * l + 3 * i + 1) for l, d in enumerate(DILS) for i in (0, 2)]
+        else:
+            d = abs(dc)
+            terms = [((i - 1) * d, 9 * LEVEL[d] + 3 * i + (0 if dc < 0 else 2)) for i in range(3)]
+        terms = [t for t in terms if 0 <= r + t[0] < H]
+        added = [t for t in terms if t[0] in VECTOR_ROWS]
+        heads = [t for t in terms if t[0] not in VECTOR_ROWS]
+        if dc == 0:
+            heads.append(BIAS)
+        if not heads:
+            heads, added = added[:1], added[1:]
+        for k, hd in enumerate(heads):
+            chains.append((dc, hd, added if k == 0 else []))
+    return chains
 
 
 def tile_selfattentionmodulev2_pb_t_kernel(tc, x, attn, v_w, v_b, w_w, w_b, out):
@@ -39,16 +50,17 @@ def tile_selfattentionmodulev2_pb_t_kernel(tc, x, attn, v_w, v_b, w_w, w_b, out)
         const = ctx.enter_context(tc.tile_pool(name="const", bufs=1))
         xraw = ctx.enter_context(tc.tile_pool(name="xraw", bufs=2))
         xgrp = ctx.enter_context(tc.tile_pool(name="xgrp", bufs=2))
-        xq = ctx.enter_context(tc.tile_pool(name="xq", bufs=2))
-        vpool = ctx.enter_context(tc.tile_pool(name="vpool", bufs=20))
-        ppool = ctx.enter_context(tc.tile_pool(name="ppool", bufs=8))
+        xq = ctx.enter_context(tc.tile_pool(name="xq", bufs=4))
+        vpool = ctx.enter_context(tc.tile_pool(name="vpool", bufs=12))
+        ppool = ctx.enter_context(tc.tile_pool(name="ppool", bufs=12))
+        scr = ctx.enter_context(tc.tile_pool(name="scr", bufs=1))
         cgrp = ctx.enter_context(tc.tile_pool(name="cgrp", bufs=2))
         cq = ctx.enter_context(tc.tile_pool(name="cq", bufs=2))
         opool = ctx.enter_context(tc.tile_pool(name="opool", bufs=2))
         ps_set = ctx.enter_context(tc.psum_pool(name="ps_set", bufs=2))
         ps_v = ctx.enter_context(tc.psum_pool(name="ps_v", bufs=2))
+        ps_s = ctx.enter_context(tc.psum_pool(name="ps_s", bufs=2))
         ps_c = ctx.enter_context(tc.psum_pool(name="ps_c", bufs=2))
-        ps_o = ctx.enter_context(tc.psum_pool(name="ps_o", bufs=1))
 
         a_raw = const.tile([P, PADA + 4096 + PADA], BF16)
         nc.vector.memset(a_raw[:], 0.0)
@@ -121,77 +133,99 @@ def tile_selfattentionmodulev2_pb_t_kernel(tc, x, attn, v_w, v_b, w_w, w_b, out)
             for j in (0, 2):
                 classes.append(((j - 1) * d, 9 * l + j, 3))
 
+        s_t = const.tile([P, 2, H], F32)
+
         def prep_attn(bp, h):
+            rows = slice(h * 32, (h + 1) * 32)
             for dc, n0, cnt in classes:
                 at_ps = ps_set.tile([P, 8, P], BF16, tag="setup")
                 for q in range(8):
                     s0 = PADA + ((h * 8 + q) * 4 + 2 * bp) * W - dc
                     nc.tensor.transpose(out=at_ps[:, q, :], in_=a_raw[:, s0:s0 + P], identity=ident_b[:])
-                src = at_ps[:].rearrange("p q (s n) -> p (q s) n", n=32)[:, :, n0:n0 + 3 * cnt - 2:3]
-                dst = a_t[:, bp, h * 32:(h + 1) * 32, n0:n0 + 3 * cnt - 2:3]
+                at_v = at_ps[:].rearrange("p q (s n) -> p (q s) n", n=32)
+                pick = slice(n0, n0 + 3 * cnt - 2, 3)
                 if dc == 0:
-                    nc.vector.tensor_copy(out=dst, in_=src)
+                    nc.vector.tensor_copy(out=a_t[:, bp, rows, pick], in_=at_v[:, :, pick])
+                    a_u = scr.tile([P, 32, 32], F32)
+                    for dc2, m0, cnt2 in classes:
+                        pick2 = slice(m0, m0 + 3 * cnt2 - 2, 3)
+                        if dc2 == 0:
+                            nc.vector.tensor_copy(out=a_u[:, :, pick2], in_=at_v[:, :, pick2])
+                        else:
+                            nc.vector.tensor_scalar_mul(out=a_u[:, :, pick2], in0=at_v[:, :, pick2], scalar1=msk[:, 4 - dc2:5 - dc2])
+                    for l, d in enumerate(DILS):
+                        if h == 0:
+                            nc.vector.memset(a_u[:, 0:d, 9 * l:9 * l + 3], 0.0)
+                        else:
+                            nc.vector.memset(a_u[:, 32 - d:32, 9 * l + 6:9 * l + 9], 0.0)
+                    nc.vector.tensor_reduce(out=s_t[:, bp, rows], in_=a_u[:, :, 0:27], axis=AX.X, op=ALU.add)
                 else:
-                    nc.vector.tensor_scalar_mul(out=dst, in0=src, scalar1=msk[:, dc + 4:dc + 5])
-            rows = slice(h * 32, (h + 1) * 32)
+                    nc.vector.tensor_scalar_mul(out=a_t[:, bp, rows, pick], in0=at_v[:, :, pick], scalar1=msk[:, dc + 4:dc + 5])
             nc.vector.tensor_tensor(out=a_t[:, bp, rows, 4], in0=a_t[:, bp, rows, 4], in1=a_t[:, bp, rows, 13], op=ALU.add)
             nc.vector.tensor_tensor(out=a_t[:, bp, rows, 4], in0=a_t[:, bp, rows, 4], in1=a_t[:, bp, rows, 22], op=ALU.add)
 
         prep_attn(0, 0)
 
         raws = {}
+        grps = {}
+        codes = {}
         vrow = {}
 
-        def produce(kk):
-            bp, k4 = kk // 16, kk % 16
-            if k4 % 2 == 0:
-                raw = xraw.tile([P, 4, 2, 512], BF16)
-                for be in range(2):
-                    nc.sync.dma_start(
-                        out=raw[:, :, be, :],
-                        in_=x[2 * bp + be].rearrange("(p j) r c -> p j (r c)", j=4)[:, :, k4 * 256:k4 * 256 + 512],
-                    )
-                raws[kk // 2] = raw
-            raw = raws[kk // 2]
-            grp = xgrp.tile([P, 4, P, 4], BF16, align_bytes=64)
-            for i in range(4):
-                rl = (k4 % 2) * 4 + i
-                nc.scalar.copy(
-                    out=grp[:, i].rearrange("p (b c) j -> p b c j", b=2),
-                    in_=raw[:, :, :, rl * W:(rl + 1) * W].rearrange("p j b c -> p b c j"),
+        def load(q):
+            raw = xraw.tile([P, 4, 2, 512], BF16)
+            for be in range(2):
+                nc.sync.dma_start(
+                    out=raw[:, :, be, :],
+                    in_=x[2 * (q // H) + be].rearrange("(p j) r c -> p j (r c)", j=4)[:, :, (q % H) * W:(q % H) * W + 512],
                 )
+            raws[q // 8] = raw
+
+        def regroup(q):
+            if q % 4 == 0:
+                grp = xgrp.tile([P, 4, P, 4], BF16, align_bytes=64)
+                grps[q // 4] = grp
+            nc.scalar.copy(
+                out=grps[q // 4][:, q % 4].rearrange("p (b c) j -> p b c j", b=2),
+                in_=raws[q // 8][:, :, :, (q % 8) * W:(q % 8 + 1) * W].rearrange("p j b c -> p b c j"),
+            )
+
+        def quantise(k):
             xc = xq.tile([P, 512], U32, align_bytes=64)
             xs = xq.tile([P, 512], U8, align_bytes=64)
-            nc.vector.quantize_mx(out=xc[:].bitcast(FP8X4), scales=xs[:], in_=grp[:].rearrange("p i u j -> p (i u j)"))
-            for i in range(4):
-                v_ps = ps_v.tile([P, CV], F32)
-                nc.tensor.matmul_mx(
-                    out=v_ps[:],
-                    lhsT=xc[:, i * P:(i + 1) * P].bitcast(FP8X4),
-                    lhsT_scale=xs[:, i * P:(i + 1) * P],
-                    rhs=vwc[:].bitcast(FP8X4),
-                    rhs_scale=vws[:],
-                    start=True,
-                    stop=True,
-                )
-                vp = vpool.tile([P, CV], F32)
-                nc.vector.tensor_tensor(out=vp[:], in0=v_ps[:], in1=vb_bc[:], op=ALU.add)
-                vrow[(bp, k4 * 4 + i)] = vp
+            nc.vector.quantize_mx(out=xc[:].bitcast(FP8X4), scales=xs[:], in_=grps[k][:].rearrange("p i u j -> p (i u j)"))
+            codes[k] = (xc, xs)
 
-        def dest(bp, r, grp_c):
+        def value_pass(pool, q):
+            xc, xs = codes[q // 4]
+            cols = slice((q % 4) * P, (q % 4 + 1) * P)
+            bank = pool.tile([P, CV], F32)
+            nc.tensor.matmul_mx(
+                out=bank[:], lhsT=xc[:, cols].bitcast(FP8X4), lhsT_scale=xs[:, cols],
+                rhs=vwc[:].bitcast(FP8X4), rhs_scale=vws[:], start=True, stop=True,
+            )
+            return bank
+
+        def dest(g, banks, grp_c):
+            bp, r = g // H, g % H
             ctx_ps = ps_c.tile([P, 4, P], F32)
             chains = chains_for(r)
             last = len(chains) - 1
-            for ci, (dc, leaves, on_scalar) in enumerate(chains):
+            for ci, (dc, (dr, n), added) in enumerate(chains):
                 pt = ppool.tile([P, CV], F32)
-                dr0, n0 = leaves[0]
-                if on_scalar:
-                    nc.scalar.activation(out=pt[:], in_=vrow[(bp, r + dr0)][:], func=ACT.Copy, scale=a_t[:, bp, r, n0:n0 + 1])
+                if dr is None:
+                    nc.scalar.activation(out=pt[:], in_=vb_bc[:], func=ACT.Copy, scale=s_t[:, bp, r:r + 1])
+                elif dr in SCALAR_ROWS:
+                    nc.scalar.activation(out=pt[:], in_=banks[dr][:], func=ACT.Copy, scale=a_t[:, bp, r, n:n + 1])
+                elif dr in VECTOR_ROWS:
+                    nc.vector.tensor_scalar_mul(out=pt[:], in0=banks[dr][:], scalar1=a_t[:, bp, r, n:n + 1])
                 else:
-                    nc.vector.tensor_scalar_mul(out=pt[:], in0=vrow[(bp, r + dr0)][:], scalar1=a_t[:, bp, r, n0:n0 + 1])
-                for dr, n in leaves[1:]:
+                    nc.gpsimd.tensor_scalar(
+                        out=pt[:], in0=vrow[g + dr][:], scalar1=a_t[:, bp, r, n:n + 1], scalar2=0.0,
+                        op0=ALU.mult, op1=ALU.add,
+                    )
+                for dr2, n2 in added:
                     nc.vector.scalar_tensor_tensor(
-                        out=pt[:], in0=vrow[(bp, r + dr)][:], scalar=a_t[:, bp, r, n:n + 1], in1=pt[:],
+                        out=pt[:], in0=banks[dr2][:], scalar=a_t[:, bp, r, n2:n2 + 1], in1=pt[:],
                         op0=ALU.mult, op1=ALU.add,
                     )
                 for t in range(4):
@@ -205,7 +239,7 @@ def tile_selfattentionmodulev2_pb_t_kernel(tc, x, attn, v_w, v_b, w_w, w_b, out)
             cc = cq.tile([P, 512], U32, align_bytes=64)
             cs = cq.tile([P, 512], U8, align_bytes=64)
             nc.vector.quantize_mx(out=cc[:].bitcast(FP8X4), scales=cs[:], in_=grp_c[:].rearrange("p i u t -> p (i u t)"))
-            o_ps = ps_o.tile([P, 512], F32)
+            o_ps = ps_set.tile([P, 512], F32, tag="setup")
             nc.tensor.matmul_mx(
                 out=o_ps[:], lhsT=wc[:].bitcast(FP8X4), lhsT_scale=ws[:], rhs=cc[:].bitcast(FP8X4), rhs_scale=cs[:],
                 start=True, stop=True,
@@ -221,16 +255,31 @@ def tile_selfattentionmodulev2_pb_t_kernel(tc, x, attn, v_w, v_b, w_w, w_b, out)
                 in_=o_sb[:].rearrange("p b r c -> p b (r c)"),
             )
 
-        produce(0)
-        produce(1)
-        for g in range(2 * H):
-            bp, r = g // H, g % H
+        rows_all = 2 * H
+        for g in range(-LEAD_LOAD, rows_all):
+            if g + LEAD_LOAD < rows_all and (g + LEAD_LOAD) % 8 == 0:
+                load(g + LEAD_LOAD)
+            if 0 <= g + LEAD_GROUP < rows_all:
+                regroup(g + LEAD_GROUP)
+            if 0 <= g + LEAD_QUANT < rows_all and (g + LEAD_QUANT) % 4 == 0:
+                quantise((g + LEAD_QUANT) // 4)
+            banks = {}
+            if 0 <= g + LEAD_VALUE < rows_all:
+                banks[4] = value_pass(ps_s, g + LEAD_VALUE)
+                vp = vpool.tile([P, CV], F32)
+                nc.scalar.copy(out=vp[:], in_=banks[4][:])
+                vrow[g + LEAD_VALUE] = vp
+            if g < 0:
+                continue
             if g % 4 == 0:
-                if g // 4 + 2 < 32:
-                    produce(g // 4 + 2)
                 grp_c = cgrp.tile([P, 4, P, 4], BF16, align_bytes=64)
             if g % 32 == 8 and g < 96:
                 prep_attn((g // 32 + 1) // 2, (g // 32 + 1) % 2)
-            dest(bp, r, grp_c)
+            banks[0] = value_pass(ps_v, g)
+            if g % H > 0:
+                banks[-1] = value_pass(ps_v, g - 1)
+            if g % H < H - 1:
+                banks[1] = value_pass(ps_s, g + 1)
+            dest(g, banks, grp_c)
             if g % 4 == 3:
-                finish(bp, r - 3, grp_c)
+                finish(g // H, g % H - 3, grp_c)

@@ -16,32 +16,21 @@ B, CIN, CV, COUT, H, W = 4, 512, 512, 128, 64, 64
 P = 128
 DILS = (1, 2, 4)
 PADA = 16
-LEVEL = {1: 0, 2: 1, 4: 2}
-VECTOR_ROWS = (0, -1)
-SCALAR_ROWS = (1, 4)
-BIAS = (None, None)
-LEAD_LOAD, LEAD_GROUP, LEAD_QUANT, LEAD_VALUE = 16, 10, 6, 4
 FLOPS = 2 * B * H * W * (CIN * CV + CV * COUT + 27 * CV)
 
 
 def chains_for(r):
+    def rows(l, j, picks):
+        d = DILS[l]
+        return [((i - 1) * d, 9 * l + 3 * i + j) for i in picks if 0 <= r + (i - 1) * d < H]
+
     chains = []
-    for dc in (0, -1, 1, -2, 2, -4, 4):
-        if dc == 0:
-            terms = [(0, 4)] + [((i - 1) * d, 9 * l + 3 * i + 1) for l, d in enumerate(DILS) for i in (0, 2)]
-        else:
-            d = abs(dc)
-            terms = [((i - 1) * d, 9 * LEVEL[d] + 3 * i + (0 if dc < 0 else 2)) for i in range(3)]
-        terms = [t for t in terms if 0 <= r + t[0] < H]
-        added = [t for t in terms if t[0] in VECTOR_ROWS]
-        heads = [t for t in terms if t[0] not in VECTOR_ROWS]
-        if dc == 0:
-            heads.append(BIAS)
-        if not heads:
-            heads, added = added[:1], added[1:]
-        for k, hd in enumerate(heads):
-            chains.append((dc, hd, added if k == 0 else []))
-    return chains
+    for l, d in enumerate(DILS):
+        chains.append((0, ([(0, 4)] if l == 0 else []) + rows(l, 1, (0, 2)), True))
+        for j in (0, 2):
+            chains.append(((j - 1) * d, rows(l, j, (1, 0)), True))
+            chains.append(((j - 1) * d, rows(l, j, (2,)), False))
+    return [c for c in chains if c[1]]
 
 
 def tile_selfattentionmodulev2_pb_t_kernel(tc, x, attn, v_w, v_b, w_w, w_b, out):
@@ -50,17 +39,16 @@ def tile_selfattentionmodulev2_pb_t_kernel(tc, x, attn, v_w, v_b, w_w, w_b, out)
         const = ctx.enter_context(tc.tile_pool(name="const", bufs=1))
         xraw = ctx.enter_context(tc.tile_pool(name="xraw", bufs=2))
         xgrp = ctx.enter_context(tc.tile_pool(name="xgrp", bufs=2))
-        xq = ctx.enter_context(tc.tile_pool(name="xq", bufs=4))
-        vpool = ctx.enter_context(tc.tile_pool(name="vpool", bufs=12))
-        ppool = ctx.enter_context(tc.tile_pool(name="ppool", bufs=12))
-        scr = ctx.enter_context(tc.tile_pool(name="scr", bufs=1))
+        xq = ctx.enter_context(tc.tile_pool(name="xq", bufs=2))
+        vpool = ctx.enter_context(tc.tile_pool(name="vpool", bufs=20))
+        ppool = ctx.enter_context(tc.tile_pool(name="ppool", bufs=8))
         cgrp = ctx.enter_context(tc.tile_pool(name="cgrp", bufs=2))
         cq = ctx.enter_context(tc.tile_pool(name="cq", bufs=2))
         opool = ctx.enter_context(tc.tile_pool(name="opool", bufs=2))
         ps_set = ctx.enter_context(tc.psum_pool(name="ps_set", bufs=2))
         ps_v = ctx.enter_context(tc.psum_pool(name="ps_v", bufs=2))
-        ps_s = ctx.enter_context(tc.psum_pool(name="ps_s", bufs=2))
         ps_c = ctx.enter_context(tc.psum_pool(name="ps_c", bufs=2))
+        ps_o = ctx.enter_context(tc.psum_pool(name="ps_o", bufs=1))
 
         a_raw = const.tile([P, PADA + 4096 + PADA], BF16)
         nc.vector.memset(a_raw[:], 0.0)
@@ -133,99 +121,77 @@ def tile_selfattentionmodulev2_pb_t_kernel(tc, x, attn, v_w, v_b, w_w, w_b, out)
             for j in (0, 2):
                 classes.append(((j - 1) * d, 9 * l + j, 3))
 
-        s_t = const.tile([P, 2, H], F32)
-
         def prep_attn(bp, h):
-            rows = slice(h * 32, (h + 1) * 32)
             for dc, n0, cnt in classes:
                 at_ps = ps_set.tile([P, 8, P], BF16, tag="setup")
                 for q in range(8):
                     s0 = PADA + ((h * 8 + q) * 4 + 2 * bp) * W - dc
                     nc.tensor.transpose(out=at_ps[:, q, :], in_=a_raw[:, s0:s0 + P], identity=ident_b[:])
-                at_v = at_ps[:].rearrange("p q (s n) -> p (q s) n", n=32)
-                pick = slice(n0, n0 + 3 * cnt - 2, 3)
+                src = at_ps[:].rearrange("p q (s n) -> p (q s) n", n=32)[:, :, n0:n0 + 3 * cnt - 2:3]
+                dst = a_t[:, bp, h * 32:(h + 1) * 32, n0:n0 + 3 * cnt - 2:3]
                 if dc == 0:
-                    nc.vector.tensor_copy(out=a_t[:, bp, rows, pick], in_=at_v[:, :, pick])
-                    a_u = scr.tile([P, 32, 32], F32)
-                    for dc2, m0, cnt2 in classes:
-                        pick2 = slice(m0, m0 + 3 * cnt2 - 2, 3)
-                        if dc2 == 0:
-                            nc.vector.tensor_copy(out=a_u[:, :, pick2], in_=at_v[:, :, pick2])
-                        else:
-                            nc.vector.tensor_scalar_mul(out=a_u[:, :, pick2], in0=at_v[:, :, pick2], scalar1=msk[:, 4 - dc2:5 - dc2])
-                    for l, d in enumerate(DILS):
-                        if h == 0:
-                            nc.vector.memset(a_u[:, 0:d, 9 * l:9 * l + 3], 0.0)
-                        else:
-                            nc.vector.memset(a_u[:, 32 - d:32, 9 * l + 6:9 * l + 9], 0.0)
-                    nc.vector.tensor_reduce(out=s_t[:, bp, rows], in_=a_u[:, :, 0:27], axis=AX.X, op=ALU.add)
+                    nc.vector.tensor_copy(out=dst, in_=src)
                 else:
-                    nc.vector.tensor_scalar_mul(out=a_t[:, bp, rows, pick], in0=at_v[:, :, pick], scalar1=msk[:, dc + 4:dc + 5])
+                    nc.vector.tensor_scalar_mul(out=dst, in0=src, scalar1=msk[:, dc + 4:dc + 5])
+            rows = slice(h * 32, (h + 1) * 32)
             nc.vector.tensor_tensor(out=a_t[:, bp, rows, 4], in0=a_t[:, bp, rows, 4], in1=a_t[:, bp, rows, 13], op=ALU.add)
             nc.vector.tensor_tensor(out=a_t[:, bp, rows, 4], in0=a_t[:, bp, rows, 4], in1=a_t[:, bp, rows, 22], op=ALU.add)
 
         prep_attn(0, 0)
 
         raws = {}
-        grps = {}
-        codes = {}
         vrow = {}
 
-        def load(q):
-            raw = xraw.tile([P, 4, 2, 512], BF16)
-            for be in range(2):
-                nc.sync.dma_start(
-                    out=raw[:, :, be, :],
-                    in_=x[2 * (q // H) + be].rearrange("(p j) r c -> p j (r c)", j=4)[:, :, (q % H) * W:(q % H) * W + 512],
+        def produce(kk):
+            bp, k4 = kk // 16, kk % 16
+            if k4 % 2 == 0:
+                raw = xraw.tile([P, 4, 2, 512], BF16)
+                for be in range(2):
+                    nc.sync.dma_start(
+                        out=raw[:, :, be, :],
+                        in_=x[2 * bp + be].rearrange("(p j) r c -> p j (r c)", j=4)[:, :, k4 * 256:k4 * 256 + 512],
+                    )
+                raws[kk // 2] = raw
+            raw = raws[kk // 2]
+            grp = xgrp.tile([P, 4, P, 4], BF16, align_bytes=64)
+            for i in range(4):
+                rl = (k4 % 2) * 4 + i
+                nc.scalar.copy(
+                    out=grp[:, i].rearrange("p (b c) j -> p b c j", b=2),
+                    in_=raw[:, :, :, rl * W:(rl + 1) * W].rearrange("p j b c -> p b c j"),
                 )
-            raws[q // 8] = raw
-
-        def regroup(q):
-            if q % 4 == 0:
-                grp = xgrp.tile([P, 4, P, 4], BF16, align_bytes=64)
-                grps[q // 4] = grp
-            nc.scalar.copy(
-                out=grps[q // 4][:, q % 4].rearrange("p (b c) j -> p b c j", b=2),
-                in_=raws[q // 8][:, :, :, (q % 8) * W:(q % 8 + 1) * W].rearrange("p j b c -> p b c j"),
-            )
-
-        def quantise(k):
             xc = xq.tile([P, 512], U32, align_bytes=64)
             xs = xq.tile([P, 512], U8, align_bytes=64)
-            nc.vector.quantize_mx(out=xc[:].bitcast(FP8X4), scales=xs[:], in_=grps[k][:].rearrange("p i u j -> p (i u j)"))
-            codes[k] = (xc, xs)
+            nc.vector.quantize_mx(out=xc[:].bitcast(FP8X4), scales=xs[:], in_=grp[:].rearrange("p i u j -> p (i u j)"))
+            for i in range(4):
+                v_ps = ps_v.tile([P, CV], F32)
+                nc.tensor.matmul_mx(
+                    out=v_ps[:],
+                    lhsT=xc[:, i * P:(i + 1) * P].bitcast(FP8X4),
+                    lhsT_scale=xs[:, i * P:(i + 1) * P],
+                    rhs=vwc[:].bitcast(FP8X4),
+                    rhs_scale=vws[:],
+                    start=True,
+                    stop=True,
+                )
+                vp = vpool.tile([P, CV], F32)
+                nc.vector.tensor_tensor(out=vp[:], in0=v_ps[:], in1=vb_bc[:], op=ALU.add)
+                vrow[(bp, k4 * 4 + i)] = vp
 
-        def value_pass(pool, q):
-            xc, xs = codes[q // 4]
-            cols = slice((q % 4) * P, (q % 4 + 1) * P)
-            bank = pool.tile([P, CV], F32)
-            nc.tensor.matmul_mx(
-                out=bank[:], lhsT=xc[:, cols].bitcast(FP8X4), lhsT_scale=xs[:, cols],
-                rhs=vwc[:].bitcast(FP8X4), rhs_scale=vws[:], start=True, stop=True,
-            )
-            return bank
-
-        def dest(g, banks, grp_c):
-            bp, r = g // H, g % H
+        def dest(bp, r, grp_c):
             ctx_ps = ps_c.tile([P, 4, P], F32)
             chains = chains_for(r)
             last = len(chains) - 1
-            for ci, (dc, (dr, n), added) in enumerate(chains):
+            for ci, (dc, leaves, on_scalar) in enumerate(chains):
                 pt = ppool.tile([P, CV], F32)
-                if dr is None:
-                    nc.scalar.activation(out=pt[:], in_=vb_bc[:], func=ACT.Copy, scale=s_t[:, bp, r:r + 1])
-                elif dr in SCALAR_ROWS:
-                    nc.scalar.activation(out=pt[:], in_=banks[dr][:], func=ACT.Copy, scale=a_t[:, bp, r, n:n + 1])
-                elif dr in VECTOR_ROWS:
-                    nc.vector.tensor_scalar_mul(out=pt[:], in0=banks[dr][:], scalar1=a_t[:, bp, r, n:n + 1])
+                dr0, n0 = leaves[0]
+                if on_scalar:
+                    nc.scalar.activation(out=pt[:], in_=vrow[(bp, r + dr0)][:], func=ACT.Copy, scale=a_t[:, bp, r, n0:n0 + 1])
                 else:
-                    nc.gpsimd.tensor_scalar(
-                        out=pt[:], in0=vrow[g + dr][:], scalar1=a_t[:, bp, r, n:n + 1], scalar2=0.0,
-                        op0=ALU.mult, op1=ALU.add,
-                    )
-                for dr2, n2 in added:
+                    nc.vector.tensor_scalar_mul(out=pt[:], in0=vrow[(bp, r + dr0)][:], scalar1=a_t[:, bp, r, n0:n0 + 1])
+                for dr, n in leaves[1:]:
                     nc.vector.scalar_tensor_tensor(
-                        out=pt[:], in0=banks[dr2][:], scalar=a_t[:, bp, r, n2:n2 + 1], in1=pt[:],
+                        out=pt[:], in0=vrow[(bp, r + dr)][:], scalar=a_t[:, bp, r, n:n + 1], in1=pt[:],
                         op0=ALU.mult, op1=ALU.add,
                     )
                 for t in range(4):
@@ -239,7 +205,7 @@ def tile_selfattentionmodulev2_pb_t_kernel(tc, x, attn, v_w, v_b, w_w, w_b, out)
             cc = cq.tile([P, 512], U32, align_bytes=64)
             cs = cq.tile([P, 512], U8, align_bytes=64)
             nc.vector.quantize_mx(out=cc[:].bitcast(FP8X4), scales=cs[:], in_=grp_c[:].rearrange("p i u t -> p (i u t)"))
-            o_ps = ps_set.tile([P, 512], F32, tag="setup")
+            o_ps = ps_o.tile([P, 512], F32)
             nc.tensor.matmul_mx(
                 out=o_ps[:], lhsT=wc[:].bitcast(FP8X4), lhsT_scale=ws[:], rhs=cc[:].bitcast(FP8X4), rhs_scale=cs[:],
                 start=True, stop=True,
@@ -255,31 +221,16 @@ def tile_selfattentionmodulev2_pb_t_kernel(tc, x, attn, v_w, v_b, w_w, w_b, out)
                 in_=o_sb[:].rearrange("p b r c -> p b (r c)"),
             )
 
-        rows_all = 2 * H
-        for g in range(-LEAD_LOAD, rows_all):
-            if g + LEAD_LOAD < rows_all and (g + LEAD_LOAD) % 8 == 0:
-                load(g + LEAD_LOAD)
-            if 0 <= g + LEAD_GROUP < rows_all:
-                regroup(g + LEAD_GROUP)
-            if 0 <= g + LEAD_QUANT < rows_all and (g + LEAD_QUANT) % 4 == 0:
-                quantise((g + LEAD_QUANT) // 4)
-            banks = {}
-            if 0 <= g + LEAD_VALUE < rows_all:
-                banks[4] = value_pass(ps_s, g + LEAD_VALUE)
-                vp = vpool.tile([P, CV], F32)
-                nc.scalar.copy(out=vp[:], in_=banks[4][:])
-                vrow[g + LEAD_VALUE] = vp
-            if g < 0:
-                continue
+        produce(0)
+        produce(1)
+        for g in range(2 * H):
+            bp, r = g // H, g % H
             if g % 4 == 0:
+                if g // 4 + 2 < 32:
+                    produce(g // 4 + 2)
                 grp_c = cgrp.tile([P, 4, P, 4], BF16, align_bytes=64)
             if g % 32 == 8 and g < 96:
                 prep_attn((g // 32 + 1) // 2, (g // 32 + 1) % 2)
-            banks[0] = value_pass(ps_v, g)
-            if g % H > 0:
-                banks[-1] = value_pass(ps_v, g - 1)
-            if g % H < H - 1:
-                banks[1] = value_pass(ps_s, g + 1)
-            dest(g, banks, grp_c)
+            dest(bp, r, grp_c)
             if g % 4 == 3:
-                finish(g // H, g % H - 3, grp_c)
+                finish(bp, r - 3, grp_c)

@@ -41,14 +41,13 @@ def tile_selfattentionmodulev2_pb_t_kernel(tc, x, attn, v_w, v_b, w_w, w_b, out)
         xgrp = ctx.enter_context(tc.tile_pool(name="xgrp", bufs=2))
         xq = ctx.enter_context(tc.tile_pool(name="xq", bufs=2))
         vpool = ctx.enter_context(tc.tile_pool(name="vpool", bufs=20))
-        ppool = ctx.enter_context(tc.tile_pool(name="ppool", bufs=8))
+        ppool = ctx.enter_context(tc.tile_pool(name="ppool", bufs=14))
         cgrp = ctx.enter_context(tc.tile_pool(name="cgrp", bufs=2))
         cq = ctx.enter_context(tc.tile_pool(name="cq", bufs=2))
         opool = ctx.enter_context(tc.tile_pool(name="opool", bufs=2))
         ps_set = ctx.enter_context(tc.psum_pool(name="ps_set", bufs=2))
-        ps_v = ctx.enter_context(tc.psum_pool(name="ps_v", bufs=2))
+        ps_v = ctx.enter_context(tc.psum_pool(name="ps_v", bufs=4))
         ps_c = ctx.enter_context(tc.psum_pool(name="ps_c", bufs=2))
-        ps_o = ctx.enter_context(tc.psum_pool(name="ps_o", bufs=1))
 
         a_raw = const.tile([P, PADA + 4096 + PADA], BF16)
         nc.vector.memset(a_raw[:], 0.0)
@@ -205,7 +204,7 @@ def tile_selfattentionmodulev2_pb_t_kernel(tc, x, attn, v_w, v_b, w_w, w_b, out)
             cc = cq.tile([P, 512], U32, align_bytes=64)
             cs = cq.tile([P, 512], U8, align_bytes=64)
             nc.vector.quantize_mx(out=cc[:].bitcast(FP8X4), scales=cs[:], in_=grp_c[:].rearrange("p i u t -> p (i u t)"))
-            o_ps = ps_o.tile([P, 512], F32)
+            o_ps = ps_set.tile([P, 512], F32, tag="setup")
             nc.tensor.matmul_mx(
                 out=o_ps[:], lhsT=wc[:].bitcast(FP8X4), lhsT_scale=ws[:], rhs=cc[:].bitcast(FP8X4), rhs_scale=cs[:],
                 start=True, stop=True,

@@ -20,17 +20,13 @@ FLOPS = 2 * B * H * W * (CIN * CV + CV * COUT + 27 * CV)
 
 
 def chains_for(r):
-    def rows(l, j, picks):
-        d = DILS[l]
-        return [((i - 1) * d, 9 * l + 3 * i + j) for i in picks if 0 <= r + (i - 1) * d < H]
-
-    chains = []
+    groups = []
     for l, d in enumerate(DILS):
-        chains.append((0, ([(0, 4)] if l == 0 else []) + rows(l, 1, (0, 2)), True))
-        for j in (0, 2):
-            chains.append(((j - 1) * d, rows(l, j, (1, 0)), True))
-            chains.append(((j - 1) * d, rows(l, j, (2,)), False))
-    return [c for c in chains if c[1]]
+        rows = [i for i in (1, 0, 2) if 0 <= r + (i - 1) * d < H]
+        groups.append([((j - 1) * d, [((i - 1) * d, 9 * l + 3 * i + j) for i in rows], True) for j in (0, 2)])
+        lone = [(0, [((i - 1) * d, 9 * l + 3 * i + 1)], l < 2) for i in rows if i != 1 or l == 0]
+        groups.append(lone)
+    return groups
 
 
 def tile_selfattentionmodulev2_pb_t_kernel(tc, x, attn, v_w, v_b, w_w, w_b, out):
@@ -41,7 +37,7 @@ def tile_selfattentionmodulev2_pb_t_kernel(tc, x, attn, v_w, v_b, w_w, w_b, out)
         xgrp = ctx.enter_context(tc.tile_pool(name="xgrp", bufs=2))
         xq = ctx.enter_context(tc.tile_pool(name="xq", bufs=2))
         vpool = ctx.enter_context(tc.tile_pool(name="vpool", bufs=20))
-        ppool = ctx.enter_context(tc.tile_pool(name="ppool", bufs=14))
+        ppool = ctx.enter_context(tc.tile_pool(name="ppool", bufs=24))
         cgrp = ctx.enter_context(tc.tile_pool(name="cgrp", bufs=2))
         cq = ctx.enter_context(tc.tile_pool(name="cq", bufs=2))
         opool = ctx.enter_context(tc.tile_pool(name="opool", bufs=2))
@@ -179,25 +175,35 @@ def tile_selfattentionmodulev2_pb_t_kernel(tc, x, attn, v_w, v_b, w_w, w_b, out)
 
         def dest(bp, r, grp_c):
             ctx_ps = ps_c.tile([P, 4, P], F32)
-            chains = chains_for(r)
-            last = len(chains) - 1
-            for ci, (dc, leaves, on_scalar) in enumerate(chains):
-                pt = ppool.tile([P, CV], F32)
-                dr0, n0 = leaves[0]
-                if on_scalar:
-                    nc.scalar.activation(out=pt[:], in_=vrow[(bp, r + dr0)][:], func=ACT.Copy, scale=a_t[:, bp, r, n0:n0 + 1])
-                else:
-                    nc.vector.tensor_scalar_mul(out=pt[:], in0=vrow[(bp, r + dr0)][:], scalar1=a_t[:, bp, r, n0:n0 + 1])
-                for dr, n in leaves[1:]:
-                    nc.vector.scalar_tensor_tensor(
-                        out=pt[:], in0=vrow[(bp, r + dr)][:], scalar=a_t[:, bp, r, n:n + 1], in1=pt[:],
-                        op0=ALU.mult, op1=ALU.add,
-                    )
-                for t in range(4):
-                    nc.tensor.matmul(
-                        out=ctx_ps[:, t, :], lhsT=pt[:, t * P:(t + 1) * P], rhs=perm[dc],
-                        start=(ci == 0 and t == 0), stop=(ci == last and t == 3), is_transpose=True,
-                    )
+            groups = chains_for(r)
+            left = sum(len(grp) for grp in groups)
+            first = True
+            for grp in groups:
+                pts = []
+                for dc, terms, on_scalar in grp:
+                    pt = ppool.tile([P, CV], F32)
+                    pts.append(pt)
+                    dr0, n0 = terms[0]
+                    if on_scalar:
+                        nc.scalar.activation(out=pt[:], in_=vrow[(bp, r + dr0)][:], func=ACT.Copy, scale=a_t[:, bp, r, n0:n0 + 1])
+                    else:
+                        nc.vector.tensor_scalar_mul(out=pt[:], in0=vrow[(bp, r + dr0)][:], scalar1=a_t[:, bp, r, n0:n0 + 1])
+                for k in range(1, 3):
+                    for pt, (dc, terms, on_scalar) in zip(pts, grp):
+                        if k < len(terms):
+                            dr, n = terms[k]
+                            nc.vector.scalar_tensor_tensor(
+                                out=pt[:], in0=vrow[(bp, r + dr)][:], scalar=a_t[:, bp, r, n:n + 1], in1=pt[:],
+                                op0=ALU.mult, op1=ALU.add,
+                            )
+                for pt, (dc, terms, on_scalar) in zip(pts, grp):
+                    left -= 1
+                    for t in range(4):
+                        nc.tensor.matmul(
+                            out=ctx_ps[:, t, :], lhsT=pt[:, t * P:(t + 1) * P], rhs=perm[dc],
+                            start=(first and t == 0), stop=(left == 0 and t == 3), is_transpose=True,
+                        )
+                    first = False
             nc.scalar.copy(out=grp_c[:, r % 4], in_=ctx_ps[:].rearrange("p t u -> p u t"))
 
         def finish(bp, r0, grp_c):

@@ -19,14 +19,17 @@ PADA = 16
 FLOPS = 2 * B * H * W * (CIN * CV + CV * COUT + 27 * CV)
 
 
-def chains_for(r):
-    groups = []
+SCALAR_LONE = 5
+
+
+def terms_for(r):
+    chains, lone = [], []
     for l, d in enumerate(DILS):
         rows = [i for i in (1, 0, 2) if 0 <= r + (i - 1) * d < H]
-        groups.append([((j - 1) * d, [((i - 1) * d, 9 * l + 3 * i + j) for i in rows], True) for j in (0, 2)])
-        lone = [(0, [((i - 1) * d, 9 * l + 3 * i + 1)], l < 2) for i in rows if i != 1 or l == 0]
-        groups.append(lone)
-    return groups
+        for j in (0, 2):
+            chains.append(((j - 1) * d, [((i - 1) * d, 9 * l + 3 * i + j) for i in rows]))
+        lone.extend(((i - 1) * d, 9 * l + 3 * i + 1) for i in rows if i != 1 or l == 0)
+    return chains, lone
 
 
 def tile_selfattentionmodulev2_pb_t_kernel(tc, x, attn, v_w, v_b, w_w, w_b, out):
@@ -37,7 +40,8 @@ def tile_selfattentionmodulev2_pb_t_kernel(tc, x, attn, v_w, v_b, w_w, w_b, out)
         xgrp = ctx.enter_context(tc.tile_pool(name="xgrp", bufs=2))
         xq = ctx.enter_context(tc.tile_pool(name="xq", bufs=2))
         vpool = ctx.enter_context(tc.tile_pool(name="vpool", bufs=20))
-        ppool = ctx.enter_context(tc.tile_pool(name="ppool", bufs=24))
+        chpool = ctx.enter_context(tc.tile_pool(name="chpool", bufs=20))
+        lopool = ctx.enter_context(tc.tile_pool(name="lopool", bufs=16))
         cgrp = ctx.enter_context(tc.tile_pool(name="cgrp", bufs=2))
         cq = ctx.enter_context(tc.tile_pool(name="cq", bufs=2))
         opool = ctx.enter_context(tc.tile_pool(name="opool", bufs=2))
@@ -116,48 +120,61 @@ def tile_selfattentionmodulev2_pb_t_kernel(tc, x, attn, v_w, v_b, w_w, w_b, out)
             for j in (0, 2):
                 classes.append(((j - 1) * d, 9 * l + j, 3))
 
-        def prep_attn(bp, h):
-            for dc, n0, cnt in classes:
-                at_ps = ps_set.tile([P, 8, P], BF16, tag="setup")
-                for q in range(8):
-                    s0 = PADA + ((h * 8 + q) * 4 + 2 * bp) * W - dc
-                    nc.tensor.transpose(out=at_ps[:, q, :], in_=a_raw[:, s0:s0 + P], identity=ident_b[:])
-                src = at_ps[:].rearrange("p q (s n) -> p (q s) n", n=32)[:, :, n0:n0 + 3 * cnt - 2:3]
-                dst = a_t[:, bp, h * 32:(h + 1) * 32, n0:n0 + 3 * cnt - 2:3]
-                if dc == 0:
-                    nc.vector.tensor_copy(out=dst, in_=src)
-                else:
-                    nc.vector.tensor_scalar_mul(out=dst, in0=src, scalar1=msk[:, dc + 4:dc + 5])
+        def prep_class(bp, h, k):
             rows = slice(h * 32, (h + 1) * 32)
-            nc.vector.tensor_tensor(out=a_t[:, bp, rows, 4], in0=a_t[:, bp, rows, 4], in1=a_t[:, bp, rows, 13], op=ALU.add)
-            nc.vector.tensor_tensor(out=a_t[:, bp, rows, 4], in0=a_t[:, bp, rows, 4], in1=a_t[:, bp, rows, 22], op=ALU.add)
+            if k == len(classes):
+                nc.vector.tensor_tensor(out=a_t[:, bp, rows, 4], in0=a_t[:, bp, rows, 4], in1=a_t[:, bp, rows, 13], op=ALU.add)
+                nc.vector.tensor_tensor(out=a_t[:, bp, rows, 4], in0=a_t[:, bp, rows, 4], in1=a_t[:, bp, rows, 22], op=ALU.add)
+                return
+            dc, n0, cnt = classes[k]
+            at_ps = ps_set.tile([P, 8, P], BF16, tag="setup")
+            for q in range(8):
+                s0 = PADA + ((h * 8 + q) * 4 + 2 * bp) * W - dc
+                nc.tensor.transpose(out=at_ps[:, q, :], in_=a_raw[:, s0:s0 + P], identity=ident_b[:])
+            src = at_ps[:].rearrange("p q (s n) -> p (q s) n", n=32)[:, :, n0:n0 + 3 * cnt - 2:3]
+            dst = a_t[:, bp, rows, n0:n0 + 3 * cnt - 2:3]
+            if dc == 0:
+                nc.vector.tensor_copy(out=dst, in_=src)
+            else:
+                nc.vector.tensor_scalar_mul(out=dst, in0=src, scalar1=msk[:, dc + 4:dc + 5])
 
-        prep_attn(0, 0)
+        for k in range(len(classes) + 1):
+            prep_class(0, 0, k)
 
-        raws = {}
-        vrow = {}
+        NT = 2 * H
+        NG = NT // 4
+        raws, grps, xqs, vps, vrow = {}, {}, {}, {}, {}
+        cht, lot, ctxs, cgs, ops = {}, {}, {}, {}, {}
 
-        def produce(kk):
+        def load_x(kk):
             bp, k4 = kk // 16, kk % 16
-            if k4 % 2 == 0:
-                raw = xraw.tile([P, 4, 2, 512], BF16)
-                for be in range(2):
-                    nc.sync.dma_start(
-                        out=raw[:, :, be, :],
-                        in_=x[2 * bp + be].rearrange("(p j) r c -> p j (r c)", j=4)[:, :, k4 * 256:k4 * 256 + 512],
-                    )
-                raws[kk // 2] = raw
-            raw = raws[kk // 2]
-            grp = xgrp.tile([P, 4, P, 4], BF16, align_bytes=64)
-            for i in range(4):
-                rl = (k4 % 2) * 4 + i
-                nc.scalar.copy(
-                    out=grp[:, i].rearrange("p (b c) j -> p b c j", b=2),
-                    in_=raw[:, :, :, rl * W:(rl + 1) * W].rearrange("p j b c -> p b c j"),
+            raw = xraw.tile([P, 4, 2, 512], BF16)
+            for be in range(2):
+                nc.sync.dma_start(
+                    out=raw[:, :, be, :],
+                    in_=x[2 * bp + be].rearrange("(p j) r c -> p j (r c)", j=4)[:, :, k4 * 256:k4 * 256 + 512],
                 )
+            raws[kk] = raw
+            raws[kk + 1] = raw
+
+        def inter_x(kk, i):
+            if i == 0:
+                grp = xgrp.tile([P, 4, P, 4], BF16, align_bytes=64)
+                grps[kk] = grp
+            rl = (kk % 2) * 4 + i
+            nc.scalar.copy(
+                out=grps[kk][:, i].rearrange("p (b c) j -> p b c j", b=2),
+                in_=raws[kk][:, :, :, rl * W:(rl + 1) * W].rearrange("p j b c -> p b c j"),
+            )
+
+        def quant_x(kk):
             xc = xq.tile([P, 512], U32, align_bytes=64)
             xs = xq.tile([P, 512], U8, align_bytes=64)
-            nc.vector.quantize_mx(out=xc[:].bitcast(FP8X4), scales=xs[:], in_=grp[:].rearrange("p i u j -> p (i u j)"))
+            nc.vector.quantize_mx(out=xc[:].bitcast(FP8X4), scales=xs[:], in_=grps[kk][:].rearrange("p i u j -> p (i u j)"))
+            xqs[kk] = (xc, xs)
+
+        def value_mx(kk):
+            xc, xs = xqs[kk]
             for i in range(4):
                 v_ps = ps_v.tile([P, CV], F32)
                 nc.tensor.matmul_mx(
@@ -169,56 +186,82 @@ def tile_selfattentionmodulev2_pb_t_kernel(tc, x, attn, v_w, v_b, w_w, w_b, out)
                     start=True,
                     stop=True,
                 )
-                vp = vpool.tile([P, CV], F32)
-                nc.vector.tensor_tensor(out=vp[:], in0=v_ps[:], in1=vb_bc[:], op=ALU.add)
-                vrow[(bp, k4 * 4 + i)] = vp
+                vps[4 * kk + i] = v_ps
 
-        def dest(bp, r, grp_c):
+        def value_out(g):
+            vp = vpool.tile([P, CV], F32)
+            nc.vector.tensor_tensor(out=vp[:], in0=vps[g][:], in1=vb_bc[:], op=ALU.add)
+            vrow[g] = vp
+
+        def heads(g):
+            bp, r = g // H, g % H
+            cht[g] = []
+            for dc, terms in terms_for(r)[0]:
+                ch = chpool.tile([P, CV], F32)
+                dr0, n0 = terms[0]
+                nc.scalar.activation(out=ch[:], in_=vrow[g + dr0][:], func=ACT.Copy, scale=a_t[:, bp, r, n0:n0 + 1])
+                cht[g].append((ch, dc, terms))
+
+        def lones(g, on_scalar):
+            bp, r = g // H, g % H
+            lone = terms_for(r)[1]
+            part = lone[:SCALAR_LONE] if on_scalar else lone[SCALAR_LONE:]
+            for dr, n in part:
+                lo = lopool.tile([P, CV], F32)
+                if on_scalar:
+                    nc.scalar.activation(out=lo[:], in_=vrow[g + dr][:], func=ACT.Copy, scale=a_t[:, bp, r, n:n + 1])
+                else:
+                    nc.vector.tensor_scalar_mul(out=lo[:], in0=vrow[g + dr][:], scalar1=a_t[:, bp, r, n:n + 1])
+                lot.setdefault(g, []).append(lo)
+
+        def macs(g, k):
+            bp, r = g // H, g % H
+            for ch, dc, terms in cht[g]:
+                if k < len(terms):
+                    dr, n = terms[k]
+                    nc.vector.scalar_tensor_tensor(
+                        out=ch[:], in0=vrow[g + dr][:], scalar=a_t[:, bp, r, n:n + 1], in1=ch[:],
+                        op0=ALU.mult, op1=ALU.add,
+                    )
+
+        def flush(g):
             ctx_ps = ps_c.tile([P, 4, P], F32)
-            groups = chains_for(r)
-            left = sum(len(grp) for grp in groups)
-            first = True
-            for grp in groups:
-                pts = []
-                for dc, terms, on_scalar in grp:
-                    pt = ppool.tile([P, CV], F32)
-                    pts.append(pt)
-                    dr0, n0 = terms[0]
-                    if on_scalar:
-                        nc.scalar.activation(out=pt[:], in_=vrow[(bp, r + dr0)][:], func=ACT.Copy, scale=a_t[:, bp, r, n0:n0 + 1])
-                    else:
-                        nc.vector.tensor_scalar_mul(out=pt[:], in0=vrow[(bp, r + dr0)][:], scalar1=a_t[:, bp, r, n0:n0 + 1])
-                for k in range(1, 3):
-                    for pt, (dc, terms, on_scalar) in zip(pts, grp):
-                        if k < len(terms):
-                            dr, n = terms[k]
-                            nc.vector.scalar_tensor_tensor(
-                                out=pt[:], in0=vrow[(bp, r + dr)][:], scalar=a_t[:, bp, r, n:n + 1], in1=pt[:],
-                                op0=ALU.mult, op1=ALU.add,
-                            )
-                for pt, (dc, terms, on_scalar) in zip(pts, grp):
-                    left -= 1
-                    for t in range(4):
-                        nc.tensor.matmul(
-                            out=ctx_ps[:, t, :], lhsT=pt[:, t * P:(t + 1) * P], rhs=perm[dc],
-                            start=(first and t == 0), stop=(left == 0 and t == 3), is_transpose=True,
-                        )
-                    first = False
-            nc.scalar.copy(out=grp_c[:, r % 4], in_=ctx_ps[:].rearrange("p t u -> p u t"))
+            ctxs[g] = ctx_ps
+            prods = [(lo, 0) for lo in lot[g]] + [(ch, dc) for ch, dc, terms in cht[g]]
+            for k, (pt, dc) in enumerate(prods):
+                for t in range(4):
+                    nc.tensor.matmul(
+                        out=ctx_ps[:, t, :], lhsT=pt[:, t * P:(t + 1) * P], rhs=perm[dc],
+                        start=(k == 0 and t == 0), stop=(k == len(prods) - 1 and t == 3), is_transpose=True,
+                    )
 
-        def finish(bp, r0, grp_c):
+        def evac(g):
+            if g % 4 == 0:
+                grp_c = cgrp.tile([P, 4, P, 4], BF16, align_bytes=64)
+                cgs[g // 4] = grp_c
+            nc.scalar.copy(out=cgs[g // 4][:, g % 4], in_=ctxs[g][:].rearrange("p t u -> p u t"))
+
+        def quant_c(kk):
             cc = cq.tile([P, 512], U32, align_bytes=64)
             cs = cq.tile([P, 512], U8, align_bytes=64)
-            nc.vector.quantize_mx(out=cc[:].bitcast(FP8X4), scales=cs[:], in_=grp_c[:].rearrange("p i u t -> p (i u t)"))
+            nc.vector.quantize_mx(out=cc[:].bitcast(FP8X4), scales=cs[:], in_=cgs[kk][:].rearrange("p i u t -> p (i u t)"))
+            cgs[kk] = (cc, cs)
+
+        def out_mx(kk):
+            cc, cs = cgs[kk]
             o_ps = ps_set.tile([P, 512], F32, tag="setup")
             nc.tensor.matmul_mx(
                 out=o_ps[:], lhsT=wc[:].bitcast(FP8X4), lhsT_scale=ws[:], rhs=cc[:].bitcast(FP8X4), rhs_scale=cs[:],
                 start=True, stop=True,
             )
+            ops[kk] = o_ps
+
+        def out_store(kk):
+            bp, r0 = kk // 16, (kk % 16) * 4
             o_sb = opool.tile([P, 2, 4, W], F32)
             nc.scalar.activation(
                 out=o_sb[:].rearrange("p b r c -> p r b c"),
-                in_=o_ps[:].rearrange("p (r b c) -> p r b c", r=4, b=2),
+                in_=ops[kk][:].rearrange("p (r b c) -> p r b c", r=4, b=2),
                 func=ACT.Identity, bias=wb[:, 0:1],
             )
             nc.sync.dma_start(
@@ -226,16 +269,46 @@ def tile_selfattentionmodulev2_pb_t_kernel(tc, x, attn, v_w, v_b, w_w, w_b, out)
                 in_=o_sb[:].rearrange("p b r c -> p b (r c)"),
             )
 
-        produce(0)
-        produce(1)
-        for g in range(2 * H):
-            bp, r = g // H, g % H
-            if g % 4 == 0:
-                if g // 4 + 2 < 32:
-                    produce(g // 4 + 2)
-                grp_c = cgrp.tile([P, 4, P, 4], BF16, align_bytes=64)
-            if g % 32 == 8 and g < 96:
-                prep_attn((g // 32 + 1) // 2, (g // 32 + 1) % 2)
-            dest(bp, r, grp_c)
-            if g % 4 == 3:
-                finish(bp, r - 3, grp_c)
+        load_x(0)
+        load_x(2)
+        for kk in range(2):
+            for i in range(4):
+                inter_x(kk, i)
+            quant_x(kk)
+            value_mx(kk)
+            for i in range(4):
+                value_out(4 * kk + i)
+        for i in range(4):
+            inter_x(2, i)
+
+        for t in range(-2, NT + 2):
+            if 0 <= t - 1 < NT:
+                evac(t - 1)
+            if t >= 5 and t % 4 == 1:
+                out_store(t // 4 - 1)
+            if t >= 1 and t + 7 < NT:
+                value_out(t + 7)
+            if 0 <= t + 1 < NT:
+                lones(t + 1, True)
+                macs(t + 1, 1)
+            if t >= 4 and t % 4 == 0:
+                quant_c(t // 4 - 1)
+            if t >= 0 and t % 4 == 0 and t // 4 + 2 < NG:
+                quant_x(t // 4 + 2)
+            if 0 <= t + 1 < NT:
+                macs(t + 1, 2)
+                lones(t + 1, False)
+            if t + 2 < NT:
+                heads(t + 2)
+            if t >= 0 and t // 4 + 3 < NG:
+                inter_x(t // 4 + 3, t % 4)
+            if t >= 0 and t % 8 == 0 and t // 4 + 4 < NG:
+                load_x(t // 4 + 4)
+            if 0 <= t < NT:
+                flush(t)
+            if 8 <= t % 32 < 8 + len(classes) + 1 and t < 96:
+                prep_class((t // 32 + 1) // 2, (t // 32 + 1) % 2, t % 32 - 8)
+            if t >= 4 and t % 4 == 0:
+                out_mx(t // 4 - 1)
+            if t >= 0 and t % 4 == 0 and t // 4 + 2 < NG:
+                value_mx(t // 4 + 2)

@@ -19,13 +19,14 @@ PADA = 16
 FLOPS = 2 * B * H * W * (CIN * CV + CV * COUT + 27 * CV)
 
 
-SCALAR_LONE = 5
+SCALAR_LONE = 3
+GPSIMD_ADDS = 2
 
 
 def terms_for(r):
     chains, lone = [], []
     for l, d in enumerate(DILS):
-        rows = [i for i in (1, 0, 2) if 0 <= r + (i - 1) * d < H]
+        rows = [i for i in (0, 1, 2) if 0 <= r + (i - 1) * d < H]
         for j in (0, 2):
             chains.append(((j - 1) * d, [((i - 1) * d, 9 * l + 3 * i + j) for i in rows]))
         lone.extend(((i - 1) * d, 9 * l + 3 * i + 1) for i in rows if i != 1 or l == 0)
@@ -36,84 +37,90 @@ def tile_selfattentionmodulev2_pb_t_kernel(tc, x, attn, v_w, v_b, w_w, w_b, out)
     nc = tc.nc
     with ExitStack() as ctx:
         const = ctx.enter_context(tc.tile_pool(name="const", bufs=1))
-        xraw = ctx.enter_context(tc.tile_pool(name="xraw", bufs=2))
-        xgrp = ctx.enter_context(tc.tile_pool(name="xgrp", bufs=2))
-        xq = ctx.enter_context(tc.tile_pool(name="xq", bufs=2))
-        vpool = ctx.enter_context(tc.tile_pool(name="vpool", bufs=20))
-        chpool = ctx.enter_context(tc.tile_pool(name="chpool", bufs=20))
-        lopool = ctx.enter_context(tc.tile_pool(name="lopool", bufs=16))
-        cgrp = ctx.enter_context(tc.tile_pool(name="cgrp", bufs=2))
-        cq = ctx.enter_context(tc.tile_pool(name="cq", bufs=2))
-        opool = ctx.enter_context(tc.tile_pool(name="opool", bufs=2))
         ps_set = ctx.enter_context(tc.psum_pool(name="ps_set", bufs=2))
         ps_v = ctx.enter_context(tc.psum_pool(name="ps_v", bufs=4))
         ps_c = ctx.enter_context(tc.psum_pool(name="ps_c", bufs=2))
 
-        a_raw = const.tile([P, PADA + 4096 + PADA], BF16)
-        nc.vector.memset(a_raw[:], 0.0)
-        a_view = a_raw[:, PADA:PADA + 4096].rearrange("p (q b c) -> p q b c", q=16, b=4)
-        a_src = attn.rearrange("b n (q s) c -> b n q s c", s=4)
-        vw_sb = const.tile([P, 4, CIN], BF16)
-        nc.sync.dma_start(out=vw_sb[:], in_=v_w.rearrange("(p t) k -> p t k", t=4))
-        for b in range(B):
-            for s in range(4):
-                eng = nc.sync if (b * 4 + s) % 2 == 0 else nc.scalar
-                eng.dma_start(out=a_view[s * 32:s * 32 + 27, :, b, :], in_=a_src[b, :, :, s, :])
-        vb_raw = const.tile([P, CV], BF16)
-        nc.scalar.dma_start(out=vb_raw[:], in_=v_b.partition_broadcast(P))
-        w_sb = const.tile([P, CV], BF16)
-        nc.scalar.dma_start(out=w_sb[:], in_=w_w)
-        wb_raw = const.tile([P, 1], BF16)
-        with nc.allow_non_contiguous_dma(reason="one bias value to a partition"):
-            nc.scalar.dma_start(out=wb_raw[:], in_=w_b.rearrange("(p o) -> p o", o=1))
+        with tc.tile_pool(name="setup", bufs=1) as setup:
+            a_raw = const.tile([P, PADA + 4096 + PADA], BF16)
+            nc.vector.memset(a_raw[:], 0.0)
+            a_view = a_raw[:, PADA:PADA + 4096].rearrange("p (q b c) -> p q b c", q=16, b=4)
+            a_src = attn.rearrange("b n (q s) c -> b n q s c", s=4)
+            vw_sb = setup.tile([P, 4, CIN], BF16)
+            nc.sync.dma_start(out=vw_sb[:], in_=v_w.rearrange("(p t) k -> p t k", t=4))
+            for b in range(B):
+                for s in range(4):
+                    eng = nc.sync if (b * 4 + s) % 2 == 0 else nc.scalar
+                    eng.dma_start(out=a_view[s * 32:s * 32 + 27, :, b, :], in_=a_src[b, :, :, s, :])
+            vb_raw = setup.tile([P, CV], BF16)
+            nc.scalar.dma_start(out=vb_raw[:], in_=v_b.partition_broadcast(P))
+            w_sb = setup.tile([P, CV], BF16)
+            nc.scalar.dma_start(out=w_sb[:], in_=w_w)
+            wb_raw = const.tile([P, 1], BF16)
+            with nc.allow_non_contiguous_dma(reason="one bias value to a partition"):
+                nc.scalar.dma_start(out=wb_raw[:], in_=w_b.rearrange("(p o) -> p o", o=1))
 
-        ident_f = const.tile([P, P], F32)
-        make_identity(nc, ident_f[:])
-        ident_b = const.tile([P, P], BF16)
-        nc.vector.tensor_copy(out=ident_b[:], in_=ident_f[:])
-        i3 = ident_f[:].rearrange("p (b c) -> p b c", b=2)
-        msk = const.tile([P, 16], F32)
-        perm = {0: ident_f[:]}
-        for dc in (-4, -2, -1, 1, 2, 4):
-            pm = const.tile([P, 2, W], F32, name="perm%d" % (dc + 4))
-            e = abs(dc)
-            if dc > 0:
-                nc.vector.tensor_copy(out=pm[:, :, 0:W - e], in_=i3[:, :, e:W])
-                nc.vector.tensor_copy(out=pm[:, :, W - e:W], in_=i3[:, :, 0:e])
-                nc.vector.tensor_reduce(out=msk[:, dc + 4:dc + 5], in_=i3[:, :, e:W], axis=AX.XY, op=ALU.add)
-            else:
-                nc.vector.tensor_copy(out=pm[:, :, e:W], in_=i3[:, :, 0:W - e])
-                nc.vector.tensor_copy(out=pm[:, :, 0:e], in_=i3[:, :, W - e:W])
-                nc.vector.tensor_reduce(out=msk[:, dc + 4:dc + 5], in_=i3[:, :, 0:W - e], axis=AX.XY, op=ALU.add)
-            perm[dc] = pm[:].rearrange("p b c -> p (b c)")
+            ident_f = const.tile([P, P], F32)
+            make_identity(nc, ident_f[:])
+            ident_b = const.tile([P, P], BF16)
+            nc.vector.tensor_copy(out=ident_b[:], in_=ident_f[:])
+            i3 = ident_f[:].rearrange("p (b c) -> p b c", b=2)
+            msk = const.tile([P, 16], F32)
+            perm = {0: ident_f[:]}
+            for dc in (-4, -2, -1, 1, 2, 4):
+                pm = const.tile([P, 2, W], F32, name="perm%d" % (dc + 4))
+                e = abs(dc)
+                if dc > 0:
+                    nc.vector.tensor_copy(out=pm[:, :, 0:W - e], in_=i3[:, :, e:W])
+                    nc.vector.tensor_copy(out=pm[:, :, W - e:W], in_=i3[:, :, 0:e])
+                    nc.vector.tensor_reduce(out=msk[:, dc + 4:dc + 5], in_=i3[:, :, e:W], axis=AX.XY, op=ALU.add)
+                else:
+                    nc.vector.tensor_copy(out=pm[:, :, e:W], in_=i3[:, :, 0:W - e])
+                    nc.vector.tensor_copy(out=pm[:, :, 0:e], in_=i3[:, :, W - e:W])
+                    nc.vector.tensor_reduce(out=msk[:, dc + 4:dc + 5], in_=i3[:, :, 0:W - e], axis=AX.XY, op=ALU.add)
+                perm[dc] = pm[:].rearrange("p b c -> p (b c)")
 
-        vw_perm = const.tile([P, 4, 4, P], BF16)
-        nc.vector.tensor_copy(out=vw_perm[:], in_=vw_sb[:].rearrange("a t (p j) -> a t j p", j=4))
-        vw_grp = const.tile([P, 4, P, 4], BF16, align_bytes=64)
-        for t in range(4):
-            tp = ps_set.tile([P, 8, P], BF16, tag="setup")
+            vw_perm = setup.tile([P, 4, 4, P], BF16)
+            nc.vector.tensor_copy(out=vw_perm[:], in_=vw_sb[:].rearrange("a t (p j) -> a t j p", j=4))
+            vw_grp = setup.tile([P, 4, P, 4], BF16, align_bytes=64)
+            for t in range(4):
+                tp = ps_set.tile([P, 8, P], BF16, tag="setup")
+                for j in range(4):
+                    nc.tensor.transpose(out=tp[:, j, :], in_=vw_perm[:, t, j, :], identity=ident_b[:])
+                nc.vector.tensor_copy(out=vw_grp[:, t], in_=tp[:, 0:4, :].rearrange("p j a -> p a j"))
+            vwc = const.tile([P, CV], U32, align_bytes=64)
+            vws = const.tile([P, CV], U8, align_bytes=64)
+            nc.vector.quantize_mx(out=vwc[:].bitcast(FP8X4), scales=vws[:], in_=vw_grp[:].rearrange("p t a j -> p (t a j)"))
+            vb_bc = const.tile([P, CV], F32)
+            nc.vector.tensor_copy(out=vb_bc[:].rearrange("p (t a) -> p t a", t=4), in_=vb_raw[:].rearrange("p (a t) -> p t a", t=4))
+
+            w_perm = setup.tile([P, 4, P], BF16)
+            nc.vector.tensor_copy(out=w_perm[:], in_=w_sb[:].rearrange("a (p j) -> a j p", j=4))
+            w_grp = setup.tile([P, P, 4], BF16, align_bytes=64)
+            tpw = ps_set.tile([P, 8, P], BF16, tag="setup")
             for j in range(4):
-                nc.tensor.transpose(out=tp[:, j, :], in_=vw_perm[:, t, j, :], identity=ident_b[:])
-            nc.vector.tensor_copy(out=vw_grp[:, t], in_=tp[:, 0:4, :].rearrange("p j a -> p a j"))
-        vwc = const.tile([P, CV], U32, align_bytes=64)
-        vws = const.tile([P, CV], U8, align_bytes=64)
-        nc.vector.quantize_mx(out=vwc[:].bitcast(FP8X4), scales=vws[:], in_=vw_grp[:].rearrange("p t a j -> p (t a j)"))
-        vb_bc = const.tile([P, CV], F32)
-        nc.vector.tensor_copy(out=vb_bc[:].rearrange("p (t a) -> p t a", t=4), in_=vb_raw[:].rearrange("p (a t) -> p t a", t=4))
+                nc.tensor.transpose(out=tpw[:, j, :], in_=w_perm[:, j, :], identity=ident_b[:])
+            nc.vector.tensor_copy(out=w_grp[:], in_=tpw[:, 0:4, :].rearrange("p j a -> p a j"))
+            wc = const.tile([P, COUT], U32, align_bytes=64)
+            ws = const.tile([P, COUT], U8, align_bytes=64)
+            nc.vector.quantize_mx(out=wc[:].bitcast(FP8X4), scales=ws[:], in_=w_grp[:].rearrange("p a j -> p (a j)"))
+            wb = const.tile([P, 1], F32)
+            nc.vector.tensor_copy(out=wb[:], in_=wb_raw[:])
 
-        w_perm = const.tile([P, 4, P], BF16)
-        nc.vector.tensor_copy(out=w_perm[:], in_=w_sb[:].rearrange("a (p j) -> a j p", j=4))
-        w_grp = const.tile([P, P, 4], BF16, align_bytes=64)
-        tpw = ps_set.tile([P, 8, P], BF16, tag="setup")
-        for j in range(4):
-            nc.tensor.transpose(out=tpw[:, j, :], in_=w_perm[:, j, :], identity=ident_b[:])
-        nc.vector.tensor_copy(out=w_grp[:], in_=tpw[:, 0:4, :].rearrange("p j a -> p a j"))
-        wc = const.tile([P, COUT], U32, align_bytes=64)
-        ws = const.tile([P, COUT], U8, align_bytes=64)
-        nc.vector.quantize_mx(out=wc[:].bitcast(FP8X4), scales=ws[:], in_=w_grp[:].rearrange("p a j -> p (a j)"))
-        wb = const.tile([P, 1], F32)
-        nc.vector.tensor_copy(out=wb[:], in_=wb_raw[:])
+        xraw = ctx.enter_context(tc.tile_pool(name="xraw", bufs=2))
+        xgrp = ctx.enter_context(tc.tile_pool(name="xgrp", bufs=2))
+        xq = ctx.enter_context(tc.tile_pool(name="xq", bufs=2))
+        vpool = ctx.enter_context(tc.tile_pool(name="vpool", bufs=11))
+        chpool = ctx.enter_context(tc.tile_pool(name="chpool", bufs=44))
+        lopool = ctx.enter_context(tc.tile_pool(name="lopool", bufs=7))
+        gacc = ctx.enter_context(tc.tile_pool(name="gacc", bufs=7))
+        gtmp = ctx.enter_context(tc.tile_pool(name="gtmp", bufs=4))
+        cgrp = ctx.enter_context(tc.tile_pool(name="cgrp", bufs=2))
+        cq = ctx.enter_context(tc.tile_pool(name="cq", bufs=2))
+        opool = ctx.enter_context(tc.tile_pool(name="opool", bufs=2))
 
+        s_all = const.tile([P, 2, H], F32)
+        s_tmp = const.tile([P, 32, 27], F32)
         a_t = const.tile([P, 2, H, 32], F32)
         classes = [(0, 1, 9)]
         for l, d in enumerate(DILS):
@@ -131,12 +138,22 @@ def tile_selfattentionmodulev2_pb_t_kernel(tc, x, attn, v_w, v_b, w_w, w_b, out)
             for q in range(8):
                 s0 = PADA + ((h * 8 + q) * 4 + 2 * bp) * W - dc
                 nc.tensor.transpose(out=at_ps[:, q, :], in_=a_raw[:, s0:s0 + P], identity=ident_b[:])
-            src = at_ps[:].rearrange("p q (s n) -> p (q s) n", n=32)[:, :, n0:n0 + 3 * cnt - 2:3]
+            view = at_ps[:].rearrange("p q (s n) -> p (q s) n", n=32)
+            src = view[:, :, n0:n0 + 3 * cnt - 2:3]
             dst = a_t[:, bp, rows, n0:n0 + 3 * cnt - 2:3]
-            if dc == 0:
-                nc.vector.tensor_copy(out=dst, in_=src)
-            else:
+            if dc != 0:
                 nc.vector.tensor_scalar_mul(out=dst, in0=src, scalar1=msk[:, dc + 4:dc + 5])
+                return
+            nc.vector.tensor_copy(out=dst, in_=src)
+            nc.vector.tensor_copy(out=s_tmp[:, :, n0:n0 + 3 * cnt - 2:3], in_=src)
+            for odc, m0, ocnt in classes[1:]:
+                nc.vector.tensor_scalar_mul(out=s_tmp[:, :, m0:m0 + 7:3], in0=view[:, :, m0:m0 + 7:3], scalar1=msk[:, 4 - odc:5 - odc])
+            for l, d in enumerate(DILS):
+                if h == 0:
+                    nc.vector.memset(s_tmp[:, 0:d, 9 * l:9 * l + 3], 0.0)
+                else:
+                    nc.vector.memset(s_tmp[:, 32 - d:32, 9 * l + 6:9 * l + 9], 0.0)
+            nc.vector.tensor_reduce(out=s_all[:, bp, rows], in_=s_tmp[:], axis=AX.X, op=ALU.add)
 
         for k in range(len(classes) + 1):
             prep_class(0, 0, k)
@@ -144,27 +161,27 @@ def tile_selfattentionmodulev2_pb_t_kernel(tc, x, attn, v_w, v_b, w_w, w_b, out)
         NT = 2 * H
         NG = NT // 4
         raws, grps, xqs, vps, vrow = {}, {}, {}, {}, {}
-        cht, lot, ctxs, cgs, ops = {}, {}, {}, {}, {}
+        cht, lot, ctxs, cgs, cqs, ops = {}, {}, {}, {}, {}, {}
 
         def load_x(kk):
             bp, k4 = kk // 16, kk % 16
-            raw = xraw.tile([P, 4, 2, 512], BF16)
+            raw = xraw.tile([P, 4, 2, 256], BF16)
             for be in range(2):
                 nc.sync.dma_start(
                     out=raw[:, :, be, :],
-                    in_=x[2 * bp + be].rearrange("(p j) r c -> p j (r c)", j=4)[:, :, k4 * 256:k4 * 256 + 512],
+                    in_=x[2 * bp + be].rearrange("(p j) r c -> p j (r c)", j=4)[:, :, k4 * 256:(k4 + 1) * 256],
                 )
             raws[kk] = raw
-            raws[kk + 1] = raw
 
-        def inter_x(kk, i):
+        def inter_x(g):
+            kk, i = g // 4, g % 4
             if i == 0:
                 grp = xgrp.tile([P, 4, P, 4], BF16, align_bytes=64)
                 grps[kk] = grp
-            rl = (kk % 2) * 4 + i
-            nc.scalar.copy(
+            nc.gpsimd.tensor_scalar(
                 out=grps[kk][:, i].rearrange("p (b c) j -> p b c j", b=2),
-                in_=raws[kk][:, :, :, rl * W:(rl + 1) * W].rearrange("p j b c -> p b c j"),
+                in0=raws[kk][:, :, :, i * W:(i + 1) * W].rearrange("p j b c -> p b c j"),
+                scalar1=1.0, scalar2=0.0, op0=ALU.mult, op1=ALU.add,
             )
 
         def quant_x(kk):
@@ -173,61 +190,76 @@ def tile_selfattentionmodulev2_pb_t_kernel(tc, x, attn, v_w, v_b, w_w, w_b, out)
             nc.vector.quantize_mx(out=xc[:].bitcast(FP8X4), scales=xs[:], in_=grps[kk][:].rearrange("p i u j -> p (i u j)"))
             xqs[kk] = (xc, xs)
 
-        def value_mx(kk):
-            xc, xs = xqs[kk]
-            for i in range(4):
-                v_ps = ps_v.tile([P, CV], F32)
-                nc.tensor.matmul_mx(
-                    out=v_ps[:],
-                    lhsT=xc[:, i * P:(i + 1) * P].bitcast(FP8X4),
-                    lhsT_scale=xs[:, i * P:(i + 1) * P],
-                    rhs=vwc[:].bitcast(FP8X4),
-                    rhs_scale=vws[:],
-                    start=True,
-                    stop=True,
-                )
-                vps[4 * kk + i] = v_ps
+        def value_mx(g):
+            xc, xs = xqs[g // 4]
+            i = g % 4
+            v_ps = ps_v.tile([P, CV], F32)
+            nc.tensor.matmul_mx(
+                out=v_ps[:],
+                lhsT=xc[:, i * P:(i + 1) * P].bitcast(FP8X4),
+                lhsT_scale=xs[:, i * P:(i + 1) * P],
+                rhs=vwc[:].bitcast(FP8X4),
+                rhs_scale=vws[:],
+                start=True,
+                stop=True,
+            )
+            vps[g] = v_ps
 
         def value_out(g):
             vp = vpool.tile([P, CV], F32)
-            nc.vector.tensor_tensor(out=vp[:], in0=vps[g][:], in1=vb_bc[:], op=ALU.add)
+            nc.scalar.copy(out=vp[:], in_=vps[g][:])
             vrow[g] = vp
 
-        def heads(g):
+        def heads(g, own_row):
             bp, r = g // H, g % H
-            cht[g] = []
             for dc, terms in terms_for(r)[0]:
-                ch = chpool.tile([P, CV], F32)
                 dr0, n0 = terms[0]
-                nc.scalar.activation(out=ch[:], in_=vrow[g + dr0][:], func=ACT.Copy, scale=a_t[:, bp, r, n0:n0 + 1])
-                cht[g].append((ch, dc, terms))
+                if (dr0 == 0) == own_row:
+                    ch = chpool.tile([P, CV], F32)
+                    nc.scalar.activation(out=ch[:], in_=vrow[g + dr0][:], func=ACT.Copy, scale=a_t[:, bp, r, n0:n0 + 1])
+                    cht.setdefault(g, []).append((ch, dc, terms))
 
-        def lones(g, on_scalar):
+        def macs_of(t):
+            todo = []
+            for back in (0, 1, 2, 4):
+                g = t - back
+                if g in cht:
+                    for ch, dc, terms in cht[g]:
+                        todo.extend((ch, g, n) for dr, n in terms[1:] if dr == back)
+            return todo
+
+        def mac(t, ch, g, n):
+            nc.vector.scalar_tensor_tensor(
+                out=ch[:], in0=vps[t][:], scalar=a_t[:, g // H, g % H, n:n + 1], in1=ch[:],
+                op0=ALU.mult, op1=ALU.add,
+            )
+
+        def lones(g):
             bp, r = g // H, g % H
             lone = terms_for(r)[1]
-            part = lone[:SCALAR_LONE] if on_scalar else lone[SCALAR_LONE:]
-            for dr, n in part:
+            lot[g] = []
+            for dr, n in lone[:SCALAR_LONE]:
                 lo = lopool.tile([P, CV], F32)
-                if on_scalar:
-                    nc.scalar.activation(out=lo[:], in_=vrow[g + dr][:], func=ACT.Copy, scale=a_t[:, bp, r, n:n + 1])
+                nc.scalar.activation(out=lo[:], in_=vrow[g + dr][:], func=ACT.Copy, scale=a_t[:, bp, r, n:n + 1])
+                lot[g].append(lo)
+            mine = [(vb_bc, s_all[:, bp, r:r + 1])] + [(vrow[g + dr], a_t[:, bp, r, n:n + 1]) for dr, n in lone[SCALAR_LONE:]]
+            pairs = min(GPSIMD_ADDS, len(mine) // 2)
+            made = []
+            for k, (src_t, fac) in enumerate(mine):
+                if k < 2 * pairs and k % 2 == 1:
+                    gp = gtmp.tile([P, CV], F32)
                 else:
-                    nc.vector.tensor_scalar_mul(out=lo[:], in0=vrow[g + dr][:], scalar1=a_t[:, bp, r, n:n + 1])
-                lot.setdefault(g, []).append(lo)
-
-        def macs(g, k):
-            bp, r = g // H, g % H
-            for ch, dc, terms in cht[g]:
-                if k < len(terms):
-                    dr, n = terms[k]
-                    nc.vector.scalar_tensor_tensor(
-                        out=ch[:], in0=vrow[g + dr][:], scalar=a_t[:, bp, r, n:n + 1], in1=ch[:],
-                        op0=ALU.mult, op1=ALU.add,
-                    )
+                    gp = gacc.tile([P, CV], F32)
+                    lot[g].append(gp)
+                nc.gpsimd.tensor_scalar(out=gp[:], in0=src_t[:], scalar1=fac, scalar2=0.0, op0=ALU.mult, op1=ALU.add)
+                made.append(gp)
+            for k in range(pairs):
+                nc.gpsimd.tensor_tensor(out=made[2 * k][:], in0=made[2 * k][:], in1=made[2 * k + 1][:], op=ALU.add)
 
         def flush(g):
             ctx_ps = ps_c.tile([P, 4, P], F32)
             ctxs[g] = ctx_ps
-            prods = [(lo, 0) for lo in lot[g]] + [(ch, dc) for ch, dc, terms in cht[g]]
+            prods = [(ch, dc) for ch, dc, terms in cht[g]] + [(lo, 0) for lo in lot[g]]
             for k, (pt, dc) in enumerate(prods):
                 for t in range(4):
                     nc.tensor.matmul(
@@ -245,10 +277,10 @@ def tile_selfattentionmodulev2_pb_t_kernel(tc, x, attn, v_w, v_b, w_w, w_b, out)
             cc = cq.tile([P, 512], U32, align_bytes=64)
             cs = cq.tile([P, 512], U8, align_bytes=64)
             nc.vector.quantize_mx(out=cc[:].bitcast(FP8X4), scales=cs[:], in_=cgs[kk][:].rearrange("p i u t -> p (i u t)"))
-            cgs[kk] = (cc, cs)
+            cqs[kk] = (cc, cs)
 
         def out_mx(kk):
-            cc, cs = cgs[kk]
+            cc, cs = cqs[kk]
             o_ps = ps_set.tile([P, 512], F32, tag="setup")
             nc.tensor.matmul_mx(
                 out=o_ps[:], lhsT=wc[:].bitcast(FP8X4), lhsT_scale=ws[:], rhs=cc[:].bitcast(FP8X4), rhs_scale=cs[:],
@@ -269,46 +301,37 @@ def tile_selfattentionmodulev2_pb_t_kernel(tc, x, attn, v_w, v_b, w_w, w_b, out)
                 in_=o_sb[:].rearrange("p b r c -> p b (r c)"),
             )
 
-        load_x(0)
-        load_x(2)
-        for kk in range(2):
-            for i in range(4):
-                inter_x(kk, i)
-            quant_x(kk)
-            value_mx(kk)
-            for i in range(4):
-                value_out(4 * kk + i)
-        for i in range(4):
-            inter_x(2, i)
-
-        for t in range(-2, NT + 2):
-            if 0 <= t - 1 < NT:
-                evac(t - 1)
-            if t >= 5 and t % 4 == 1:
-                out_store(t // 4 - 1)
-            if t >= 1 and t + 7 < NT:
-                value_out(t + 7)
+        for t in range(-12, NT + 10):
+            if t % 4 == 0 and 0 <= t // 4 + 3 < NG:
+                load_x(t // 4 + 3)
+            if 0 <= t + 8 < NT:
+                inter_x(t + 8)
+            if 0 <= t - 6 < NT:
+                evac(t - 6)
             if 0 <= t + 1 < NT:
-                lones(t + 1, True)
-                macs(t + 1, 1)
-            if t >= 4 and t % 4 == 0:
-                quant_c(t // 4 - 1)
-            if t >= 0 and t % 4 == 0 and t // 4 + 2 < NG:
-                quant_x(t // 4 + 2)
+                heads(t + 1, False)
+            if 0 <= t - 4 < NT:
+                lones(t - 4)
             if 0 <= t + 1 < NT:
-                macs(t + 1, 2)
-                lones(t + 1, False)
-            if t + 2 < NT:
-                heads(t + 2)
-            if t >= 0 and t // 4 + 3 < NG:
-                inter_x(t // 4 + 3, t % 4)
-            if t >= 0 and t % 8 == 0 and t // 4 + 4 < NG:
-                load_x(t // 4 + 4)
-            if 0 <= t < NT:
-                flush(t)
-            if 8 <= t % 32 < 8 + len(classes) + 1 and t < 96:
+                value_out(t + 1)
+                heads(t + 1, True)
+            if t % 4 == 1 and 0 <= (t - 13) // 4 < NG:
+                out_store((t - 13) // 4)
+            todo = macs_of(t) if 0 <= t < NT else []
+            for ch, g, n in todo[:6]:
+                mac(t, ch, g, n)
+            if t % 4 == 0 and 0 <= t // 4 + 1 < NG:
+                quant_x(t // 4 + 1)
+            if t % 4 == 2 and 0 <= (t - 10) // 4 < NG:
+                quant_c((t - 10) // 4)
+            for ch, g, n in todo[6:]:
+                mac(t, ch, g, n)
+            if 0 <= t - 5 < NT:
+                flush(t - 5)
+            if t % 4 == 0 and 0 <= (t - 12) // 4 < NG:
+                out_mx((t - 12) // 4)
+            if t % 2 == 0 and 0 <= t + 2 < NT:
+                value_mx(t + 2)
+                value_mx(t + 3)
+            if 8 <= t % 32 < 8 + len(classes) + 1 and 0 <= t < 96:
                 prep_class((t // 32 + 1) // 2, (t // 32 + 1) % 2, t % 32 - 8)
-            if t >= 4 and t % 4 == 0:
-                out_mx(t // 4 - 1)
-            if t >= 0 and t % 4 == 0 and t // 4 + 2 < NG:
-                value_mx(t // 4 + 2)

@@ -21,6 +21,7 @@ FLOPS = 2 * B * H * W * (CIN * CV + CV * COUT + 27 * CV)
 
 SCALAR_LONE = 3
 GPSIMD_ADDS = 2
+LAST = 4
 
 
 def terms_for(r):
@@ -113,7 +114,7 @@ def tile_selfattentionmodulev2_pb_t_kernel(tc, x, attn, v_w, v_b, w_w, w_b, out)
         vpool = ctx.enter_context(tc.tile_pool(name="vpool", bufs=11))
         chpool = ctx.enter_context(tc.tile_pool(name="chpool", bufs=44))
         lopool = ctx.enter_context(tc.tile_pool(name="lopool", bufs=7))
-        gacc = ctx.enter_context(tc.tile_pool(name="gacc", bufs=7))
+        gacc = ctx.enter_context(tc.tile_pool(name="gacc", bufs=9))
         gtmp = ctx.enter_context(tc.tile_pool(name="gtmp", bufs=4))
         cgrp = ctx.enter_context(tc.tile_pool(name="cgrp", bufs=2))
         cq = ctx.enter_context(tc.tile_pool(name="cq", bufs=2))
@@ -127,7 +128,17 @@ def tile_selfattentionmodulev2_pb_t_kernel(tc, x, attn, v_w, v_b, w_w, w_b, out)
             for j in (0, 2):
                 classes.append(((j - 1) * d, 9 * l + j, 3))
 
-        def prep_class(bp, h, k):
+        def masked(on_scalar, dst, src, dc):
+            if on_scalar and dc == 0:
+                nc.scalar.copy(out=dst, in_=src)
+            elif on_scalar:
+                nc.scalar.activation(out=dst, in_=src, func=ACT.Copy, scale=msk[:, dc + 4:dc + 5])
+            elif dc == 0:
+                nc.vector.tensor_copy(out=dst, in_=src)
+            else:
+                nc.vector.tensor_scalar_mul(out=dst, in0=src, scalar1=msk[:, dc + 4:dc + 5])
+
+        def prep_class(bp, h, k, on_scalar):
             rows = slice(h * 32, (h + 1) * 32)
             if k == len(classes):
                 nc.vector.tensor_tensor(out=a_t[:, bp, rows, 4], in0=a_t[:, bp, rows, 4], in1=a_t[:, bp, rows, 13], op=ALU.add)
@@ -141,13 +152,12 @@ def tile_selfattentionmodulev2_pb_t_kernel(tc, x, attn, v_w, v_b, w_w, w_b, out)
             view = at_ps[:].rearrange("p q (s n) -> p (q s) n", n=32)
             src = view[:, :, n0:n0 + 3 * cnt - 2:3]
             dst = a_t[:, bp, rows, n0:n0 + 3 * cnt - 2:3]
+            masked(on_scalar, dst, src, dc)
             if dc != 0:
-                nc.vector.tensor_scalar_mul(out=dst, in0=src, scalar1=msk[:, dc + 4:dc + 5])
                 return
-            nc.vector.tensor_copy(out=dst, in_=src)
-            nc.vector.tensor_copy(out=s_tmp[:, :, n0:n0 + 3 * cnt - 2:3], in_=src)
+            masked(on_scalar, s_tmp[:, :, n0:n0 + 3 * cnt - 2:3], src, 0)
             for odc, m0, ocnt in classes[1:]:
-                nc.vector.tensor_scalar_mul(out=s_tmp[:, :, m0:m0 + 7:3], in0=view[:, :, m0:m0 + 7:3], scalar1=msk[:, 4 - odc:5 - odc])
+                masked(on_scalar, s_tmp[:, :, m0:m0 + 7:3], view[:, :, m0:m0 + 7:3], -odc)
             for l, d in enumerate(DILS):
                 if h == 0:
                     nc.vector.memset(s_tmp[:, 0:d, 9 * l:9 * l + 3], 0.0)
@@ -156,7 +166,7 @@ def tile_selfattentionmodulev2_pb_t_kernel(tc, x, attn, v_w, v_b, w_w, w_b, out)
             nc.vector.tensor_reduce(out=s_all[:, bp, rows], in_=s_tmp[:], axis=AX.X, op=ALU.add)
 
         for k in range(len(classes) + 1):
-            prep_class(0, 0, k)
+            prep_class(0, 0, k, k % 2 == 1)
 
         NT = 2 * H
         NG = NT // 4
@@ -238,18 +248,30 @@ def tile_selfattentionmodulev2_pb_t_kernel(tc, x, attn, v_w, v_b, w_w, w_b, out)
             bp, r = g // H, g % H
             lone = terms_for(r)[1]
             lot[g] = []
+            if g >= NT - LAST:
+                acc0 = gacc.tile([P, CV], F32, tag="gp")
+                nc.vector.tensor_scalar_mul(out=acc0[:], in0=vb_bc[:], scalar1=s_all[:, bp, r:r + 1])
+                acc1 = gacc.tile([P, CV], F32, tag="gp")
+                nc.vector.tensor_scalar_mul(out=acc1[:], in0=vrow[g + lone[0][0]][:], scalar1=a_t[:, bp, r, lone[0][1]:lone[0][1] + 1])
+                for k, (dr, n) in enumerate(lone[1:]):
+                    acc = acc0 if k % 2 == 0 else acc1
+                    nc.vector.scalar_tensor_tensor(
+                        out=acc[:], in0=vrow[g + dr][:], scalar=a_t[:, bp, r, n:n + 1], in1=acc[:], op0=ALU.mult, op1=ALU.add,
+                    )
+                lot[g].extend([acc0, acc1])
+                return
             for dr, n in lone[:SCALAR_LONE]:
                 lo = lopool.tile([P, CV], F32)
                 nc.scalar.activation(out=lo[:], in_=vrow[g + dr][:], func=ACT.Copy, scale=a_t[:, bp, r, n:n + 1])
                 lot[g].append(lo)
             mine = [(vb_bc, s_all[:, bp, r:r + 1])] + [(vrow[g + dr], a_t[:, bp, r, n:n + 1]) for dr, n in lone[SCALAR_LONE:]]
-            pairs = min(GPSIMD_ADDS, len(mine) // 2)
+            pairs = min(GPSIMD_ADDS - g % 2, len(mine) // 2)
             made = []
             for k, (src_t, fac) in enumerate(mine):
                 if k < 2 * pairs and k % 2 == 1:
                     gp = gtmp.tile([P, CV], F32)
                 else:
-                    gp = gacc.tile([P, CV], F32)
+                    gp = gacc.tile([P, CV], F32, tag="gp")
                     lot[g].append(gp)
                 nc.gpsimd.tensor_scalar(out=gp[:], in0=src_t[:], scalar1=fac, scalar2=0.0, op0=ALU.mult, op1=ALU.add)
                 made.append(gp)
@@ -333,5 +355,6 @@ def tile_selfattentionmodulev2_pb_t_kernel(tc, x, attn, v_w, v_b, w_w, w_b, out)
             if t % 2 == 0 and 0 <= t + 2 < NT:
                 value_mx(t + 2)
                 value_mx(t + 3)
-            if 8 <= t % 32 < 8 + len(classes) + 1 and 0 <= t < 96:
-                prep_class((t // 32 + 1) // 2, (t // 32 + 1) % 2, t % 32 - 8)
+            if -1 <= t < 5:
+                for i in range(4 * (t + 1), 4 * (t + 2)):
+                    prep_class((i // 8 + 1) // 2, (i // 8 + 1) % 2, i % 8, True)

@@ -109,15 +109,13 @@ def tile_selfattentionmodulev2_pb_t_kernel(tc, x, attn, v_w, v_b, w_w, w_b, out)
             nc.vector.tensor_copy(out=wb[:], in_=wb_raw[:])
 
         xraw = ctx.enter_context(tc.tile_pool(name="xraw", bufs=2))
-        xgrp = ctx.enter_context(tc.tile_pool(name="xgrp", bufs=2))
-        xq = ctx.enter_context(tc.tile_pool(name="xq", bufs=2))
+        qin = ctx.enter_context(tc.tile_pool(name="qin", bufs=2))
+        qout = ctx.enter_context(tc.tile_pool(name="qout", bufs=2))
         vpool = ctx.enter_context(tc.tile_pool(name="vpool", bufs=11))
         chpool = ctx.enter_context(tc.tile_pool(name="chpool", bufs=44))
         lopool = ctx.enter_context(tc.tile_pool(name="lopool", bufs=7))
         gacc = ctx.enter_context(tc.tile_pool(name="gacc", bufs=9))
         gtmp = ctx.enter_context(tc.tile_pool(name="gtmp", bufs=4))
-        cgrp = ctx.enter_context(tc.tile_pool(name="cgrp", bufs=2))
-        cq = ctx.enter_context(tc.tile_pool(name="cq", bufs=2))
         opool = ctx.enter_context(tc.tile_pool(name="opool", bufs=2))
 
         s_all = const.tile([P, 2, H], F32)
@@ -170,8 +168,8 @@ def tile_selfattentionmodulev2_pb_t_kernel(tc, x, attn, v_w, v_b, w_w, w_b, out)
 
         NT = 2 * H
         NG = NT // 4
-        raws, grps, xqs, vps, vrow = {}, {}, {}, {}, {}
-        cht, lot, ctxs, cgs, cqs, ops = {}, {}, {}, {}, {}, {}
+        raws, stages, codes, vps, vrow = {}, {}, {}, {}, {}
+        cht, lot, ctxs, ops = {}, {}, {}, {}
 
         def load_x(kk):
             bp, k4 = kk // 16, kk % 16
@@ -183,31 +181,39 @@ def tile_selfattentionmodulev2_pb_t_kernel(tc, x, attn, v_w, v_b, w_w, w_b, out)
                 )
             raws[kk] = raw
 
+        def stage(kq):
+            if kq not in stages:
+                st = qin.tile([P, 2, 4, P, 4], BF16, align_bytes=64)
+                stages[kq] = st
+            return stages[kq]
+
         def inter_x(g):
             kk, i = g // 4, g % 4
-            if i == 0:
-                grp = xgrp.tile([P, 4, P, 4], BF16, align_bytes=64)
-                grps[kk] = grp
             nc.gpsimd.tensor_scalar(
-                out=grps[kk][:, i].rearrange("p (b c) j -> p b c j", b=2),
+                out=stage(kk - 4)[:, 0, i].rearrange("p (b c) j -> p b c j", b=2),
                 in0=raws[kk][:, :, :, i * W:(i + 1) * W].rearrange("p j b c -> p b c j"),
                 scalar1=1.0, scalar2=0.0, op0=ALU.mult, op1=ALU.add,
             )
 
-        def quant_x(kk):
-            xc = xq.tile([P, 512], U32, align_bytes=64)
-            xs = xq.tile([P, 512], U8, align_bytes=64)
-            nc.vector.quantize_mx(out=xc[:].bitcast(FP8X4), scales=xs[:], in_=grps[kk][:].rearrange("p i u j -> p (i u j)"))
-            xqs[kk] = (xc, xs)
+        def quant(kq):
+            qc = qout.tile([P, 2, 512], U32, align_bytes=64)
+            qs = qout.tile([P, 2, 512], U8, align_bytes=64)
+            lo, hi = (0 if kq + 4 < NG else 1), (2 if kq >= 0 else 1)
+            nc.vector.quantize_mx(
+                out=qc[:, lo:hi, :].rearrange("p h w -> p (h w)").bitcast(FP8X4),
+                scales=qs[:, lo:hi, :].rearrange("p h w -> p (h w)"),
+                in_=stages[kq][:, lo:hi].rearrange("p h i u j -> p (h i u j)"),
+            )
+            codes[kq] = (qc, qs)
 
         def value_mx(g):
-            xc, xs = xqs[g // 4]
+            qc, qs = codes[g // 4 - 4]
             i = g % 4
             v_ps = ps_v.tile([P, CV], F32)
             nc.tensor.matmul_mx(
                 out=v_ps[:],
-                lhsT=xc[:, i * P:(i + 1) * P].bitcast(FP8X4),
-                lhsT_scale=xs[:, i * P:(i + 1) * P],
+                lhsT=qc[:, 0, i * P:(i + 1) * P].bitcast(FP8X4),
+                lhsT_scale=qs[:, 0, i * P:(i + 1) * P],
                 rhs=vwc[:].bitcast(FP8X4),
                 rhs_scale=vws[:],
                 start=True,
@@ -290,22 +296,13 @@ def tile_selfattentionmodulev2_pb_t_kernel(tc, x, attn, v_w, v_b, w_w, w_b, out)
                     )
 
         def evac(g):
-            if g % 4 == 0:
-                grp_c = cgrp.tile([P, 4, P, 4], BF16, align_bytes=64)
-                cgs[g // 4] = grp_c
-            nc.scalar.copy(out=cgs[g // 4][:, g % 4], in_=ctxs[g][:].rearrange("p t u -> p u t"))
-
-        def quant_c(kk):
-            cc = cq.tile([P, 512], U32, align_bytes=64)
-            cs = cq.tile([P, 512], U8, align_bytes=64)
-            nc.vector.quantize_mx(out=cc[:].bitcast(FP8X4), scales=cs[:], in_=cgs[kk][:].rearrange("p i u t -> p (i u t)"))
-            cqs[kk] = (cc, cs)
+            nc.scalar.copy(out=stage(g // 4)[:, 1, g % 4], in_=ctxs[g][:].rearrange("p t u -> p u t"))
 
         def out_mx(kk):
-            cc, cs = cqs[kk]
+            qc, qs = codes[kk]
             o_ps = ps_set.tile([P, 512], F32, tag="setup")
             nc.tensor.matmul_mx(
-                out=o_ps[:], lhsT=wc[:].bitcast(FP8X4), lhsT_scale=ws[:], rhs=cc[:].bitcast(FP8X4), rhs_scale=cs[:],
+                out=o_ps[:], lhsT=wc[:].bitcast(FP8X4), lhsT_scale=ws[:], rhs=qc[:, 1, :].bitcast(FP8X4), rhs_scale=qs[:, 1, :],
                 start=True, stop=True,
             )
             ops[kk] = o_ps
@@ -323,11 +320,11 @@ def tile_selfattentionmodulev2_pb_t_kernel(tc, x, attn, v_w, v_b, w_w, w_b, out)
                 in_=o_sb[:].rearrange("p b r c -> p b (r c)"),
             )
 
-        for t in range(-12, NT + 10):
-            if t % 4 == 0 and 0 <= t // 4 + 3 < NG:
-                load_x(t // 4 + 3)
-            if 0 <= t + 8 < NT:
-                inter_x(t + 8)
+        for t in range(-14, NT + 10):
+            if t % 4 == 2 and 0 <= (t + 14) // 4 < NG:
+                load_x((t + 14) // 4)
+            if 0 <= t + 10 < NT:
+                inter_x(t + 10)
             if 0 <= t - 6 < NT:
                 evac(t - 6)
             if 0 <= t + 1 < NT:
@@ -342,10 +339,8 @@ def tile_selfattentionmodulev2_pb_t_kernel(tc, x, attn, v_w, v_b, w_w, w_b, out)
             todo = macs_of(t) if 0 <= t < NT else []
             for ch, g, n in todo[:6]:
                 mac(t, ch, g, n)
-            if t % 4 == 0 and 0 <= t // 4 + 1 < NG:
-                quant_x(t // 4 + 1)
-            if t % 4 == 2 and 0 <= (t - 10) // 4 < NG:
-                quant_c((t - 10) // 4)
+            if t % 4 == 2 and -4 <= (t - 10) // 4 < NG:
+                quant((t - 10) // 4)
             for ch, g, n in todo[6:]:
                 mac(t, ch, g, n)
             if 0 <= t - 5 < NT:

@@ -173,11 +173,11 @@ def tile_selfattentionmodulev2_pb_t_kernel(tc, x, attn, v_w, v_b, w_w, w_b, out)
 
         def load_x(kk):
             bp, k4 = kk // 16, kk % 16
-            raw = xraw.tile([P, 4, 2, 256], BF16)
+            raw = xraw.tile([P, 4, 4, 2, W], BF16)
             for be in range(2):
                 nc.sync.dma_start(
-                    out=raw[:, :, be, :],
-                    in_=x[2 * bp + be].rearrange("(p j) r c -> p j (r c)", j=4)[:, :, k4 * 256:(k4 + 1) * 256],
+                    out=raw[:, :, :, be, :],
+                    in_=x[2 * bp + be].rearrange("(p j) r c -> p j r c", j=4)[:, :, 4 * k4:4 * k4 + 4, :],
                 )
             raws[kk] = raw
 
@@ -187,11 +187,10 @@ def tile_selfattentionmodulev2_pb_t_kernel(tc, x, attn, v_w, v_b, w_w, w_b, out)
                 stages[kq] = st
             return stages[kq]
 
-        def inter_x(g):
-            kk, i = g // 4, g % 4
+        def inter_x(kk):
             nc.gpsimd.tensor_scalar(
-                out=stage(kk - 4)[:, 0, i].rearrange("p (b c) j -> p b c j", b=2),
-                in0=raws[kk][:, :, :, i * W:(i + 1) * W].rearrange("p j b c -> p b c j"),
+                out=stage(kk - 4)[:, 0].rearrange("p i u j -> p (i u) j"),
+                in0=raws[kk][:].rearrange("p j i b c -> p (i b c) j"),
                 scalar1=1.0, scalar2=0.0, op0=ALU.mult, op1=ALU.add,
             )
 
@@ -323,8 +322,8 @@ def tile_selfattentionmodulev2_pb_t_kernel(tc, x, attn, v_w, v_b, w_w, w_b, out)
         for t in range(-14, NT + 10):
             if t % 4 == 2 and 0 <= (t + 14) // 4 < NG:
                 load_x((t + 14) // 4)
-            if 0 <= t + 10 < NT:
-                inter_x(t + 10)
+            if t % 4 == 0 and 0 <= (t + 8) // 4 < NG:
+                inter_x((t + 8) // 4)
             if 0 <= t - 6 < NT:
                 evac(t - 6)
             if 0 <= t + 1 < NT:

@@ -236,7 +236,7 @@ def tile_selfattentionmodulev2_pb_t_kernel(tc, x, attn, v_w, v_b, w_w, w_b, out)
 
         def macs_of(t):
             todo = []
-            for back in (0, 1, 2, 4):
+            for back in (4, 2, 1, 0):
                 g = t - back
                 if g in cht:
                     for ch, dc, terms in cht[g]:
@@ -322,8 +322,8 @@ def tile_selfattentionmodulev2_pb_t_kernel(tc, x, attn, v_w, v_b, w_w, w_b, out)
         for t in range(-14, NT + 10):
             if t % 4 == 2 and 0 <= (t + 14) // 4 < NG:
                 load_x((t + 14) // 4)
-            if t % 4 == 0 and 0 <= (t + 8) // 4 < NG:
-                inter_x((t + 8) // 4)
+            if t % 4 == 3 and 0 <= (t + 9) // 4 < NG:
+                inter_x((t + 9) // 4)
             if 0 <= t - 6 < NT:
                 evac(t - 6)
             if 0 <= t + 1 < NT:
@@ -351,4 +351,4 @@ def tile_selfattentionmodulev2_pb_t_kernel(tc, x, attn, v_w, v_b, w_w, w_b, out)
                 value_mx(t + 3)
             if -1 <= t < 5:
                 for i in range(4 * (t + 1), 4 * (t + 2)):
-                    prep_class((i // 8 + 1) // 2, (i // 8 + 1) % 2, i % 8, True)
+                    prep_class((i // 8 + 1) // 2, (i // 8 + 1) % 2, i % 8, t >= 2)

@@ -15,27 +15,42 @@ AX = mybir.AxisListType
 B, CIN, CV, COUT, H, W = 4, 512, 512, 128, 64, 64
 P = 128
 DILS = (1, 2, 4)
+BAND_DUE = {1: -1, 2: 1, 4: 3}
 PADA = 16
+IMG_ROW = H * W
+SLOT = 144
 FLOPS = 2 * B * H * W * (CIN * CV + CV * COUT + 27 * CV)
 
 
-SCALAR_LONE = 3
-GPSIMD_ADDS = 2
-LAST = 4
+def banded(r):
+    return r % 2 == 0 and r >= 4
 
 
 def terms_for(r):
-    chains, lone = [], []
+    band = banded(r)
+    cols = []
     for l, d in enumerate(DILS):
-        rows = [i for i in (0, 1, 2) if 0 <= r + (i - 1) * d < H]
+        rows = [i for i in (0, 1, 2) if 0 <= r + (i - 1) * d < H and not (band and i == 1)]
         for j in (0, 2):
-            chains.append(((j - 1) * d, [((i - 1) * d, 9 * l + 3 * i + j) for i in rows]))
-        lone.extend(((i - 1) * d, 9 * l + 3 * i + 1) for i in rows if i != 1 or l == 0)
-    return chains, lone
+            cols.append(((j - 1) * d, [((i - 1) * d, 9 * l + 3 * i + j) for i in rows], BAND_DUE[d] if band else -1))
+    up = {d: (-d, 9 * l + 1) for l, d in enumerate(DILS) if r - d >= 0}
+    down = {d: (d, 9 * l + 7) for l, d in enumerate(DILS) if r + d < H}
+    pick = lambda side, ds: [side[d] for d in ds if d in side]
+    gp = pick(up, (1, 2))
+    if band:
+        return cols, (gp, pick(up, (4,)), pick(down, (1, 2, 4)), [], [])
+    own = pick(up, (4,)) + pick(down, (4,))
+    return cols, (gp, [], pick(down, (1,)), own, [(0, 4)] + pick(down, (2,)))
 
 
 def tile_selfattentionmodulev2_pb_t_kernel(tc, x, attn, v_w, v_b, w_w, w_b, out):
     nc = tc.nc
+    out_flat = out.rearrange("b o r c -> (b o r c)")
+
+    def scratch(pitch, first, width):
+        base = 2 * P * IMG_ROW + 48 * W + first
+        return out_flat[base:base + P * pitch].rearrange("(q w) -> q w", w=pitch)[:, 0:width]
+
     with ExitStack() as ctx:
         const = ctx.enter_context(tc.tile_pool(name="const", bufs=1))
         ps_set = ctx.enter_context(tc.psum_pool(name="ps_set", bufs=2))
@@ -53,6 +68,9 @@ def tile_selfattentionmodulev2_pb_t_kernel(tc, x, attn, v_w, v_b, w_w, w_b, out)
                 for s in range(4):
                     eng = nc.sync if (b * 4 + s) % 2 == 0 else nc.scalar
                     eng.dma_start(out=a_view[s * 32:s * 32 + 27, :, b, :], in_=a_src[b, :, :, s, :])
+            zero = setup.tile([P, 1024], F32)
+            nc.gpsimd.memset(zero[:], 0.0)
+            nc.sync.dma_start(out=scratch(IMG_ROW, 0, 1024), in_=zero[:])
             vb_raw = setup.tile([P, CV], BF16)
             nc.scalar.dma_start(out=vb_raw[:], in_=v_b.partition_broadcast(P))
             w_sb = setup.tile([P, CV], BF16)
@@ -112,15 +130,18 @@ def tile_selfattentionmodulev2_pb_t_kernel(tc, x, attn, v_w, v_b, w_w, w_b, out)
         qin = ctx.enter_context(tc.tile_pool(name="qin", bufs=2))
         qout = ctx.enter_context(tc.tile_pool(name="qout", bufs=2))
         vpool = ctx.enter_context(tc.tile_pool(name="vpool", bufs=11))
-        chpool = ctx.enter_context(tc.tile_pool(name="chpool", bufs=44))
+        chpool = ctx.enter_context(tc.tile_pool(name="chpool", bufs=48))
         lopool = ctx.enter_context(tc.tile_pool(name="lopool", bufs=7))
         gacc = ctx.enter_context(tc.tile_pool(name="gacc", bufs=9))
         gtmp = ctx.enter_context(tc.tile_pool(name="gtmp", bufs=4))
+        bands = ctx.enter_context(tc.tile_pool(name="bands", bufs=3))
         opool = ctx.enter_context(tc.tile_pool(name="opool", bufs=2))
 
         s_all = const.tile([P, 2, H], F32)
         s_tmp = const.tile([P, 32, 27], F32)
-        a_t = const.tile([P, 2, H, 32], F32)
+        a_t = const.tile([P, 2, H, 27], F32)
+        strip = const.tile([P, 2, H // 2, 9], F32)
+        nc.vector.memset(strip[:], 0.0)
         classes = [(0, 1, 9)]
         for l, d in enumerate(DILS):
             for j in (0, 2):
@@ -141,6 +162,8 @@ def tile_selfattentionmodulev2_pb_t_kernel(tc, x, attn, v_w, v_b, w_w, w_b, out)
             if k == len(classes):
                 nc.vector.tensor_tensor(out=a_t[:, bp, rows, 4], in0=a_t[:, bp, rows, 4], in1=a_t[:, bp, rows, 13], op=ALU.add)
                 nc.vector.tensor_tensor(out=a_t[:, bp, rows, 4], in0=a_t[:, bp, rows, 4], in1=a_t[:, bp, rows, 22], op=ALU.add)
+                for j, n in ((0, 23), (2, 14), (3, 5), (4, 4), (5, 3), (6, 12), (8, 21)):
+                    nc.vector.tensor_copy(out=strip[:, bp, h * 16:(h + 1) * 16, j], in_=a_t[:, bp, h * 32:(h + 1) * 32:2, n])
                 return
             dc, n0, cnt = classes[k]
             at_ps = ps_set.tile([P, 8, P], BF16, tag="setup")
@@ -169,7 +192,18 @@ def tile_selfattentionmodulev2_pb_t_kernel(tc, x, attn, v_w, v_b, w_w, w_b, out)
         NT = 2 * H
         NG = NT // 4
         raws, stages, codes, vps, vrow = {}, {}, {}, {}, {}
-        cht, lot, ctxs, ops = {}, {}, {}, {}
+        cht, lot, ctxs, ops, bnd = {}, {}, {}, {}, {}
+
+        def band_write(kk):
+            bp, k4 = kk // 16, kk % 16
+            dst = scratch(IMG_ROW + 1, (kk % 3) * 2 * SLOT, 2 * SLOT).rearrange("q (s w) -> q s w", w=SLOT)
+            nc.sync.dma_start(out=dst[:, :, 0:9], in_=strip[:, bp, 2 * k4:2 * k4 + 2, :])
+
+        def band_read(kk):
+            src = scratch(IMG_ROW, (kk % 3) * 2 * SLOT, 2 * SLOT).rearrange("q (s w) -> q s w", w=SLOT)
+            bt = bands.tile([P, 2, P], F32)
+            nc.sync.dma_start(out=bt[:], in_=src[:, :, 4:4 + P])
+            bnd[kk] = bt
 
         def load_x(kk):
             bp, k4 = kk // 16, kk % 16
@@ -225,22 +259,28 @@ def tile_selfattentionmodulev2_pb_t_kernel(tc, x, attn, v_w, v_b, w_w, w_b, out)
             nc.scalar.copy(out=vp[:], in_=vps[g][:])
             vrow[g] = vp
 
-        def heads(g, own_row):
-            bp, r = g // H, g % H
-            for dc, terms in terms_for(r)[0]:
-                dr0, n0 = terms[0]
-                if (dr0 == 0) == own_row:
+        def product(pool_tile, g, term):
+            dr, n = term
+            nc.scalar.activation(out=pool_tile[:], in_=vrow[g + dr][:], func=ACT.Copy, scale=a_t[:, g // H, g % H, n:n + 1])
+
+        def heads(g, after, own_row):
+            if not 0 <= g < NT:
+                return
+            cols, plain = terms_for(g % H)
+            todo = [(dc, terms) for dc, terms, due in cols if due == after]
+            if after == 3 and plain[3]:
+                todo.append((0, plain[3]))
+            for dc, terms in todo:
+                if (terms[0][0] == 0) == own_row:
                     ch = chpool.tile([P, CV], F32)
-                    nc.scalar.activation(out=ch[:], in_=vrow[g + dr0][:], func=ACT.Copy, scale=a_t[:, bp, r, n0:n0 + 1])
-                    cht.setdefault(g, []).append((ch, dc, terms))
+                    product(ch, g, terms[0])
+                    cht.setdefault(g, []).append((ch, dc, terms[1:]))
 
         def macs_of(t):
             todo = []
             for back in (4, 2, 1, 0):
-                g = t - back
-                if g in cht:
-                    for ch, dc, terms in cht[g]:
-                        todo.extend((ch, g, n) for dr, n in terms[1:] if dr == back)
+                for ch, dc, terms in cht.get(t - back, []):
+                    todo.extend((ch, t - back, n) for dr, n in terms if dr == back)
             return todo
 
         def mac(t, ch, g, n):
@@ -249,49 +289,47 @@ def tile_selfattentionmodulev2_pb_t_kernel(tc, x, attn, v_w, v_b, w_w, w_b, out)
                 op0=ALU.mult, op1=ALU.add,
             )
 
-        def lones(g):
-            bp, r = g // H, g % H
-            lone = terms_for(r)[1]
-            lot[g] = []
-            if g >= NT - LAST:
-                acc0 = gacc.tile([P, CV], F32, tag="gp")
-                nc.vector.tensor_scalar_mul(out=acc0[:], in0=vb_bc[:], scalar1=s_all[:, bp, r:r + 1])
-                acc1 = gacc.tile([P, CV], F32, tag="gp")
-                nc.vector.tensor_scalar_mul(out=acc1[:], in0=vrow[g + lone[0][0]][:], scalar1=a_t[:, bp, r, lone[0][1]:lone[0][1] + 1])
-                for k, (dr, n) in enumerate(lone[1:]):
-                    acc = acc0 if k % 2 == 0 else acc1
-                    nc.vector.scalar_tensor_tensor(
-                        out=acc[:], in0=vrow[g + dr][:], scalar=a_t[:, bp, r, n:n + 1], in1=acc[:], op0=ALU.mult, op1=ALU.add,
-                    )
-                lot[g].extend([acc0, acc1])
+        def plain_sum(g):
+            if not 0 <= g < NT:
                 return
-            for dr, n in lone[:SCALAR_LONE]:
-                lo = lopool.tile([P, CV], F32)
-                nc.scalar.activation(out=lo[:], in_=vrow[g + dr][:], func=ACT.Copy, scale=a_t[:, bp, r, n:n + 1])
-                lot[g].append(lo)
-            mine = [(vb_bc, s_all[:, bp, r:r + 1])] + [(vrow[g + dr], a_t[:, bp, r, n:n + 1]) for dr, n in lone[SCALAR_LONE:]]
-            pairs = min(GPSIMD_ADDS - g % 2, len(mine) // 2)
-            made = []
-            for k, (src_t, fac) in enumerate(mine):
-                if k < 2 * pairs and k % 2 == 1:
-                    gp = gtmp.tile([P, CV], F32)
-                else:
-                    gp = gacc.tile([P, CV], F32, tag="gp")
-                    lot[g].append(gp)
-                nc.gpsimd.tensor_scalar(out=gp[:], in0=src_t[:], scalar1=fac, scalar2=0.0, op0=ALU.mult, op1=ALU.add)
-                made.append(gp)
-            for k in range(pairs):
-                nc.gpsimd.tensor_tensor(out=made[2 * k][:], in0=made[2 * k][:], in1=made[2 * k + 1][:], op=ALU.add)
+            bp, r = g // H, g % H
+            gp, made_by_scalar, later = terms_for(r)[1][:3]
+            acc = gacc.tile([P, CV], F32)
+            nc.gpsimd.tensor_scalar(out=acc[:], in0=vb_bc[:], scalar1=s_all[:, bp, r:r + 1], scalar2=0.0, op0=ALU.mult, op1=ALU.add)
+            more = []
+            for dr, n in gp:
+                tmp = gtmp.tile([P, CV], F32)
+                nc.gpsimd.tensor_scalar(out=tmp[:], in0=vrow[g + dr][:], scalar1=a_t[:, bp, r, n:n + 1], scalar2=0.0, op0=ALU.mult, op1=ALU.add)
+                more.append(tmp)
+            for term in made_by_scalar:
+                lo = lopool.tile([P, CV], F32, tag="lo")
+                product(lo, g, term)
+                more.append(lo)
+            for tmp in more:
+                nc.gpsimd.tensor_tensor(out=acc[:], in0=acc[:], in1=tmp[:], op=ALU.add)
+            cht.setdefault(g, []).append((acc, 0, later))
+
+        def lones(g):
+            for term in terms_for(g % H)[1][4]:
+                lo = lopool.tile([P, CV], F32, tag="lo")
+                product(lo, g, term)
+                lot.setdefault(g, []).append(lo)
 
         def flush(g):
             ctx_ps = ps_c.tile([P, 4, P], F32)
             ctxs[g] = ctx_ps
-            prods = [(ch, dc) for ch, dc, terms in cht[g]] + [(lo, 0) for lo in lot[g]]
+            prods = [(ch, dc) for ch, dc, terms in cht[g]] + [(lo, 0) for lo in lot.get(g, [])]
+            band = banded(g % H)
+            if band:
+                for t in range(4):
+                    nc.tensor.matmul(
+                        out=ctx_ps[:, t, :], lhsT=vrow[g][:, t * P:(t + 1) * P], rhs=bnd[g // 4][:, g % 4 // 2, :], start=(t == 0), stop=False,
+                    )
             for k, (pt, dc) in enumerate(prods):
                 for t in range(4):
                     nc.tensor.matmul(
                         out=ctx_ps[:, t, :], lhsT=pt[:, t * P:(t + 1) * P], rhs=perm[dc],
-                        start=(k == 0 and t == 0), stop=(k == len(prods) - 1 and t == 3), is_transpose=True,
+                        start=(k == 0 and t == 0 and not band), stop=(k == len(prods) - 1 and t == 3), is_transpose=True,
                     )
 
         def evac(g):
@@ -322,17 +360,23 @@ def tile_selfattentionmodulev2_pb_t_kernel(tc, x, attn, v_w, v_b, w_w, w_b, out)
         for t in range(-14, NT + 10):
             if t % 4 == 2 and 0 <= (t + 14) // 4 < NG:
                 load_x((t + 14) // 4)
-            if t % 4 == 3 and 0 <= (t + 9) // 4 < NG:
-                inter_x((t + 9) // 4)
+            if t % 4 == 0 and 0 <= (t + 8) // 4 < NG:
+                inter_x((t + 8) // 4)
+            if t % 4 == 3 and 0 <= (t + 5) // 4 < NG and (t + 5) // 4 % 16 != 0:
+                band_write((t + 5) // 4)
+            if t % 4 == 1 and 0 <= (t + 3) // 4 < NG and (t + 3) // 4 % 16 != 0:
+                band_read((t + 3) // 4)
             if 0 <= t - 6 < NT:
                 evac(t - 6)
-            if 0 <= t + 1 < NT:
-                heads(t + 1, False)
-            if 0 <= t - 4 < NT:
-                lones(t - 4)
+            heads(t + 1, -1, False)
+            plain_sum(t + 1)
+            heads(t - 1, 1, False)
             if 0 <= t + 1 < NT:
                 value_out(t + 1)
-                heads(t + 1, True)
+                heads(t + 1, -1, True)
+            heads(t - 3, 3, False)
+            if 0 <= t - 3 < NT:
+                lones(t - 3)
             if t % 4 == 1 and 0 <= (t - 13) // 4 < NG:
                 out_store((t - 13) // 4)
             todo = macs_of(t) if 0 <= t < NT else []

@@ -357,7 +357,7 @@ def tile_selfattentionmodulev2_pb_t_kernel(tc, x, attn, v_w, v_b, w_w, w_b, out)
                 in_=o_sb[:].rearrange("p b r c -> p b (r c)"),
             )
 
-        for t in range(-14, NT + 10):
+        def slot(t):
             if t % 4 == 2 and 0 <= (t + 14) // 4 < NG:
                 load_x((t + 14) // 4)
             if t % 4 == 0 and 0 <= (t + 8) // 4 < NG:
@@ -396,3 +396,9 @@ def tile_selfattentionmodulev2_pb_t_kernel(tc, x, attn, v_w, v_b, w_w, w_b, out)
             if -1 <= t < 5:
                 for i in range(4 * (t + 1), 4 * (t + 2)):
                     prep_class((i // 8 + 1) // 2, (i // 8 + 1) % 2, i % 8, t >= 2)
+
+        for t in range(-14, 6):
+            slot(t)
+        with tc.manual_schedule(engines={mybir.EngineType.PE, mybir.EngineType.DVE, mybir.EngineType.Activation, mybir.EngineType.Pool}):
+            for t in range(6, NT + 10):
+                slot(t)

@@ -15,6 +15,10 @@ AX = mybir.AxisListType
 B, CIN, CV, COUT, H, W = 4, 512, 512, 128, 64, 64
 P = 128
 DILS = (1, 2, 4)
+BLOCKS = [(0, 0, 4), (0, 4, 8), (0, 12, 4), (1, 0, 8), (1, 8, 8)]
+PREP = 6
+ON_S = lambda i, t: i % 2 == 1
+NN = 27
 BAND_DUE = {1: -1, 2: 1, 4: 3}
 PADA = 16
 IMG_ROW = H * W
@@ -23,7 +27,7 @@ FLOPS = 2 * B * H * W * (CIN * CV + CV * COUT + 27 * CV)
 
 
 def banded(r):
-    return r % 2 == 0 and r >= 4
+    return r % 2 == 0 and r >= 2
 
 
 def terms_for(r):
@@ -38,7 +42,7 @@ def terms_for(r):
     pick = lambda side, ds: [side[d] for d in ds if d in side]
     gp = pick(up, (1, 2))
     if band:
-        return cols, (gp, pick(up, (4,)), pick(down, (1, 2, 4)), [], [])
+        return cols, (gp, pick(up, (4,)), pick(down, (1, 2)), [], pick(down, (4,)))
     own = pick(up, (4,)) + pick(down, (4,))
     return cols, (gp, [], pick(down, (1,)), own, [(0, 4)] + pick(down, (2,)))
 
@@ -57,27 +61,51 @@ def tile_selfattentionmodulev2_pb_t_kernel(tc, x, attn, v_w, v_b, w_w, w_b, out)
         ps_v = ctx.enter_context(tc.psum_pool(name="ps_v", bufs=4))
         ps_c = ctx.enter_context(tc.psum_pool(name="ps_c", bufs=2))
 
+        xraw = ctx.enter_context(tc.tile_pool(name="xraw", bufs=2))
+        raws = {}
+
+        def load_x(kk):
+            bp, k4 = kk // 16, kk % 16
+            raw = xraw.tile([P, 4, 4, 2, W], BF16)
+            for be in range(2):
+                nc.sync.dma_start(
+                    out=raw[:, :, :, be, :],
+                    in_=x[2 * bp + be].rearrange("(p j) r c -> p j r c", j=4)[:, :, 4 * k4:4 * k4 + 4, :],
+                )
+            raws[kk] = raw
+
         with tc.tile_pool(name="setup", bufs=1) as setup:
-            a_raw = const.tile([P, PADA + 4096 + PADA], BF16)
-            nc.vector.memset(a_raw[:], 0.0)
-            a_view = a_raw[:, PADA:PADA + 4096].rearrange("p (q b c) -> p q b c", q=16, b=4)
-            a_src = attn.rearrange("b n (q s) c -> b n q s c", s=4)
             vw_sb = setup.tile([P, 4, CIN], BF16)
             nc.sync.dma_start(out=vw_sb[:], in_=v_w.rearrange("(p t) k -> p t k", t=4))
+            load_x(0)
+            a_ld = setup.tile([P, B, 16, W], BF16)
+            a_src = attn.rearrange("b n (s q) c -> (b n) s (q c)", s=4)
             for b in range(B):
+                eng = nc.scalar if b == 0 else nc.sync
                 for s in range(4):
-                    eng = nc.sync if (b * 4 + s) % 2 == 0 else nc.scalar
-                    eng.dma_start(out=a_view[s * 32:s * 32 + 27, :, b, :], in_=a_src[b, :, :, s, :])
+                    n = 32 if b < B - 1 else NN
+                    eng.dma_start(out=a_ld[s * 32:s * 32 + n, b].rearrange("p q c -> p (q c)"), in_=a_src[b * NN:b * NN + n, s, :])
+                    if n == NN:
+                        eng.dma_start(out=a_ld[s * 32 + NN:s * 32 + 32, b].rearrange("p q c -> p (q c)"), in_=a_src[0:32 - NN, s, :])
             zero = setup.tile([P, 1024], F32)
             nc.gpsimd.memset(zero[:], 0.0)
             nc.sync.dma_start(out=scratch(IMG_ROW, 0, 1024), in_=zero[:])
             vb_raw = setup.tile([P, CV], BF16)
-            nc.scalar.dma_start(out=vb_raw[:], in_=v_b.partition_broadcast(P))
+            nc.sync.dma_start(out=vb_raw[:], in_=v_b.partition_broadcast(P))
             w_sb = setup.tile([P, CV], BF16)
-            nc.scalar.dma_start(out=w_sb[:], in_=w_w)
+            nc.sync.dma_start(out=w_sb[:], in_=w_w)
             wb_raw = const.tile([P, 1], BF16)
             with nc.allow_non_contiguous_dma(reason="one bias value to a partition"):
-                nc.scalar.dma_start(out=wb_raw[:], in_=w_b.rearrange("(p o) -> p o", o=1))
+                nc.sync.dma_start(out=wb_raw[:], in_=w_b.rearrange("(p o) -> p o", o=1))
+
+            a_raw = const.tile([P, PADA + 4096 + PADA], BF16)
+            nc.vector.memset(a_raw[:, 0:PADA], 0.0)
+            nc.vector.memset(a_raw[:, PADA + 4096:], 0.0)
+            a_view = a_raw[:, PADA:PADA + 4096].rearrange("p (q b c) -> p q b c", q=16, b=4)
+            nc.vector.tensor_copy(out=a_view[:, :, 0:2, :], in_=a_ld[:, 0:2].rearrange("p b q c -> p q b c"))
+            nc.gpsimd.tensor_scalar(
+                out=a_view[:, :, 2:4, :], in0=a_ld[:, 2:4].rearrange("p b q c -> p q b c"), scalar1=1.0, scalar2=0.0, op0=ALU.mult, op1=ALU.add,
+            )
 
             ident_f = const.tile([P, P], F32)
             make_identity(nc, ident_f[:])
@@ -126,7 +154,6 @@ def tile_selfattentionmodulev2_pb_t_kernel(tc, x, attn, v_w, v_b, w_w, w_b, out)
             wb = const.tile([P, 1], F32)
             nc.vector.tensor_copy(out=wb[:], in_=wb_raw[:])
 
-        xraw = ctx.enter_context(tc.tile_pool(name="xraw", bufs=2))
         qin = ctx.enter_context(tc.tile_pool(name="qin", bufs=2))
         qout = ctx.enter_context(tc.tile_pool(name="qout", bufs=2))
         vpool = ctx.enter_context(tc.tile_pool(name="vpool", bufs=11))
@@ -138,7 +165,7 @@ def tile_selfattentionmodulev2_pb_t_kernel(tc, x, attn, v_w, v_b, w_w, w_b, out)
         opool = ctx.enter_context(tc.tile_pool(name="opool", bufs=2))
 
         s_all = const.tile([P, 2, H], F32)
-        s_tmp = const.tile([P, 32, 27], F32)
+        s_tmp = const.tile([P, 8, 4, NN], F32)
         a_t = const.tile([P, 2, H, 27], F32)
         strip = const.tile([P, 2, H // 2, 9], F32)
         nc.vector.memset(strip[:], 0.0)
@@ -157,41 +184,43 @@ def tile_selfattentionmodulev2_pb_t_kernel(tc, x, attn, v_w, v_b, w_w, w_b, out)
             else:
                 nc.vector.tensor_scalar_mul(out=dst, in0=src, scalar1=msk[:, dc + 4:dc + 5])
 
-        def prep_class(bp, h, k, on_scalar):
-            rows = slice(h * 32, (h + 1) * 32)
+        def prep_class(block, k, on_scalar):
+            bp, q0, nq = block
+            a_blk = a_t[:, bp].rearrange("p (s q) n -> p q s n", q=16)[:, q0:q0 + nq]
             if k == len(classes):
-                nc.vector.tensor_tensor(out=a_t[:, bp, rows, 4], in0=a_t[:, bp, rows, 4], in1=a_t[:, bp, rows, 13], op=ALU.add)
-                nc.vector.tensor_tensor(out=a_t[:, bp, rows, 4], in0=a_t[:, bp, rows, 4], in1=a_t[:, bp, rows, 22], op=ALU.add)
+                nc.vector.tensor_tensor(out=a_blk[:, :, :, 4], in0=a_blk[:, :, :, 4], in1=a_blk[:, :, :, 13], op=ALU.add)
+                nc.vector.tensor_tensor(out=a_blk[:, :, :, 4], in0=a_blk[:, :, :, 4], in1=a_blk[:, :, :, 22], op=ALU.add)
+                s_blk = strip[:, bp].rearrange("p (s q) j -> p q s j", q=8)[:, q0 // 2:(q0 + nq) // 2]
                 for j, n in ((0, 23), (2, 14), (3, 5), (4, 4), (5, 3), (6, 12), (8, 21)):
-                    nc.vector.tensor_copy(out=strip[:, bp, h * 16:(h + 1) * 16, j], in_=a_t[:, bp, h * 32:(h + 1) * 32:2, n])
+                    nc.vector.tensor_copy(out=s_blk[:, :, :, j], in_=a_blk[:, 0:nq:2, :, n])
                 return
             dc, n0, cnt = classes[k]
             at_ps = ps_set.tile([P, 8, P], BF16, tag="setup")
-            for q in range(8):
-                s0 = PADA + ((h * 8 + q) * 4 + 2 * bp) * W - dc
+            for q in range(nq):
+                s0 = PADA + ((q0 + q) * 4 + 2 * bp) * W - dc
                 nc.tensor.transpose(out=at_ps[:, q, :], in_=a_raw[:, s0:s0 + P], identity=ident_b[:])
-            view = at_ps[:].rearrange("p q (s n) -> p (q s) n", n=32)
-            src = view[:, :, n0:n0 + 3 * cnt - 2:3]
-            dst = a_t[:, bp, rows, n0:n0 + 3 * cnt - 2:3]
-            masked(on_scalar, dst, src, dc)
+            view = at_ps[:, 0:nq].rearrange("p q (s n) -> p q s n", n=32)
+            src = view[:, :, :, n0:n0 + 3 * cnt - 2:3]
+            masked(on_scalar, a_blk[:, :, :, n0:n0 + 3 * cnt - 2:3], src, dc)
             if dc != 0:
                 return
-            masked(on_scalar, s_tmp[:, :, n0:n0 + 3 * cnt - 2:3], src, 0)
+            masked(on_scalar, s_tmp[:, 0:nq, :, n0:n0 + 3 * cnt - 2:3], src, 0)
             for odc, m0, ocnt in classes[1:]:
-                masked(on_scalar, s_tmp[:, :, m0:m0 + 7:3], view[:, :, m0:m0 + 7:3], -odc)
+                masked(on_scalar, s_tmp[:, 0:nq, :, m0:m0 + 7:3], view[:, :, :, m0:m0 + 7:3], -odc)
             for l, d in enumerate(DILS):
-                if h == 0:
-                    nc.vector.memset(s_tmp[:, 0:d, 9 * l:9 * l + 3], 0.0)
-                else:
-                    nc.vector.memset(s_tmp[:, 32 - d:32, 9 * l + 6:9 * l + 9], 0.0)
-            nc.vector.tensor_reduce(out=s_all[:, bp, rows], in_=s_tmp[:], axis=AX.X, op=ALU.add)
+                top, end = min(d - q0, nq), min(q0 + nq - (16 - d), nq)
+                if top > 0:
+                    nc.vector.memset(s_tmp[:, 0:top, 0, 9 * l:9 * l + 3], 0.0)
+                if end > 0:
+                    nc.vector.memset(s_tmp[:, nq - end:nq, 3, 9 * l + 6:9 * l + 9], 0.0)
+            nc.vector.tensor_reduce(out=s_all[:, bp].rearrange("p (s q) -> p q s", q=16)[:, q0:q0 + nq], in_=s_tmp[:, 0:nq], axis=AX.X, op=ALU.add)
 
         for k in range(len(classes) + 1):
-            prep_class(0, 0, k, k % 2 == 1)
+            prep_class(BLOCKS[0], k, k % 2 == 1)
 
         NT = 2 * H
         NG = NT // 4
-        raws, stages, codes, vps, vrow = {}, {}, {}, {}, {}
+        stages, codes, vps, vrow = {}, {}, {}, {}
         cht, lot, ctxs, ops, bnd = {}, {}, {}, {}, {}
 
         def band_write(kk):
@@ -204,16 +233,6 @@ def tile_selfattentionmodulev2_pb_t_kernel(tc, x, attn, v_w, v_b, w_w, w_b, out)
             bt = bands.tile([P, 2, P], F32)
             nc.sync.dma_start(out=bt[:], in_=src[:, :, 4:4 + P])
             bnd[kk] = bt
-
-        def load_x(kk):
-            bp, k4 = kk // 16, kk % 16
-            raw = xraw.tile([P, 4, 4, 2, W], BF16)
-            for be in range(2):
-                nc.sync.dma_start(
-                    out=raw[:, :, :, be, :],
-                    in_=x[2 * bp + be].rearrange("(p j) r c -> p j r c", j=4)[:, :, 4 * k4:4 * k4 + 4, :],
-                )
-            raws[kk] = raw
 
         def stage(kq):
             if kq not in stages:
@@ -358,22 +377,22 @@ def tile_selfattentionmodulev2_pb_t_kernel(tc, x, attn, v_w, v_b, w_w, w_b, out)
             )
 
         def slot(t):
-            if t % 4 == 2 and 0 <= (t + 14) // 4 < NG:
+            if t % 4 == 2 and 1 <= (t + 14) // 4 < NG:
                 load_x((t + 14) // 4)
             if t % 4 == 0 and 0 <= (t + 8) // 4 < NG:
                 inter_x((t + 8) // 4)
-            if t % 4 == 3 and 0 <= (t + 5) // 4 < NG and (t + 5) // 4 % 16 != 0:
-                band_write((t + 5) // 4)
-            if t % 4 == 1 and 0 <= (t + 3) // 4 < NG and (t + 3) // 4 % 16 != 0:
-                band_read((t + 3) // 4)
-            if 0 <= t - 6 < NT:
-                evac(t - 6)
+            if t % 4 == 3 and 0 <= (t + 1) // 4 < NG:
+                band_write((t + 1) // 4)
+            if t % 4 == 1 and 0 <= (t - 1) // 4 < NG:
+                band_read((t - 1) // 4)
             heads(t + 1, -1, False)
             plain_sum(t + 1)
             heads(t - 1, 1, False)
             if 0 <= t + 1 < NT:
                 value_out(t + 1)
                 heads(t + 1, -1, True)
+            if 0 <= t - 6 < NT:
+                evac(t - 6)
             heads(t - 3, 3, False)
             if 0 <= t - 3 < NT:
                 lones(t - 3)
@@ -393,9 +412,9 @@ def tile_selfattentionmodulev2_pb_t_kernel(tc, x, attn, v_w, v_b, w_w, w_b, out)
             if t % 2 == 0 and 0 <= t + 2 < NT:
                 value_mx(t + 2)
                 value_mx(t + 3)
-            if -1 <= t < 5:
-                for i in range(4 * (t + 1), 4 * (t + 2)):
-                    prep_class((i // 8 + 1) // 2, (i // 8 + 1) % 2, i % 8, t >= 2)
+            if -1 <= t < 6:
+                for i in range(PREP * (t + 1), min(PREP * (t + 2), 8 * len(BLOCKS) - 8)):
+                    prep_class(BLOCKS[1 + i // 8], i % 8, ON_S(i, t))
 
         for t in range(-14, 6):
             slot(t)

@@ -19,6 +19,7 @@ BLOCKS = [(0, 0, 4), (0, 4, 8), (0, 12, 4), (1, 0, 8), (1, 8, 8)]
 PREP = 6
 ON_S = lambda i, t: i % 2 == 1
 NN = 27
+PLAIN = {True: ((-1,), (1,), (-2, -4), (2, 4)), False: ((-1, -2), (1,), (2,), (-4, 0, 4))}
 BAND_DUE = {1: -1, 2: 1, 4: 3}
 PADA = 16
 IMG_ROW = H * W
@@ -30,21 +31,22 @@ def banded(r):
     return r % 2 == 0 and r >= 2
 
 
-def terms_for(r):
+def columns_for(r):
     band = banded(r)
     cols = []
     for l, d in enumerate(DILS):
         rows = [i for i in (0, 1, 2) if 0 <= r + (i - 1) * d < H and not (band and i == 1)]
         for j in (0, 2):
             cols.append(((j - 1) * d, [((i - 1) * d, 9 * l + 3 * i + j) for i in rows], BAND_DUE[d] if band else -1))
-    up = {d: (-d, 9 * l + 1) for l, d in enumerate(DILS) if r - d >= 0}
-    down = {d: (d, 9 * l + 7) for l, d in enumerate(DILS) if r + d < H}
-    pick = lambda side, ds: [side[d] for d in ds if d in side]
-    gp = pick(up, (1, 2))
-    if band:
-        return cols, (gp, pick(up, (4,)), pick(down, (1, 2)), [], pick(down, (4,)))
-    own = pick(up, (4,)) + pick(down, (4,))
-    return cols, (gp, [], pick(down, (1,)), own, [(0, 4)] + pick(down, (2,)))
+    return cols
+
+
+def plain_for(r):
+    term = {0: (0, 4)}
+    for l, d in enumerate(DILS):
+        term[-d], term[d] = (-d, 9 * l + 1), (d, 9 * l + 7)
+    summed, added, by_gpsimd, by_scalar = PLAIN[banded(r)]
+    return [[term[s] for s in shifts if 0 <= r + s < H] for shifts in (summed, added, by_gpsimd, by_scalar)]
 
 
 def tile_selfattentionmodulev2_pb_t_kernel(tc, x, attn, v_w, v_b, w_w, w_b, out):
@@ -156,11 +158,12 @@ def tile_selfattentionmodulev2_pb_t_kernel(tc, x, attn, v_w, v_b, w_w, w_b, out)
 
         qin = ctx.enter_context(tc.tile_pool(name="qin", bufs=2))
         qout = ctx.enter_context(tc.tile_pool(name="qout", bufs=2))
-        vpool = ctx.enter_context(tc.tile_pool(name="vpool", bufs=11))
-        chpool = ctx.enter_context(tc.tile_pool(name="chpool", bufs=48))
-        lopool = ctx.enter_context(tc.tile_pool(name="lopool", bufs=7))
-        gacc = ctx.enter_context(tc.tile_pool(name="gacc", bufs=9))
-        gtmp = ctx.enter_context(tc.tile_pool(name="gtmp", bufs=4))
+        vpool = ctx.enter_context(tc.tile_pool(name="vpool", bufs=10))
+        chpool = ctx.enter_context(tc.tile_pool(name="chpool", bufs=44))
+        lopool = ctx.enter_context(tc.tile_pool(name="lopool", bufs=8))
+        gacc = ctx.enter_context(tc.tile_pool(name="gacc", bufs=8))
+        gtmp = ctx.enter_context(tc.tile_pool(name="gtmp", bufs=2))
+        glpool = ctx.enter_context(tc.tile_pool(name="glpool", bufs=6))
         bands = ctx.enter_context(tc.tile_pool(name="bands", bufs=3))
         opool = ctx.enter_context(tc.tile_pool(name="opool", bufs=2))
 
@@ -258,20 +261,24 @@ def tile_selfattentionmodulev2_pb_t_kernel(tc, x, attn, v_w, v_b, w_w, w_b, out)
             )
             codes[kq] = (qc, qs)
 
-        def value_mx(g):
+        def value_mx(g, times):
+            if not 0 <= g < NT:
+                return
             qc, qs = codes[g // 4 - 4]
             i = g % 4
-            v_ps = ps_v.tile([P, CV], F32)
-            nc.tensor.matmul_mx(
-                out=v_ps[:],
-                lhsT=qc[:, 0, i * P:(i + 1) * P].bitcast(FP8X4),
-                lhsT_scale=qs[:, 0, i * P:(i + 1) * P],
-                rhs=vwc[:].bitcast(FP8X4),
-                rhs_scale=vws[:],
-                start=True,
-                stop=True,
-            )
-            vps[g] = v_ps
+            if g not in vps:
+                v_ps = ps_v.tile([P, CV], F32)
+                vps[g] = v_ps
+            for k in range(times):
+                nc.tensor.matmul_mx(
+                    out=vps[g][:],
+                    lhsT=qc[:, 0, i * P:(i + 1) * P].bitcast(FP8X4),
+                    lhsT_scale=qs[:, 0, i * P:(i + 1) * P],
+                    rhs=vwc[:].bitcast(FP8X4),
+                    rhs_scale=vws[:],
+                    start=True,
+                    stop=True,
+                )
 
         def value_out(g):
             vp = vpool.tile([P, CV], F32)
@@ -285,10 +292,7 @@ def tile_selfattentionmodulev2_pb_t_kernel(tc, x, attn, v_w, v_b, w_w, w_b, out)
         def heads(g, after, own_row):
             if not 0 <= g < NT:
                 return
-            cols, plain = terms_for(g % H)
-            todo = [(dc, terms) for dc, terms, due in cols if due == after]
-            if after == 3 and plain[3]:
-                todo.append((0, plain[3]))
+            todo = [(dc, terms) for dc, terms, due in columns_for(g % H) if due == after]
             for dc, terms in todo:
                 if (terms[0][0] == 0) == own_row:
                     ch = chpool.tile([P, CV], F32)
@@ -308,48 +312,57 @@ def tile_selfattentionmodulev2_pb_t_kernel(tc, x, attn, v_w, v_b, w_w, w_b, out)
                 op0=ALU.mult, op1=ALU.add,
             )
 
+        def gp_product(gp, src, factor):
+            nc.gpsimd.tensor_scalar(out=gp[:], in0=src[:], scalar1=factor, scalar2=0.0, op0=ALU.mult, op1=ALU.add)
+
         def plain_sum(g):
             if not 0 <= g < NT:
                 return
             bp, r = g // H, g % H
-            gp, made_by_scalar, later = terms_for(r)[1][:3]
+            summed, added = plain_for(r)[:2]
             acc = gacc.tile([P, CV], F32)
-            nc.gpsimd.tensor_scalar(out=acc[:], in0=vb_bc[:], scalar1=s_all[:, bp, r:r + 1], scalar2=0.0, op0=ALU.mult, op1=ALU.add)
+            gp_product(acc, vb_bc, s_all[:, bp, r:r + 1])
             more = []
-            for dr, n in gp:
+            for dr, n in summed:
                 tmp = gtmp.tile([P, CV], F32)
-                nc.gpsimd.tensor_scalar(out=tmp[:], in0=vrow[g + dr][:], scalar1=a_t[:, bp, r, n:n + 1], scalar2=0.0, op0=ALU.mult, op1=ALU.add)
+                gp_product(tmp, vrow[g + dr], a_t[:, bp, r, n:n + 1])
                 more.append(tmp)
-            for term in made_by_scalar:
-                lo = lopool.tile([P, CV], F32, tag="lo")
-                product(lo, g, term)
-                more.append(lo)
             for tmp in more:
                 nc.gpsimd.tensor_tensor(out=acc[:], in0=acc[:], in1=tmp[:], op=ALU.add)
-            cht.setdefault(g, []).append((acc, 0, later))
+            cht.setdefault(g, []).append((acc, 0, added))
 
         def lones(g):
-            for term in terms_for(g % H)[1][4]:
-                lo = lopool.tile([P, CV], F32, tag="lo")
+            by_gpsimd, by_scalar = plain_for(g % H)[2:]
+            for dr, n in by_gpsimd:
+                gl = glpool.tile([P, CV], F32)
+                gp_product(gl, vrow[g + dr], a_t[:, g // H, g % H, n:n + 1])
+                lot.setdefault(g, []).append(gl)
+            for term in by_scalar:
+                lo = lopool.tile([P, CV], F32)
                 product(lo, g, term)
                 lot.setdefault(g, []).append(lo)
 
-        def flush(g):
+        def flush(g, row):
             ctx_ps = ps_c.tile([P, 4, P], F32)
             ctxs[g] = ctx_ps
             prods = [(ch, dc) for ch, dc, terms in cht[g]] + [(lo, 0) for lo in lot.get(g, [])]
             band = banded(g % H)
-            if band:
-                for t in range(4):
-                    nc.tensor.matmul(
-                        out=ctx_ps[:, t, :], lhsT=vrow[g][:, t * P:(t + 1) * P], rhs=bnd[g // 4][:, g % 4 // 2, :], start=(t == 0), stop=False,
-                    )
-            for k, (pt, dc) in enumerate(prods):
-                for t in range(4):
-                    nc.tensor.matmul(
-                        out=ctx_ps[:, t, :], lhsT=pt[:, t * P:(t + 1) * P], rhs=perm[dc],
-                        start=(k == 0 and t == 0 and not band), stop=(k == len(prods) - 1 and t == 3), is_transpose=True,
-                    )
+            n = len(prods)
+            for part in range(3):
+                if band and part < 2:
+                    for t in (2 * part, 2 * part + 1):
+                        nc.tensor.matmul(
+                            out=ctx_ps[:, t, :], lhsT=vrow[g][:, t * P:(t + 1) * P], rhs=bnd[g // 4][:, g % 4 // 2, :], start=(t == 0), stop=False,
+                        )
+                else:
+                    value_mx(row, 2)
+                for k in range(n * part // 3, n * (part + 1) // 3):
+                    pt, dc = prods[k]
+                    for t in range(4):
+                        nc.tensor.matmul(
+                            out=ctx_ps[:, t, :], lhsT=pt[:, t * P:(t + 1) * P], rhs=perm[dc],
+                            start=(k == 0 and t == 0 and not band), stop=(k == n - 1 and t == 3), is_transpose=True,
+                        )
 
         def evac(g):
             nc.scalar.copy(out=stage(g // 4)[:, 1, g % 4], in_=ctxs[g][:].rearrange("p t u -> p u t"))
@@ -406,12 +419,11 @@ def tile_selfattentionmodulev2_pb_t_kernel(tc, x, attn, v_w, v_b, w_w, w_b, out)
             for ch, g, n in todo[6:]:
                 mac(t, ch, g, n)
             if 0 <= t - 5 < NT:
-                flush(t - 5)
+                flush(t - 5, t + 2)
+            else:
+                value_mx(t + 2, 1)
             if t % 4 == 0 and 0 <= (t - 12) // 4 < NG:
                 out_mx((t - 12) // 4)
-            if t % 2 == 0 and 0 <= t + 2 < NT:
-                value_mx(t + 2)
-                value_mx(t + 3)
             if -1 <= t < 6:
                 for i in range(PREP * (t + 1), min(PREP * (t + 2), 8 * len(BLOCKS) - 8)):
                     prep_class(BLOCKS[1 + i // 8], i % 8, ON_S(i, t))

@@ -19,7 +19,7 @@ BLOCKS = [(0, 0, 4), (0, 4, 8), (0, 12, 4), (1, 0, 8), (1, 8, 8)]
 PREP = 6
 ON_S = lambda i, t: i % 2 == 1
 NN = 27
-PLAIN = {True: ((-1,), (1,), (-2, -4), (2, 4)), False: ((-1, -2), (1,), (2,), (-4, 0, 4))}
+PLAIN = {True: ((-1, -2), (1,), (-4,), (2, 4)), False: ((-1, -2), (1, 2), (), (-4, 0, 4))}
 BAND_DUE = {1: -1, 2: 1, 4: 3}
 PADA = 16
 IMG_ROW = H * W

@@ -19,7 +19,7 @@ BLOCKS = [(0, 0, 4), (0, 4, 8), (0, 12, 4), (1, 0, 8), (1, 8, 8)]
 PREP = 6
 ON_S = lambda i, t: i % 2 == 1
 NN = 27
-PLAIN = {True: ((-1, -2), (1,), (-4,), (2, 4)), False: ((-1, -2), (1, 2), (), (-4, 0, 4))}
+PLAIN = {True: ((-1, -2), (1,), (-4, 2, 4)), False: ((-1, -2), (1, 2), (-4, 0, 4))}
 BAND_DUE = {1: -1, 2: 1, 4: 3}
 PADA = 16
 IMG_ROW = H * W
@@ -45,8 +45,8 @@ def plain_for(r):
     term = {0: (0, 4)}
     for l, d in enumerate(DILS):
         term[-d], term[d] = (-d, 9 * l + 1), (d, 9 * l + 7)
-    summed, added, by_gpsimd, by_scalar = PLAIN[banded(r)]
-    return [[term[s] for s in shifts if 0 <= r + s < H] for shifts in (summed, added, by_gpsimd, by_scalar)]
+    summed, added, by_scalar = PLAIN[banded(r)]
+    return [[term[s] for s in shifts if 0 <= r + s < H] for shifts in (summed, added, by_scalar)]
 
 
 def tile_selfattentionmodulev2_pb_t_kernel(tc, x, attn, v_w, v_b, w_w, w_b, out):
@@ -159,11 +159,10 @@ def tile_selfattentionmodulev2_pb_t_kernel(tc, x, attn, v_w, v_b, w_w, w_b, out)
         qin = ctx.enter_context(tc.tile_pool(name="qin", bufs=2))
         qout = ctx.enter_context(tc.tile_pool(name="qout", bufs=2))
         vpool = ctx.enter_context(tc.tile_pool(name="vpool", bufs=10))
-        chpool = ctx.enter_context(tc.tile_pool(name="chpool", bufs=44))
-        lopool = ctx.enter_context(tc.tile_pool(name="lopool", bufs=8))
+        chpool = ctx.enter_context(tc.tile_pool(name="chpool", bufs=46))
+        lopool = ctx.enter_context(tc.tile_pool(name="lopool", bufs=10))
         gacc = ctx.enter_context(tc.tile_pool(name="gacc", bufs=8))
         gtmp = ctx.enter_context(tc.tile_pool(name="gtmp", bufs=2))
-        glpool = ctx.enter_context(tc.tile_pool(name="glpool", bufs=6))
         bands = ctx.enter_context(tc.tile_pool(name="bands", bufs=3))
         opool = ctx.enter_context(tc.tile_pool(name="opool", bufs=2))
 
@@ -332,12 +331,7 @@ def tile_selfattentionmodulev2_pb_t_kernel(tc, x, attn, v_w, v_b, w_w, w_b, out)
             cht.setdefault(g, []).append((acc, 0, added))
 
         def lones(g):
-            by_gpsimd, by_scalar = plain_for(g % H)[2:]
-            for dr, n in by_gpsimd:
-                gl = glpool.tile([P, CV], F32)
-                gp_product(gl, vrow[g + dr], a_t[:, g // H, g % H, n:n + 1])
-                lot.setdefault(g, []).append(gl)
-            for term in by_scalar:
+            for term in plain_for(g % H)[2]:
                 lo = lopool.tile([P, CV], F32)
                 product(lo, g, term)
                 lot.setdefault(g, []).append(lo)

@@ -8,6 +8,7 @@ BF16 = mybir.dt.bfloat16
 F32 = mybir.dt.float32
 U32 = mybir.dt.uint32
 U8 = mybir.dt.uint8
+I32 = mybir.dt.int32
 ALU = mybir.AluOpType
 ACT = mybir.ActivationFunctionType
 AX = mybir.AxisListType
@@ -19,23 +20,23 @@ BLOCKS = [(0, 0, 4), (0, 4, 8), (0, 12, 4), (1, 0, 8), (1, 8, 8)]
 PREP = 6
 ON_S = lambda i, t: i % 2 == 1
 NN = 27
-PLAIN = {True: ((-1, -2), (1,), (-4, 2, 4)), False: ((-1, -2), (1, 2), (-4, 0, 4))}
-BAND_DUE = {1: -1, 2: 1, 4: 3}
+PLAIN = {0: ((-1, -2), (2, 4), (-4,)), 1: ((-2, -4), (2, 4), (1,)), 2: ((-1, -2), (1, 2), (-4, 0, 4)), 3: ((-1, -2), (1, 2), (-4, 0, 4))}
+BAND_DUE = {1: 3, 2: 1, 4: 3}
 PADA = 16
 IMG_ROW = H * W
-SLOT = 144
+SLOT = 72
 FLOPS = 2 * B * H * W * (CIN * CV + CV * COUT + 27 * CV)
 
 
 def banded(r):
-    return r % 2 == 0 and r >= 2
+    return r % 4 < 2 and r >= 4
 
 
 def columns_for(r):
     band = banded(r)
     cols = []
     for l, d in enumerate(DILS):
-        rows = [i for i in (0, 1, 2) if 0 <= r + (i - 1) * d < H and not (band and i == 1)]
+        rows = [i for i in (0, 1, 2) if 0 <= r + (i - 1) * d < H and not (band and (i == 1 or d == 1 and i == (2, 0)[r % 4]))]
         for j in (0, 2):
             cols.append(((j - 1) * d, [((i - 1) * d, 9 * l + 3 * i + j) for i in rows], BAND_DUE[d] if band else -1))
     return cols
@@ -45,7 +46,7 @@ def plain_for(r):
     term = {0: (0, 4)}
     for l, d in enumerate(DILS):
         term[-d], term[d] = (-d, 9 * l + 1), (d, 9 * l + 7)
-    summed, added, by_scalar = PLAIN[banded(r)]
+    summed, added, by_scalar = PLAIN[r % 4 if banded(r) else 2 + r % 2]
     return [[term[s] for s in shifts if 0 <= r + s < H] for shifts in (summed, added, by_scalar)]
 
 
@@ -53,9 +54,9 @@ def tile_selfattentionmodulev2_pb_t_kernel(tc, x, attn, v_w, v_b, w_w, w_b, out)
     nc = tc.nc
     out_flat = out.rearrange("b o r c -> (b o r c)")
 
-    def scratch(pitch, first, width):
+    def scratch(pitch, first, width, rows):
         base = 2 * P * IMG_ROW + 48 * W + first
-        return out_flat[base:base + P * pitch].rearrange("(q w) -> q w", w=pitch)[:, 0:width]
+        return out_flat[base:base + rows * pitch].rearrange("(q w) -> q w", w=pitch)[:, 0:width]
 
     with ExitStack() as ctx:
         const = ctx.enter_context(tc.tile_pool(name="const", bufs=1))
@@ -64,6 +65,11 @@ def tile_selfattentionmodulev2_pb_t_kernel(tc, x, attn, v_w, v_b, w_w, w_b, out)
         ps_c = ctx.enter_context(tc.psum_pool(name="ps_c", bufs=2))
 
         xraw = ctx.enter_context(tc.tile_pool(name="xraw", bufs=2))
+        qin = ctx.enter_context(tc.tile_pool(name="qin", bufs=2))
+        qout = ctx.enter_context(tc.tile_pool(name="qout", bufs=2))
+        vpool = ctx.enter_context(tc.tile_pool(name="vpool", bufs=10))
+        gacc = ctx.enter_context(tc.tile_pool(name="gacc", bufs=8))
+        gtmp = ctx.enter_context(tc.tile_pool(name="gtmp", bufs=2))
         raws = {}
 
         def load_x(kk):
@@ -77,42 +83,48 @@ def tile_selfattentionmodulev2_pb_t_kernel(tc, x, attn, v_w, v_b, w_w, w_b, out)
             raws[kk] = raw
 
         with tc.tile_pool(name="setup", bufs=1) as setup:
+            a_src = attn.rearrange("b n (s q) c -> (b n s) (q c)", s=4)
+            a_ld = setup.tile([P, 2, 16, W], BF16)
+            a_raw = []
+            for bp in range(2):
+                raw = const.tile([P, PADA + 2048 + PADA], BF16, name="a_raw%d" % bp)
+                nc.vector.memset(raw[:, 0:PADA], 0.0)
+                nc.vector.memset(raw[:, PADA + 2048:], 0.0)
+                a_raw.append(raw)
+
+            def side_by_side(bp):
+                return a_raw[bp][:, PADA:PADA + 2048].rearrange("p (q b c) -> p b q c", q=16, b=2)
+
+            def load_weights(b, dst, eng):
+                first = b * 4 * NN
+                n = min(P, B * 4 * NN - first)
+                eng.dma_start(out=dst[0:n], in_=a_src[first:first + n, :].rearrange("p (q c) -> p q c", c=W))
+                if n < P:
+                    eng.dma_start(out=dst[n:P], in_=a_src[0:P - n, :].rearrange("p (q c) -> p q c", c=W))
+
+            load_weights(0, a_ld[:, 0], nc.scalar)
+            load_weights(1, a_ld[:, 1], nc.sync)
             vw_sb = setup.tile([P, 4, CIN], BF16)
-            nc.sync.dma_start(out=vw_sb[:], in_=v_w.rearrange("(p t) k -> p t k", t=4))
+            nc.scalar.dma_start(out=vw_sb[:], in_=v_w.rearrange("(p t) k -> p t k", t=4))
             load_x(0)
-            a_ld = setup.tile([P, B, 16, W], BF16)
-            a_src = attn.rearrange("b n (s q) c -> (b n) s (q c)", s=4)
-            for b in range(B):
-                eng = nc.scalar if b == 0 else nc.sync
-                for s in range(4):
-                    n = 32 if b < B - 1 else NN
-                    eng.dma_start(out=a_ld[s * 32:s * 32 + n, b].rearrange("p q c -> p (q c)"), in_=a_src[b * NN:b * NN + n, s, :])
-                    if n == NN:
-                        eng.dma_start(out=a_ld[s * 32 + NN:s * 32 + 32, b].rearrange("p q c -> p (q c)"), in_=a_src[0:32 - NN, s, :])
-            zero = setup.tile([P, 1024], F32)
-            nc.gpsimd.memset(zero[:], 0.0)
-            nc.sync.dma_start(out=scratch(IMG_ROW, 0, 1024), in_=zero[:])
             vb_raw = setup.tile([P, CV], BF16)
             nc.sync.dma_start(out=vb_raw[:], in_=v_b.partition_broadcast(P))
-            w_sb = setup.tile([P, CV], BF16)
+            w_sb = const.tile([P, CV], BF16)
             nc.sync.dma_start(out=w_sb[:], in_=w_w)
             wb_raw = const.tile([P, 1], BF16)
             with nc.allow_non_contiguous_dma(reason="one bias value to a partition"):
                 nc.sync.dma_start(out=wb_raw[:], in_=w_b.rearrange("(p o) -> p o", o=1))
-
-            a_raw = const.tile([P, PADA + 4096 + PADA], BF16)
-            nc.vector.memset(a_raw[:, 0:PADA], 0.0)
-            nc.vector.memset(a_raw[:, PADA + 4096:], 0.0)
-            a_view = a_raw[:, PADA:PADA + 4096].rearrange("p (q b c) -> p q b c", q=16, b=4)
-            nc.vector.tensor_copy(out=a_view[:, :, 0:2, :], in_=a_ld[:, 0:2].rearrange("p b q c -> p q b c"))
-            nc.gpsimd.tensor_scalar(
-                out=a_view[:, :, 2:4, :], in0=a_ld[:, 2:4].rearrange("p b q c -> p q b c"), scalar1=1.0, scalar2=0.0, op0=ALU.mult, op1=ALU.add,
-            )
+            zero = setup.tile([P, 1024], F32)
+            nc.gpsimd.memset(zero[:], 0.0)
+            nc.sync.dma_start(out=scratch(IMG_ROW, 0, 1024, P), in_=zero[:])
+            load_weights(2, side_by_side(1)[:, 0], nc.sync)
+            load_weights(3, side_by_side(1)[:, 1], nc.sync)
 
             ident_f = const.tile([P, P], F32)
             make_identity(nc, ident_f[:])
             ident_b = const.tile([P, P], BF16)
             nc.vector.tensor_copy(out=ident_b[:], in_=ident_f[:])
+            nc.vector.tensor_copy(out=side_by_side(0), in_=a_ld[:])
             i3 = ident_f[:].rearrange("p (b c) -> p b c", b=2)
             msk = const.tile([P, 16], F32)
             perm = {0: ident_f[:]}
@@ -129,6 +141,90 @@ def tile_selfattentionmodulev2_pb_t_kernel(tc, x, attn, v_w, v_b, w_w, w_b, out)
                     nc.vector.tensor_reduce(out=msk[:, dc + 4:dc + 5], in_=i3[:, :, 0:W - e], axis=AX.XY, op=ALU.add)
                 perm[dc] = pm[:].rearrange("p b c -> p (b c)")
 
+            scale_tiles = []
+            for k in range(2):
+                sc = const.tile([P, 2, 512], U8, align_bytes=64, name="scales%d" % k)
+                nc.gpsimd.memset(sc[:].rearrange("p h w -> p (h w)").bitcast(I32), 0)
+                scale_tiles.append(sc)
+
+            s_tmp = const.tile([P, 8, 4, NN], F32)
+            a_t, s_all, strip = [], [], []
+            for k, (bp, q0, nq) in enumerate(BLOCKS):
+                a_blk = const.tile([P, nq, 4, NN], F32, name="a_t%d" % k)
+                s_blk = const.tile([P, nq, 4], F32, name="s_all%d" % k)
+                p_blk = const.tile([P, nq // 4, 4, 2, 2, 9], F32, name="strip%d" % k)
+                nc.gpsimd.memset(p_blk[:], 0.0)
+                a_t.append(a_blk)
+                s_all.append(s_blk)
+                strip.append(p_blk)
+
+            def place(g):
+                bp, s, q = g // H, g % H // 16, g % 16
+                for k, (b, q0, nq) in enumerate(BLOCKS):
+                    if b == bp and q0 <= q < q0 + nq:
+                        return k, q - q0, s
+
+            def weight(g, n):
+                k, q, s = place(g)
+                return a_t[k][:, q, s, n:n + 1]
+
+            def bias_weight(g):
+                k, q, s = place(g)
+                return s_all[k][:, q, s:s + 1]
+
+            classes = [(0, 1, 9)]
+            for l, d in enumerate(DILS):
+                for j in (0, 2):
+                    classes.append(((j - 1) * d, 9 * l + j, 3))
+
+            def masked(on_scalar, dst, src, dc):
+                if on_scalar and dc == 0:
+                    nc.scalar.copy(out=dst, in_=src)
+                elif on_scalar:
+                    nc.scalar.activation(out=dst, in_=src, func=ACT.Copy, scale=msk[:, dc + 4:dc + 5])
+                elif dc == 0:
+                    nc.vector.tensor_copy(out=dst, in_=src)
+                else:
+                    nc.vector.tensor_scalar_mul(out=dst, in0=src, scalar1=msk[:, dc + 4:dc + 5])
+
+            def prep_class(block, k, on_scalar):
+                bp, q0, nq = BLOCKS[block]
+                a_blk = a_t[block]
+                if k == len(classes):
+                    nc.vector.tensor_tensor(out=a_blk[:, :, :, 4], in0=a_blk[:, :, :, 4], in1=a_blk[:, :, :, 13], op=ALU.add)
+                    nc.vector.tensor_tensor(out=a_blk[:, :, :, 4], in0=a_blk[:, :, :, 4], in1=a_blk[:, :, :, 22], op=ALU.add)
+                    s_blk = strip[block][:].rearrange("p k s i j e -> p k s (i j) e")
+                    p_blk = a_blk[:].rearrange("p (k i) s n -> p k s i n", i=4)
+                    for e, n in ((0, 23), (2, 14), (3, 5), (4, 4), (5, 3), (6, 12), (8, 21)):
+                        nc.vector.tensor_copy(out=s_blk[:, :, :, 0:4:3, e], in_=p_blk[:, :, :, 0:2, n])
+                    for e in (3, 4, 5):
+                        nc.vector.tensor_copy(out=s_blk[:, :, :, 2, e], in_=p_blk[:, :, :, 0, 11 - e])
+                        nc.vector.tensor_copy(out=s_blk[:, :, :, 1, e], in_=p_blk[:, :, :, 1, 5 - e])
+                    return
+                dc, n0, cnt = classes[k]
+                at_ps = ps_set.tile([P, 8, P], BF16, tag="setup")
+                for q in range(nq):
+                    s0 = PADA + (q0 + q) * P - dc
+                    nc.tensor.transpose(out=at_ps[:, q, :], in_=a_raw[bp][:, s0:s0 + P], identity=ident_b[:])
+                view = at_ps[:, 0:nq].rearrange("p q (n s) -> p q s n", s=4)
+                src = view[:, :, :, n0:n0 + 3 * cnt - 2:3]
+                masked(on_scalar, a_blk[:, :, :, n0:n0 + 3 * cnt - 2:3], src, dc)
+                if dc != 0:
+                    return
+                masked(on_scalar, s_tmp[:, 0:nq, :, n0:n0 + 3 * cnt - 2:3], src, 0)
+                for odc, m0, ocnt in classes[1:]:
+                    masked(on_scalar, s_tmp[:, 0:nq, :, m0:m0 + 7:3], view[:, :, :, m0:m0 + 7:3], -odc)
+                for l, d in enumerate(DILS):
+                    top, end = min(d - q0, nq), min(q0 + nq - (16 - d), nq)
+                    if top > 0:
+                        nc.vector.memset(s_tmp[:, 0:top, 0, 9 * l:9 * l + 3], 0.0)
+                    if end > 0:
+                        nc.vector.memset(s_tmp[:, nq - end:nq, 3, 9 * l + 6:9 * l + 9], 0.0)
+                nc.vector.tensor_reduce(out=s_all[block][:], in_=s_tmp[:, 0:nq], axis=AX.X, op=ALU.add)
+
+            for k in range(len(classes) + 1):
+                prep_class(0, k, k % 2 == 1)
+
             vw_perm = setup.tile([P, 4, 4, P], BF16)
             nc.vector.tensor_copy(out=vw_perm[:], in_=vw_sb[:].rearrange("a t (p j) -> a t j p", j=4))
             vw_grp = setup.tile([P, 4, P, 4], BF16, align_bytes=64)
@@ -143,9 +239,17 @@ def tile_selfattentionmodulev2_pb_t_kernel(tc, x, attn, v_w, v_b, w_w, w_b, out)
             vb_bc = const.tile([P, CV], F32)
             nc.vector.tensor_copy(out=vb_bc[:].rearrange("p (t a) -> p t a", t=4), in_=vb_raw[:].rearrange("p (a t) -> p t a", t=4))
 
-            w_perm = setup.tile([P, 4, P], BF16)
+        chpool = ctx.enter_context(tc.tile_pool(name="chpool", bufs=40))
+        lopool = ctx.enter_context(tc.tile_pool(name="lopool", bufs=10))
+        pair = ctx.enter_context(tc.tile_pool(name="pair", bufs=2))
+        pvals = ctx.enter_context(tc.tile_pool(name="pvals", bufs=5))
+        bands = ctx.enter_context(tc.tile_pool(name="bands", bufs=3))
+        opool = ctx.enter_context(tc.tile_pool(name="opool", bufs=2))
+
+        def prep_w():
+            w_perm = const.tile([P, 4, P], BF16)
             nc.vector.tensor_copy(out=w_perm[:], in_=w_sb[:].rearrange("a (p j) -> a j p", j=4))
-            w_grp = setup.tile([P, P, 4], BF16, align_bytes=64)
+            w_grp = const.tile([P, P, 4], BF16, align_bytes=64)
             tpw = ps_set.tile([P, 8, P], BF16, tag="setup")
             for j in range(4):
                 nc.tensor.transpose(out=tpw[:, j, :], in_=w_perm[:, j, :], identity=ident_b[:])
@@ -155,86 +259,63 @@ def tile_selfattentionmodulev2_pb_t_kernel(tc, x, attn, v_w, v_b, w_w, w_b, out)
             nc.vector.quantize_mx(out=wc[:].bitcast(FP8X4), scales=ws[:], in_=w_grp[:].rearrange("p a j -> p (a j)"))
             wb = const.tile([P, 1], F32)
             nc.vector.tensor_copy(out=wb[:], in_=wb_raw[:])
-
-        qin = ctx.enter_context(tc.tile_pool(name="qin", bufs=2))
-        qout = ctx.enter_context(tc.tile_pool(name="qout", bufs=2))
-        vpool = ctx.enter_context(tc.tile_pool(name="vpool", bufs=10))
-        chpool = ctx.enter_context(tc.tile_pool(name="chpool", bufs=46))
-        lopool = ctx.enter_context(tc.tile_pool(name="lopool", bufs=10))
-        gacc = ctx.enter_context(tc.tile_pool(name="gacc", bufs=8))
-        gtmp = ctx.enter_context(tc.tile_pool(name="gtmp", bufs=2))
-        bands = ctx.enter_context(tc.tile_pool(name="bands", bufs=3))
-        opool = ctx.enter_context(tc.tile_pool(name="opool", bufs=2))
-
-        s_all = const.tile([P, 2, H], F32)
-        s_tmp = const.tile([P, 8, 4, NN], F32)
-        a_t = const.tile([P, 2, H, 27], F32)
-        strip = const.tile([P, 2, H // 2, 9], F32)
-        nc.vector.memset(strip[:], 0.0)
-        classes = [(0, 1, 9)]
-        for l, d in enumerate(DILS):
-            for j in (0, 2):
-                classes.append(((j - 1) * d, 9 * l + j, 3))
-
-        def masked(on_scalar, dst, src, dc):
-            if on_scalar and dc == 0:
-                nc.scalar.copy(out=dst, in_=src)
-            elif on_scalar:
-                nc.scalar.activation(out=dst, in_=src, func=ACT.Copy, scale=msk[:, dc + 4:dc + 5])
-            elif dc == 0:
-                nc.vector.tensor_copy(out=dst, in_=src)
-            else:
-                nc.vector.tensor_scalar_mul(out=dst, in0=src, scalar1=msk[:, dc + 4:dc + 5])
-
-        def prep_class(block, k, on_scalar):
-            bp, q0, nq = block
-            a_blk = a_t[:, bp].rearrange("p (s q) n -> p q s n", q=16)[:, q0:q0 + nq]
-            if k == len(classes):
-                nc.vector.tensor_tensor(out=a_blk[:, :, :, 4], in0=a_blk[:, :, :, 4], in1=a_blk[:, :, :, 13], op=ALU.add)
-                nc.vector.tensor_tensor(out=a_blk[:, :, :, 4], in0=a_blk[:, :, :, 4], in1=a_blk[:, :, :, 22], op=ALU.add)
-                s_blk = strip[:, bp].rearrange("p (s q) j -> p q s j", q=8)[:, q0 // 2:(q0 + nq) // 2]
-                for j, n in ((0, 23), (2, 14), (3, 5), (4, 4), (5, 3), (6, 12), (8, 21)):
-                    nc.vector.tensor_copy(out=s_blk[:, :, :, j], in_=a_blk[:, 0:nq:2, :, n])
-                return
-            dc, n0, cnt = classes[k]
-            at_ps = ps_set.tile([P, 8, P], BF16, tag="setup")
-            for q in range(nq):
-                s0 = PADA + ((q0 + q) * 4 + 2 * bp) * W - dc
-                nc.tensor.transpose(out=at_ps[:, q, :], in_=a_raw[:, s0:s0 + P], identity=ident_b[:])
-            view = at_ps[:, 0:nq].rearrange("p q (s n) -> p q s n", n=32)
-            src = view[:, :, :, n0:n0 + 3 * cnt - 2:3]
-            masked(on_scalar, a_blk[:, :, :, n0:n0 + 3 * cnt - 2:3], src, dc)
-            if dc != 0:
-                return
-            masked(on_scalar, s_tmp[:, 0:nq, :, n0:n0 + 3 * cnt - 2:3], src, 0)
-            for odc, m0, ocnt in classes[1:]:
-                masked(on_scalar, s_tmp[:, 0:nq, :, m0:m0 + 7:3], view[:, :, :, m0:m0 + 7:3], -odc)
-            for l, d in enumerate(DILS):
-                top, end = min(d - q0, nq), min(q0 + nq - (16 - d), nq)
-                if top > 0:
-                    nc.vector.memset(s_tmp[:, 0:top, 0, 9 * l:9 * l + 3], 0.0)
-                if end > 0:
-                    nc.vector.memset(s_tmp[:, nq - end:nq, 3, 9 * l + 6:9 * l + 9], 0.0)
-            nc.vector.tensor_reduce(out=s_all[:, bp].rearrange("p (s q) -> p q s", q=16)[:, q0:q0 + nq], in_=s_tmp[:, 0:nq], axis=AX.X, op=ALU.add)
-
-        for k in range(len(classes) + 1):
-            prep_class(BLOCKS[0], k, k % 2 == 1)
+            return wc, ws, wb
 
         NT = 2 * H
         NG = NT // 4
         stages, codes, vps, vrow = {}, {}, {}, {}
-        cht, lot, ctxs, ops, bnd = {}, {}, {}, {}, {}
+        cht, lot, ctxs, ops = {}, {}, {}, {}
+        bnd, pairs, pps, prow = {}, {}, {}, {}
+        w_op = []
 
         def band_write(kk):
-            bp, k4 = kk // 16, kk % 16
-            dst = scratch(IMG_ROW + 1, (kk % 3) * 2 * SLOT, 2 * SLOT).rearrange("q (s w) -> q s w", w=SLOT)
-            nc.sync.dma_start(out=dst[:, :, 0:9], in_=strip[:, bp, 2 * k4:2 * k4 + 2, :])
+            k, q, s = place(4 * kk)
+            for be in range(2):
+                for i in range(2):
+                    dst = scratch(IMG_ROW + 1, i * W * IMG_ROW + ((kk % 3) * 4 + be * 2) * SLOT, 2 * SLOT, W).rearrange("q (s w) -> q s w", w=SLOT)
+                    nc.sync.dma_start(out=dst[:, :, 0:9], in_=strip[k][be * W:(be + 1) * W, q // 4, s, i])
 
         def band_read(kk):
-            src = scratch(IMG_ROW, (kk % 3) * 2 * SLOT, 2 * SLOT).rearrange("q (s w) -> q s w", w=SLOT)
-            bt = bands.tile([P, 2, P], F32)
-            nc.sync.dma_start(out=bt[:], in_=src[:, :, 4:4 + P])
+            src = scratch(IMG_ROW, (kk % 3) * 4 * SLOT, 4 * SLOT, P).rearrange("q (s w) -> q s w", w=SLOT)
+            bt = bands.tile([P, 4, W], F32)
+            nc.sync.dma_start(out=bt[:], in_=src[:, :, 4:4 + W])
             bnd[kk] = bt
+
+        def pair_codes(kk):
+            qc, qs = codes[kk - 4]
+            pc = pair.tile([P, 256], I32, align_bytes=64)
+            nc.vector.tensor_copy(
+                out=pc[:].rearrange("p (b i c) -> p i b c", b=2, i=2), in_=qc[:, 0, 0:256].rearrange("p (i b c) -> p i b c", i=2, b=2).bitcast(I32),
+            )
+            ps = pair.tile([P, 256], U8, align_bytes=64)
+            nc.vector.tensor_copy(
+                out=ps[:].rearrange("p (b i c) -> p i b c", b=2, i=2), in_=qs[:, 0, 0:256].rearrange("p (i b c) -> p i b c", i=2, b=2),
+            )
+            pairs[kk] = (pc, ps)
+
+        def pair_mx(kk, be, times):
+            pc, ps = pairs[kk]
+            if (kk, be) not in pps:
+                p_ps = ps_set.tile([P, CV], F32, tag="setup")
+                pps[(kk, be)] = p_ps
+            for k in range(times):
+                nc.tensor.matmul_mx(
+                    out=pps[(kk, be)][:],
+                    lhsT=pc[:, be * P:(be + 1) * P].bitcast(FP8X4),
+                    lhsT_scale=ps[:, be * P:(be + 1) * P],
+                    rhs=vwc[:].bitcast(FP8X4),
+                    rhs_scale=vws[:],
+                    start=True,
+                    stop=True,
+                )
+
+        def pair_out(kk, be):
+            pv = pvals.tile([P, CV], F32)
+            nc.scalar.copy(out=pv[:], in_=pps[(kk, be)][:])
+            prow[(kk, be)] = pv
+
+        def has_pair(kk):
+            return 0 <= kk < NG and banded(4 * kk % H)
 
         def stage(kq):
             if kq not in stages:
@@ -251,7 +332,7 @@ def tile_selfattentionmodulev2_pb_t_kernel(tc, x, attn, v_w, v_b, w_w, w_b, out)
 
         def quant(kq):
             qc = qout.tile([P, 2, 512], U32, align_bytes=64)
-            qs = qout.tile([P, 2, 512], U8, align_bytes=64)
+            qs = scale_tiles[kq % 2]
             lo, hi = (0 if kq + 4 < NG else 1), (2 if kq >= 0 else 1)
             nc.vector.quantize_mx(
                 out=qc[:, lo:hi, :].rearrange("p h w -> p (h w)").bitcast(FP8X4),
@@ -286,7 +367,7 @@ def tile_selfattentionmodulev2_pb_t_kernel(tc, x, attn, v_w, v_b, w_w, w_b, out)
 
         def product(pool_tile, g, term):
             dr, n = term
-            nc.scalar.activation(out=pool_tile[:], in_=vrow[g + dr][:], func=ACT.Copy, scale=a_t[:, g // H, g % H, n:n + 1])
+            nc.scalar.activation(out=pool_tile[:], in_=vrow[g + dr][:], func=ACT.Copy, scale=weight(g, n))
 
         def heads(g, after, own_row):
             if not 0 <= g < NT:
@@ -307,7 +388,7 @@ def tile_selfattentionmodulev2_pb_t_kernel(tc, x, attn, v_w, v_b, w_w, w_b, out)
 
         def mac(t, ch, g, n):
             nc.vector.scalar_tensor_tensor(
-                out=ch[:], in0=vps[t][:], scalar=a_t[:, g // H, g % H, n:n + 1], in1=ch[:],
+                out=ch[:], in0=vps[t][:], scalar=weight(g, n), in1=ch[:],
                 op0=ALU.mult, op1=ALU.add,
             )
 
@@ -317,14 +398,13 @@ def tile_selfattentionmodulev2_pb_t_kernel(tc, x, attn, v_w, v_b, w_w, w_b, out)
         def plain_sum(g):
             if not 0 <= g < NT:
                 return
-            bp, r = g // H, g % H
-            summed, added = plain_for(r)[:2]
+            summed, added = plain_for(g % H)[:2]
             acc = gacc.tile([P, CV], F32)
-            gp_product(acc, vb_bc, s_all[:, bp, r:r + 1])
+            gp_product(acc, vb_bc, bias_weight(g))
             more = []
             for dr, n in summed:
                 tmp = gtmp.tile([P, CV], F32)
-                gp_product(tmp, vrow[g + dr], a_t[:, bp, r, n:n + 1])
+                gp_product(tmp, vrow[g + dr], weight(g, n))
                 more.append(tmp)
             for tmp in more:
                 nc.gpsimd.tensor_tensor(out=acc[:], in0=acc[:], in1=tmp[:], op=ALU.add)
@@ -336,21 +416,26 @@ def tile_selfattentionmodulev2_pb_t_kernel(tc, x, attn, v_w, v_b, w_w, w_b, out)
                 product(lo, g, term)
                 lot.setdefault(g, []).append(lo)
 
-        def flush(g, row):
+        def flush(g, row, extra):
             ctx_ps = ps_c.tile([P, 4, P], F32)
             ctxs[g] = ctx_ps
             prods = [(ch, dc) for ch, dc, terms in cht[g]] + [(lo, 0) for lo in lot.get(g, [])]
             band = banded(g % H)
             n = len(prods)
-            for part in range(3):
-                if band and part < 2:
-                    for t in (2 * part, 2 * part + 1):
-                        nc.tensor.matmul(
-                            out=ctx_ps[:, t, :], lhsT=vrow[g][:, t * P:(t + 1) * P], rhs=bnd[g // 4][:, g % 4 // 2, :], start=(t == 0), stop=False,
-                        )
+            parts = 2 if band else 3
+            for part in range(parts):
+                if band and part == 0:
+                    for be in range(2):
+                        for t in range(4):
+                            nc.tensor.matmul(
+                                out=ctx_ps[:, t, be * W:(be + 1) * W], lhsT=prow[(g // 4, be)][:, t * P:(t + 1) * P],
+                                rhs=bnd[g // 4][:, be * 2 + g % 4, :], start=(be == 0 and t == 0), stop=False,
+                            )
+                elif part == 1 and extra is not None:
+                    pair_mx(extra[0], extra[1], 2)
                 else:
                     value_mx(row, 2)
-                for k in range(n * part // 3, n * (part + 1) // 3):
+                for k in range(n * part // parts, n * (part + 1) // parts):
                     pt, dc = prods[k]
                     for t in range(4):
                         nc.tensor.matmul(
@@ -365,7 +450,7 @@ def tile_selfattentionmodulev2_pb_t_kernel(tc, x, attn, v_w, v_b, w_w, w_b, out)
             qc, qs = codes[kk]
             o_ps = ps_set.tile([P, 512], F32, tag="setup")
             nc.tensor.matmul_mx(
-                out=o_ps[:], lhsT=wc[:].bitcast(FP8X4), lhsT_scale=ws[:], rhs=qc[:, 1, :].bitcast(FP8X4), rhs_scale=qs[:, 1, :],
+                out=o_ps[:], lhsT=w_op[0][0][:].bitcast(FP8X4), lhsT_scale=w_op[0][1][:], rhs=qc[:, 1, :].bitcast(FP8X4), rhs_scale=qs[:, 1, :],
                 start=True, stop=True,
             )
             ops[kk] = o_ps
@@ -376,7 +461,7 @@ def tile_selfattentionmodulev2_pb_t_kernel(tc, x, attn, v_w, v_b, w_w, w_b, out)
             nc.scalar.activation(
                 out=o_sb[:].rearrange("p b r c -> p r b c"),
                 in_=ops[kk][:].rearrange("p (r b c) -> p r b c", r=4, b=2),
-                func=ACT.Identity, bias=wb[:, 0:1],
+                func=ACT.Identity, bias=w_op[0][2][:, 0:1],
             )
             nc.sync.dma_start(
                 out=out[2 * bp:2 * bp + 2, :, r0:r0 + 4, :].rearrange("b o r c -> o b (r c)"),
@@ -388,9 +473,9 @@ def tile_selfattentionmodulev2_pb_t_kernel(tc, x, attn, v_w, v_b, w_w, w_b, out)
                 load_x((t + 14) // 4)
             if t % 4 == 0 and 0 <= (t + 8) // 4 < NG:
                 inter_x((t + 8) // 4)
-            if t % 4 == 3 and 0 <= (t + 1) // 4 < NG:
+            if t % 4 == 3 and has_pair((t + 1) // 4):
                 band_write((t + 1) // 4)
-            if t % 4 == 1 and 0 <= (t - 1) // 4 < NG:
+            if t % 4 == 1 and has_pair((t - 1) // 4):
                 band_read((t - 1) // 4)
             heads(t + 1, -1, False)
             plain_sum(t + 1)
@@ -400,6 +485,8 @@ def tile_selfattentionmodulev2_pb_t_kernel(tc, x, attn, v_w, v_b, w_w, w_b, out)
                 heads(t + 1, -1, True)
             if 0 <= t - 6 < NT:
                 evac(t - 6)
+            if t % 4 in (0, 1) and has_pair(t // 4):
+                pair_out(t // 4, t % 4)
             heads(t - 3, 3, False)
             if 0 <= t - 3 < NT:
                 lones(t - 3)
@@ -410,20 +497,30 @@ def tile_selfattentionmodulev2_pb_t_kernel(tc, x, attn, v_w, v_b, w_w, w_b, out)
                 mac(t, ch, g, n)
             if t % 4 == 2 and -4 <= (t - 10) // 4 < NG:
                 quant((t - 10) // 4)
+                if has_pair((t + 6) // 4):
+                    pair_codes((t + 6) // 4)
             for ch, g, n in todo[6:]:
                 mac(t, ch, g, n)
+            extra = None
+            if t % 4 in (3, 0) and has_pair((t + 1) // 4):
+                extra = ((t + 1) // 4, 0 if t % 4 == 3 else 1)
             if 0 <= t - 5 < NT:
-                flush(t - 5, t + 2)
+                flush(t - 5, t + 2, extra)
             else:
                 value_mx(t + 2, 1)
+                if extra is not None:
+                    pair_mx(extra[0], extra[1], 1)
             if t % 4 == 0 and 0 <= (t - 12) // 4 < NG:
                 out_mx((t - 12) // 4)
+            if t == 2:
+                w_op.append(prep_w())
             if -1 <= t < 6:
                 for i in range(PREP * (t + 1), min(PREP * (t + 2), 8 * len(BLOCKS) - 8)):
-                    prep_class(BLOCKS[1 + i // 8], i % 8, ON_S(i, t))
+                    prep_class(1 + i // 8, i % 8, ON_S(i, t))
 
-        for t in range(-14, 6):
-            slot(t)
+        with tc.manual_schedule(engines={mybir.EngineType.Pool}):
+            for t in range(-14, 6):
+                slot(t)
         with tc.manual_schedule(engines={mybir.EngineType.PE, mybir.EngineType.DVE, mybir.EngineType.Activation, mybir.EngineType.Pool}):
             for t in range(6, NT + 10):
                 slot(t)

@@ -18,7 +18,7 @@ P = 128
 DILS = (1, 2, 4)
 BLOCKS = [(0, 0, 4), (0, 4, 8), (0, 12, 4), (1, 0, 8), (1, 8, 8)]
 PREP = 6
-ON_S = lambda i, t: i % 2 == 1
+ON_S = lambda i, t: True
 NN = 27
 PLAIN = {0: ((-1, -2), (2, 4), (-4,)), 1: ((-2, -4), (2, 4), (1,)), 2: ((-1, -2), (1, 2), (-4, 0, 4)), 3: ((-1, -2), (1, 2), (-4, 0, 4))}
 BAND_DUE = {1: 3, 2: 1, 4: 3}
@@ -60,9 +60,9 @@ def tile_selfattentionmodulev2_pb_t_kernel(tc, x, attn, v_w, v_b, w_w, w_b, out)
 
     with ExitStack() as ctx:
         const = ctx.enter_context(tc.tile_pool(name="const", bufs=1))
-        ps_set = ctx.enter_context(tc.psum_pool(name="ps_set", bufs=2))
+        ps_o = ctx.enter_context(tc.psum_pool(name="ps_o", bufs=2))
         ps_v = ctx.enter_context(tc.psum_pool(name="ps_v", bufs=4))
-        ps_c = ctx.enter_context(tc.psum_pool(name="ps_c", bufs=2))
+        ps_p = ctx.enter_context(tc.psum_pool(name="ps_p", bufs=1))
 
         xraw = ctx.enter_context(tc.tile_pool(name="xraw", bufs=2))
         qin = ctx.enter_context(tc.tile_pool(name="qin", bufs=2))
@@ -147,12 +147,12 @@ def tile_selfattentionmodulev2_pb_t_kernel(tc, x, attn, v_w, v_b, w_w, w_b, out)
                 nc.gpsimd.memset(sc[:].rearrange("p h w -> p (h w)").bitcast(I32), 0)
                 scale_tiles.append(sc)
 
-            s_tmp = const.tile([P, 8, 4, NN], F32)
+            s_tmp = const.tile([P, NN, 4, 8], F32)
             a_t, s_all, strip = [], [], []
             for k, (bp, q0, nq) in enumerate(BLOCKS):
-                a_blk = const.tile([P, nq, 4, NN], F32, name="a_t%d" % k)
-                s_blk = const.tile([P, nq, 4], F32, name="s_all%d" % k)
-                p_blk = const.tile([P, nq // 4, 4, 2, 2, 9], F32, name="strip%d" % k)
+                a_blk = const.tile([P, NN, 4, nq], F32, name="a_t%d" % k)
+                s_blk = const.tile([P, 4, nq], F32, name="s_all%d" % k)
+                p_blk = const.tile([P, 4, nq // 4, 2, 2, 9], F32, name="strip%d" % k)
                 nc.gpsimd.memset(p_blk[:], 0.0)
                 a_t.append(a_blk)
                 s_all.append(s_blk)
@@ -166,11 +166,11 @@ def tile_selfattentionmodulev2_pb_t_kernel(tc, x, attn, v_w, v_b, w_w, w_b, out)
 
             def weight(g, n):
                 k, q, s = place(g)
-                return a_t[k][:, q, s, n:n + 1]
+                return a_t[k][:, n, s, q:q + 1]
 
             def bias_weight(g):
                 k, q, s = place(g)
-                return s_all[k][:, q, s:s + 1]
+                return s_all[k][:, s, q:q + 1]
 
             classes = [(0, 1, 9)]
             for l, d in enumerate(DILS):
@@ -191,45 +191,45 @@ def tile_selfattentionmodulev2_pb_t_kernel(tc, x, attn, v_w, v_b, w_w, w_b, out)
                 bp, q0, nq = BLOCKS[block]
                 a_blk = a_t[block]
                 if k == len(classes):
-                    nc.vector.tensor_tensor(out=a_blk[:, :, :, 4], in0=a_blk[:, :, :, 4], in1=a_blk[:, :, :, 13], op=ALU.add)
-                    nc.vector.tensor_tensor(out=a_blk[:, :, :, 4], in0=a_blk[:, :, :, 4], in1=a_blk[:, :, :, 22], op=ALU.add)
-                    s_blk = strip[block][:].rearrange("p k s i j e -> p k s (i j) e")
-                    p_blk = a_blk[:].rearrange("p (k i) s n -> p k s i n", i=4)
-                    for e, n in ((0, 23), (2, 14), (3, 5), (4, 4), (5, 3), (6, 12), (8, 21)):
-                        nc.vector.tensor_copy(out=s_blk[:, :, :, 0:4:3, e], in_=p_blk[:, :, :, 0:2, n])
-                    for e in (3, 4, 5):
-                        nc.vector.tensor_copy(out=s_blk[:, :, :, 2, e], in_=p_blk[:, :, :, 0, 11 - e])
-                        nc.vector.tensor_copy(out=s_blk[:, :, :, 1, e], in_=p_blk[:, :, :, 1, 5 - e])
+                    nc.vector.tensor_tensor(out=a_blk[:, 4], in0=a_blk[:, 4], in1=a_blk[:, 13], op=ALU.add)
+                    nc.vector.tensor_tensor(out=a_blk[:, 4], in0=a_blk[:, 4], in1=a_blk[:, 22], op=ALU.add)
+                    s_blk = strip[block][:].rearrange("p s k i j e -> p (s k) (i j) e")
+                    p_blk = a_blk[:].rearrange("p n s (k i) -> p (s k) i n", i=4)
+                    nc.vector.tensor_copy(out=s_blk[:, :, 0:4:3, 0:9:8], in_=p_blk[:, :, 0:2, 23:20:-2])
+                    nc.vector.tensor_copy(out=s_blk[:, :, 0:4:3, 2:7:4], in_=p_blk[:, :, 0:2, 14:11:-2])
+                    nc.vector.tensor_copy(out=s_blk[:, :, 0:4:3, 3:6], in_=p_blk[:, :, 0:2, 5:2:-1])
+                    nc.vector.tensor_copy(out=s_blk[:, :, 2, 3:6], in_=p_blk[:, :, 0, 8:5:-1])
+                    nc.vector.tensor_copy(out=s_blk[:, :, 1, 3:6], in_=p_blk[:, :, 1, 2::-1])
                     return
                 dc, n0, cnt = classes[k]
-                at_ps = ps_set.tile([P, 8, P], BF16, tag="setup")
+                at_ps = ps_o.tile([P, 8, P], BF16, tag="o")
                 for q in range(nq):
                     s0 = PADA + (q0 + q) * P - dc
                     nc.tensor.transpose(out=at_ps[:, q, :], in_=a_raw[bp][:, s0:s0 + P], identity=ident_b[:])
-                view = at_ps[:, 0:nq].rearrange("p q (n s) -> p q s n", s=4)
-                src = view[:, :, :, n0:n0 + 3 * cnt - 2:3]
-                masked(on_scalar, a_blk[:, :, :, n0:n0 + 3 * cnt - 2:3], src, dc)
+                view = at_ps[:, 0:nq].rearrange("p q (n s) -> p n s q", s=4)
+                src = view[:, n0:n0 + 3 * cnt - 2:3]
+                masked(on_scalar, a_blk[:, n0:n0 + 3 * cnt - 2:3], src, dc)
                 if dc != 0:
                     return
-                masked(on_scalar, s_tmp[:, 0:nq, :, n0:n0 + 3 * cnt - 2:3], src, 0)
+                masked(on_scalar, s_tmp[:, n0:n0 + 3 * cnt - 2:3, :, 0:nq], src, 0)
                 for odc, m0, ocnt in classes[1:]:
-                    masked(on_scalar, s_tmp[:, 0:nq, :, m0:m0 + 7:3], view[:, :, :, m0:m0 + 7:3], -odc)
+                    masked(on_scalar, s_tmp[:, m0:m0 + 7:3, :, 0:nq], view[:, m0:m0 + 7:3], -odc)
                 for l, d in enumerate(DILS):
                     top, end = min(d - q0, nq), min(q0 + nq - (16 - d), nq)
                     if top > 0:
-                        nc.vector.memset(s_tmp[:, 0:top, 0, 9 * l:9 * l + 3], 0.0)
+                        nc.vector.memset(s_tmp[:, 9 * l:9 * l + 3, 0, 0:top], 0.0)
                     if end > 0:
-                        nc.vector.memset(s_tmp[:, nq - end:nq, 3, 9 * l + 6:9 * l + 9], 0.0)
-                nc.vector.tensor_reduce(out=s_all[block][:], in_=s_tmp[:, 0:nq], axis=AX.X, op=ALU.add)
+                        nc.vector.memset(s_tmp[:, 9 * l + 6:9 * l + 9, 3, nq - end:nq], 0.0)
+                nc.vector.tensor_reduce(out=s_all[block][:], in_=s_tmp[:, :, :, 0:nq].rearrange("p n s q -> p s q n"), axis=AX.X, op=ALU.add)
 
             for k in range(len(classes) + 1):
-                prep_class(0, k, k % 2 == 1)
+                prep_class(0, k, k != 0)
 
             vw_perm = setup.tile([P, 4, 4, P], BF16)
             nc.vector.tensor_copy(out=vw_perm[:], in_=vw_sb[:].rearrange("a t (p j) -> a t j p", j=4))
             vw_grp = setup.tile([P, 4, P, 4], BF16, align_bytes=64)
             for t in range(4):
-                tp = ps_set.tile([P, 8, P], BF16, tag="setup")
+                tp = ps_o.tile([P, 8, P], BF16, tag="o")
                 for j in range(4):
                     nc.tensor.transpose(out=tp[:, j, :], in_=vw_perm[:, t, j, :], identity=ident_b[:])
                 nc.vector.tensor_copy(out=vw_grp[:, t], in_=tp[:, 0:4, :].rearrange("p j a -> p a j"))
@@ -239,10 +239,10 @@ def tile_selfattentionmodulev2_pb_t_kernel(tc, x, attn, v_w, v_b, w_w, w_b, out)
             vb_bc = const.tile([P, CV], F32)
             nc.vector.tensor_copy(out=vb_bc[:].rearrange("p (t a) -> p t a", t=4), in_=vb_raw[:].rearrange("p (a t) -> p t a", t=4))
 
-        chpool = ctx.enter_context(tc.tile_pool(name="chpool", bufs=40))
+        chpool = ctx.enter_context(tc.tile_pool(name="chpool", bufs=41))
         lopool = ctx.enter_context(tc.tile_pool(name="lopool", bufs=10))
         pair = ctx.enter_context(tc.tile_pool(name="pair", bufs=2))
-        pvals = ctx.enter_context(tc.tile_pool(name="pvals", bufs=5))
+        pvals = ctx.enter_context(tc.tile_pool(name="pvals", bufs=4))
         bands = ctx.enter_context(tc.tile_pool(name="bands", bufs=3))
         opool = ctx.enter_context(tc.tile_pool(name="opool", bufs=2))
 
@@ -250,7 +250,7 @@ def tile_selfattentionmodulev2_pb_t_kernel(tc, x, attn, v_w, v_b, w_w, w_b, out)
             w_perm = const.tile([P, 4, P], BF16)
             nc.vector.tensor_copy(out=w_perm[:], in_=w_sb[:].rearrange("a (p j) -> a j p", j=4))
             w_grp = const.tile([P, P, 4], BF16, align_bytes=64)
-            tpw = ps_set.tile([P, 8, P], BF16, tag="setup")
+            tpw = ps_o.tile([P, 8, P], BF16, tag="o")
             for j in range(4):
                 nc.tensor.transpose(out=tpw[:, j, :], in_=w_perm[:, j, :], identity=ident_b[:])
             nc.vector.tensor_copy(out=w_grp[:], in_=tpw[:, 0:4, :].rearrange("p j a -> p a j"))
@@ -273,7 +273,7 @@ def tile_selfattentionmodulev2_pb_t_kernel(tc, x, attn, v_w, v_b, w_w, w_b, out)
             for be in range(2):
                 for i in range(2):
                     dst = scratch(IMG_ROW + 1, i * W * IMG_ROW + ((kk % 3) * 4 + be * 2) * SLOT, 2 * SLOT, W).rearrange("q (s w) -> q s w", w=SLOT)
-                    nc.sync.dma_start(out=dst[:, :, 0:9], in_=strip[k][be * W:(be + 1) * W, q // 4, s, i])
+                    nc.sync.dma_start(out=dst[:, :, 0:9], in_=strip[k][be * W:(be + 1) * W, s, q // 4, i])
 
         def band_read(kk):
             src = scratch(IMG_ROW, (kk % 3) * 4 * SLOT, 4 * SLOT, P).rearrange("q (s w) -> q s w", w=SLOT)
@@ -296,7 +296,7 @@ def tile_selfattentionmodulev2_pb_t_kernel(tc, x, attn, v_w, v_b, w_w, w_b, out)
         def pair_mx(kk, be, times):
             pc, ps = pairs[kk]
             if (kk, be) not in pps:
-                p_ps = ps_set.tile([P, CV], F32, tag="setup")
+                p_ps = ps_o.tile([P, CV], F32, tag="o")
                 pps[(kk, be)] = p_ps
             for k in range(times):
                 nc.tensor.matmul_mx(
@@ -417,38 +417,54 @@ def tile_selfattentionmodulev2_pb_t_kernel(tc, x, attn, v_w, v_b, w_w, w_b, out)
                 lot.setdefault(g, []).append(lo)
 
         def flush(g, row, extra):
-            ctx_ps = ps_c.tile([P, 4, P], F32)
-            ctxs[g] = ctx_ps
+            r = g % H
+            band, j = banded(r), r % 4
+            if not band:
+                ctx_ps = ps_o.tile([P, 4, P], F32, tag="o")
+                ctxs[g] = [ctx_ps]
+            elif j == 0:
+                pair_a = ps_p.tile([P, 2, 2, P], F32)
+                pair_b = ps_p.tile([P, 2, 2, P], F32)
+                ctxs[g] = ctxs[g + 1] = [pair_a, pair_b]
             prods = [(ch, dc) for ch, dc, terms in cht[g]] + [(lo, 0) for lo in lot.get(g, [])]
-            band = banded(g % H)
             n = len(prods)
-            parts = 2 if band else 3
+            parts = 2 if band and j == 0 else 3
             for part in range(parts):
-                if band and part == 0:
-                    for be in range(2):
-                        for t in range(4):
-                            nc.tensor.matmul(
-                                out=ctx_ps[:, t, be * W:(be + 1) * W], lhsT=prow[(g // 4, be)][:, t * P:(t + 1) * P],
-                                rhs=bnd[g // 4][:, be * 2 + g % 4, :], start=(be == 0 and t == 0), stop=False,
-                            )
-                elif part == 1 and extra is not None:
+                if part == 1 and extra is not None:
                     pair_mx(extra[0], extra[1], 2)
                 else:
-                    value_mx(row, 2)
+                    value_mx(row, 1 if parts == 2 else 2)
+                if band and j == 0 and part == 0:
+                    for t in range(4):
+                        for be in range(2):
+                            nc.tensor.matmul(
+                                out=ctxs[g][t // 2][:, t % 2, :, be * W:(be + 1) * W], lhsT=prow[(g // 4, be)][:, t * P:(t + 1) * P],
+                                rhs=bnd[g // 4][:, be * 2:be * 2 + 2, :], start=(t % 2 == 0 and be == 0), stop=False,
+                            )
                 for k in range(n * part // parts, n * (part + 1) // parts):
                     pt, dc = prods[k]
                     for t in range(4):
+                        if band:
+                            dst, last = ctxs[g][t // 2][:, t % 2, j, :], j == 1 and k == n - 1 and t % 2 == 1
+                        else:
+                            dst, last = ctxs[g][0][:, t, :], k == n - 1 and t == 3
                         nc.tensor.matmul(
-                            out=ctx_ps[:, t, :], lhsT=pt[:, t * P:(t + 1) * P], rhs=perm[dc],
-                            start=(k == 0 and t == 0 and not band), stop=(k == n - 1 and t == 3), is_transpose=True,
+                            out=dst, lhsT=pt[:, t * P:(t + 1) * P], rhs=perm[dc],
+                            start=(k == 0 and t == 0 and not band), stop=last, is_transpose=True,
                         )
 
         def evac(g):
-            nc.scalar.copy(out=stage(g // 4)[:, 1, g % 4], in_=ctxs[g][:].rearrange("p t u -> p u t"))
+            j = g % 4
+            st = stage(g // 4)
+            if not banded(g % H):
+                nc.scalar.copy(out=st[:, 1, j], in_=ctxs[g][0][:].rearrange("p t u -> p u t"))
+            elif j == 1:
+                for half in range(2):
+                    nc.scalar.copy(out=st[:, 1, 0:2, :, 2 * half:2 * half + 2], in_=ctxs[g][half][:].rearrange("p t j u -> p j u t"))
 
         def out_mx(kk):
             qc, qs = codes[kk]
-            o_ps = ps_set.tile([P, 512], F32, tag="setup")
+            o_ps = ps_o.tile([P, 512], F32, tag="o")
             nc.tensor.matmul_mx(
                 out=o_ps[:], lhsT=w_op[0][0][:].bitcast(FP8X4), lhsT_scale=w_op[0][1][:], rhs=qc[:, 1, :].bitcast(FP8X4), rhs_scale=qs[:, 1, :],
                 start=True, stop=True,
@@ -485,8 +501,8 @@ def tile_selfattentionmodulev2_pb_t_kernel(tc, x, attn, v_w, v_b, w_w, w_b, out)
                 heads(t + 1, -1, True)
             if 0 <= t - 6 < NT:
                 evac(t - 6)
-            if t % 4 in (0, 1) and has_pair(t // 4):
-                pair_out(t // 4, t % 4)
+            if t % 4 in (2, 3) and has_pair(t // 4):
+                pair_out(t // 4, t % 4 - 2)
             heads(t - 3, 3, False)
             if 0 <= t - 3 < NT:
                 lones(t - 3)
@@ -497,13 +513,13 @@ def tile_selfattentionmodulev2_pb_t_kernel(tc, x, attn, v_w, v_b, w_w, w_b, out)
                 mac(t, ch, g, n)
             if t % 4 == 2 and -4 <= (t - 10) // 4 < NG:
                 quant((t - 10) // 4)
-                if has_pair((t + 6) // 4):
-                    pair_codes((t + 6) // 4)
+                if has_pair((t + 2) // 4):
+                    pair_codes((t + 2) // 4)
             for ch, g, n in todo[6:]:
                 mac(t, ch, g, n)
             extra = None
-            if t % 4 in (3, 0) and has_pair((t + 1) // 4):
-                extra = ((t + 1) // 4, 0 if t % 4 == 3 else 1)
+            if t % 4 in (1, 2) and has_pair(t // 4):
+                extra = (t // 4, t % 4 - 1)
             if 0 <= t - 5 < NT:
                 flush(t - 5, t + 2, extra)
             else:

@@ -18,9 +18,10 @@ P = 128
 DILS = (1, 2, 4)
 BLOCKS = [(0, 0, 4), (0, 4, 8), (0, 12, 4), (1, 0, 8), (1, 8, 8)]
 PREP = 6
+GL = 3
 ON_S = lambda i, t: True
 NN = 27
-PLAIN = {0: ((-1, -2), (2, 4), (-4,)), 1: ((-2, -4), (2, 4), (1,)), 2: ((-1, -2), (1, 2), (-4, 0, 4)), 3: ((-1, -2), (1, 2), (-4, 0, 4))}
+PLAIN = {0: ((-1, -2), (2, 4), (), (-4,)), 1: ((-2, -4), (2, 4), (1,), ()), 2: ((-1, -2), (1, 2), (0, 4), (-4,)), 3: ((-2, -4), (1, 2), (-1, 0, 4), ())}
 BAND_DUE = {1: 3, 2: 1, 4: 3}
 PADA = 16
 IMG_ROW = H * W
@@ -28,26 +29,27 @@ SLOT = 72
 FLOPS = 2 * B * H * W * (CIN * CV + CV * COUT + 27 * CV)
 
 
-def banded(r):
-    return r % 4 < 2 and r >= 4
+def banded(g):
+    return g % 4 < 2 and g >= 4
 
 
-def columns_for(r):
-    band = banded(r)
+def columns_for(g):
+    band, r = banded(g), g % H
     cols = []
     for l, d in enumerate(DILS):
         rows = [i for i in (0, 1, 2) if 0 <= r + (i - 1) * d < H and not (band and (i == 1 or d == 1 and i == (2, 0)[r % 4]))]
-        for j in (0, 2):
+        for j in (0, 2) if rows else ():
             cols.append(((j - 1) * d, [((i - 1) * d, 9 * l + 3 * i + j) for i in rows], BAND_DUE[d] if band else -1))
     return cols
 
 
-def plain_for(r):
+def plain_for(g):
+    r = g % H
     term = {0: (0, 4)}
     for l, d in enumerate(DILS):
         term[-d], term[d] = (-d, 9 * l + 1), (d, 9 * l + 7)
-    summed, added, by_scalar = PLAIN[r % 4 if banded(r) else 2 + r % 2]
-    return [[term[s] for s in shifts if 0 <= r + s < H] for shifts in (summed, added, by_scalar)]
+    summed, added, by_scalar, by_gpsimd = PLAIN[g % 4 if banded(g) else 2 + g % 2]
+    return [[term[s] for s in shifts if 0 <= r + s < H] for shifts in (summed, added, by_scalar, by_gpsimd)]
 
 
 def tile_selfattentionmodulev2_pb_t_kernel(tc, x, attn, v_w, v_b, w_w, w_b, out):
@@ -68,7 +70,7 @@ def tile_selfattentionmodulev2_pb_t_kernel(tc, x, attn, v_w, v_b, w_w, w_b, out)
         qin = ctx.enter_context(tc.tile_pool(name="qin", bufs=2))
         qout = ctx.enter_context(tc.tile_pool(name="qout", bufs=2))
         vpool = ctx.enter_context(tc.tile_pool(name="vpool", bufs=10))
-        gacc = ctx.enter_context(tc.tile_pool(name="gacc", bufs=8))
+        gacc = ctx.enter_context(tc.tile_pool(name="gacc", bufs=5))
         gtmp = ctx.enter_context(tc.tile_pool(name="gtmp", bufs=2))
         raws = {}
 
@@ -239,8 +241,9 @@ def tile_selfattentionmodulev2_pb_t_kernel(tc, x, attn, v_w, v_b, w_w, w_b, out)
             vb_bc = const.tile([P, CV], F32)
             nc.vector.tensor_copy(out=vb_bc[:].rearrange("p (t a) -> p t a", t=4), in_=vb_raw[:].rearrange("p (a t) -> p t a", t=4))
 
-        chpool = ctx.enter_context(tc.tile_pool(name="chpool", bufs=41))
-        lopool = ctx.enter_context(tc.tile_pool(name="lopool", bufs=10))
+        glpool = ctx.enter_context(tc.tile_pool(name="glpool", bufs=GL))
+        chpool = ctx.enter_context(tc.tile_pool(name="chpool", bufs=37))
+        lopool = ctx.enter_context(tc.tile_pool(name="lopool", bufs=8))
         pair = ctx.enter_context(tc.tile_pool(name="pair", bufs=2))
         pvals = ctx.enter_context(tc.tile_pool(name="pvals", bufs=4))
         bands = ctx.enter_context(tc.tile_pool(name="bands", bufs=3))
@@ -315,7 +318,7 @@ def tile_selfattentionmodulev2_pb_t_kernel(tc, x, attn, v_w, v_b, w_w, w_b, out)
             prow[(kk, be)] = pv
 
         def has_pair(kk):
-            return 0 <= kk < NG and banded(4 * kk % H)
+            return 0 <= kk < NG and banded(4 * kk)
 
         def stage(kq):
             if kq not in stages:
@@ -372,12 +375,12 @@ def tile_selfattentionmodulev2_pb_t_kernel(tc, x, attn, v_w, v_b, w_w, w_b, out)
         def heads(g, after, own_row):
             if not 0 <= g < NT:
                 return
-            todo = [(dc, terms) for dc, terms, due in columns_for(g % H) if due == after]
+            todo = [(dc, terms) for dc, terms, due in columns_for(g) if due == after]
             for dc, terms in todo:
                 if (terms[0][0] == 0) == own_row:
                     ch = chpool.tile([P, CV], F32)
                     product(ch, g, terms[0])
-                    cht.setdefault(g, []).append((ch, dc, terms[1:]))
+                    cht.setdefault(g, []).append((ch[:], dc, terms[1:]))
 
         def macs_of(t):
             todo = []
@@ -388,37 +391,44 @@ def tile_selfattentionmodulev2_pb_t_kernel(tc, x, attn, v_w, v_b, w_w, w_b, out)
 
         def mac(t, ch, g, n):
             nc.vector.scalar_tensor_tensor(
-                out=ch[:], in0=vps[t][:], scalar=weight(g, n), in1=ch[:],
+                out=ch, in0=vps[t][:], scalar=weight(g, n), in1=ch,
                 op0=ALU.mult, op1=ALU.add,
             )
 
-        def gp_product(gp, src, factor):
-            nc.gpsimd.tensor_scalar(out=gp[:], in0=src[:], scalar1=factor, scalar2=0.0, op0=ALU.mult, op1=ALU.add)
+        def gp_product(dst, src, factor):
+            nc.gpsimd.tensor_scalar(out=dst, in0=src, scalar1=factor, scalar2=0.0, op0=ALU.mult, op1=ALU.add)
 
-        def plain_sum(g):
+        def plain_sums(g):
             if not 0 <= g < NT:
                 return
-            summed, added = plain_for(g % H)[:2]
-            acc = gacc.tile([P, CV], F32)
-            gp_product(acc, vb_bc, bias_weight(g))
+            acc = gacc.tile([P, 2, CV], F32)
+            summed = [plain_for(g + i)[0] for i in range(2)]
+            for i in range(2):
+                gp_product(acc[:, i], vb_bc[:], bias_weight(g + i))
+                cht.setdefault(g + i, []).append((acc[:, i], 0, plain_for(g + i)[1]))
             more = []
-            for dr, n in summed:
-                tmp = gtmp.tile([P, CV], F32)
-                gp_product(tmp, vrow[g + dr], weight(g, n))
-                more.append(tmp)
-            for tmp in more:
-                nc.gpsimd.tensor_tensor(out=acc[:], in0=acc[:], in1=tmp[:], op=ALU.add)
-            cht.setdefault(g, []).append((acc, 0, added))
+            for k in range(max(len(s) for s in summed)):
+                tmp = gtmp.tile([P, 2, CV], F32)
+                both = [i for i in range(2) if k < len(summed[i])]
+                for i in both:
+                    dr, n = summed[i][k]
+                    gp_product(tmp[:, i], vrow[g + i + dr][:], weight(g + i, n))
+                more.append((tmp, both[0], both[-1] + 1))
+            for tmp, lo, hi in more:
+                nc.gpsimd.tensor_tensor(out=acc[:, lo:hi], in0=acc[:, lo:hi], in1=tmp[:, lo:hi], op=ALU.add)
 
         def lones(g):
-            for term in plain_for(g % H)[2]:
+            for dr, n in plain_for(g)[3]:
+                gl = glpool.tile([P, CV], F32)
+                gp_product(gl[:], vrow[g + dr][:], weight(g, n))
+                lot.setdefault(g, []).append(gl[:])
+            for term in plain_for(g)[2]:
                 lo = lopool.tile([P, CV], F32)
                 product(lo, g, term)
-                lot.setdefault(g, []).append(lo)
+                lot.setdefault(g, []).append(lo[:])
 
         def flush(g, row, extra):
-            r = g % H
-            band, j = banded(r), r % 4
+            band, j = banded(g), g % 4
             if not band:
                 ctx_ps = ps_o.tile([P, 4, P], F32, tag="o")
                 ctxs[g] = [ctx_ps]
@@ -456,7 +466,7 @@ def tile_selfattentionmodulev2_pb_t_kernel(tc, x, attn, v_w, v_b, w_w, w_b, out)
         def evac(g):
             j = g % 4
             st = stage(g // 4)
-            if not banded(g % H):
+            if not banded(g):
                 nc.scalar.copy(out=st[:, 1, j], in_=ctxs[g][0][:].rearrange("p t u -> p u t"))
             elif j == 1:
                 for half in range(2):
@@ -494,11 +504,12 @@ def tile_selfattentionmodulev2_pb_t_kernel(tc, x, attn, v_w, v_b, w_w, w_b, out)
             if t % 4 == 1 and has_pair((t - 1) // 4):
                 band_read((t - 1) // 4)
             heads(t + 1, -1, False)
-            plain_sum(t + 1)
-            heads(t - 1, 1, False)
+            if t % 2 == 1:
+                plain_sums(t + 1)
             if 0 <= t + 1 < NT:
                 value_out(t + 1)
                 heads(t + 1, -1, True)
+            heads(t - 1, 1, False)
             if 0 <= t - 6 < NT:
                 evac(t - 6)
             if t % 4 in (2, 3) and has_pair(t // 4):

@@ -224,9 +224,6 @@ def tile_selfattentionmodulev2_pb_t_kernel(tc, x, attn, v_w, v_b, w_w, w_b, out)
                         nc.vector.memset(s_tmp[:, 9 * l + 6:9 * l + 9, 3, nq - end:nq], 0.0)
                 nc.vector.tensor_reduce(out=s_all[block][:], in_=s_tmp[:, :, :, 0:nq].rearrange("p n s q -> p s q n"), axis=AX.X, op=ALU.add)
 
-            for k in range(len(classes) + 1):
-                prep_class(0, k, k != 0)
-
             vw_perm = setup.tile([P, 4, 4, P], BF16)
             nc.vector.tensor_copy(out=vw_perm[:], in_=vw_sb[:].rearrange("a t (p j) -> a t j p", j=4))
             vw_grp = setup.tile([P, 4, P, 4], BF16, align_bytes=64)
@@ -234,12 +231,19 @@ def tile_selfattentionmodulev2_pb_t_kernel(tc, x, attn, v_w, v_b, w_w, w_b, out)
                 tp = ps_o.tile([P, 8, P], BF16, tag="o")
                 for j in range(4):
                     nc.tensor.transpose(out=tp[:, j, :], in_=vw_perm[:, t, j, :], identity=ident_b[:])
-                nc.vector.tensor_copy(out=vw_grp[:, t], in_=tp[:, 0:4, :].rearrange("p j a -> p a j"))
+                grouped = tp[:, 0:4, :].rearrange("p j a -> p a j")
+                if t % 2 == 0:
+                    nc.vector.tensor_copy(out=vw_grp[:, t], in_=grouped)
+                else:
+                    nc.scalar.copy(out=vw_grp[:, t], in_=grouped)
             vwc = const.tile([P, CV], U32, align_bytes=64)
             vws = const.tile([P, CV], U8, align_bytes=64)
             nc.vector.quantize_mx(out=vwc[:].bitcast(FP8X4), scales=vws[:], in_=vw_grp[:].rearrange("p t a j -> p (t a j)"))
             vb_bc = const.tile([P, CV], F32)
             nc.vector.tensor_copy(out=vb_bc[:].rearrange("p (t a) -> p t a", t=4), in_=vb_raw[:].rearrange("p (a t) -> p t a", t=4))
+
+            for k in range(len(classes) + 1):
+                prep_class(0, k, k != 0)
 
         glpool = ctx.enter_context(tc.tile_pool(name="glpool", bufs=GL))
         chpool = ctx.enter_context(tc.tile_pool(name="chpool", bufs=37))
@@ -287,13 +291,16 @@ def tile_selfattentionmodulev2_pb_t_kernel(tc, x, attn, v_w, v_b, w_w, w_b, out)
         def pair_codes(kk):
             qc, qs = codes[kk - 4]
             pc = pair.tile([P, 256], I32, align_bytes=64)
-            nc.vector.tensor_copy(
-                out=pc[:].rearrange("p (b i c) -> p i b c", b=2, i=2), in_=qc[:, 0, 0:256].rearrange("p (i b c) -> p i b c", i=2, b=2).bitcast(I32),
-            )
             ps = pair.tile([P, 256], U8, align_bytes=64)
-            nc.vector.tensor_copy(
-                out=ps[:].rearrange("p (b i c) -> p i b c", b=2, i=2), in_=qs[:, 0, 0:256].rearrange("p (i b c) -> p i b c", i=2, b=2),
-            )
+            for be in range(2):
+                nc.sync.dma_start(
+                    out=pc[:, be * P:(be + 1) * P].rearrange("p (i c) -> p i c", i=2),
+                    in_=qc[:, 0, 0:256].bitcast(I32).rearrange("p (i b c) -> p b i c", i=2, b=2)[:, be],
+                )
+                nc.sync.dma_start(
+                    out=ps[:, be * P:(be + 1) * P].bitcast(I32).rearrange("p (i c) -> p i c", i=2),
+                    in_=qs[:, 0, 0:256].bitcast(I32).rearrange("p (i b c) -> p b i c", i=2, b=2)[:, be],
+                )
             pairs[kk] = (pc, ps)
 
         def pair_mx(kk, be, times):
@@ -438,29 +445,31 @@ def tile_selfattentionmodulev2_pb_t_kernel(tc, x, attn, v_w, v_b, w_w, w_b, out)
                 ctxs[g] = ctxs[g + 1] = [pair_a, pair_b]
             prods = [(ch, dc) for ch, dc, terms in cht[g]] + [(lo, 0) for lo in lot.get(g, [])]
             n = len(prods)
-            parts = 2 if band and j == 0 else 3
+            first = band and j == 0
+            parts = 2 if band else 3
             for part in range(parts):
                 if part == 1 and extra is not None:
-                    pair_mx(extra[0], extra[1], 2)
+                    pair_mx(extra[0], extra[1], 1 if first else 2)
                 else:
-                    value_mx(row, 1 if parts == 2 else 2)
-                if band and j == 0 and part == 0:
-                    for t in range(4):
+                    value_mx(row, 1 if first else 2)
+                quarters, mine = range(4), prods[n * part // parts:n * (part + 1) // parts]
+                if first:
+                    quarters, mine = range(2 * part, 2 * part + 2), prods
+                    for t in quarters:
                         for be in range(2):
                             nc.tensor.matmul(
-                                out=ctxs[g][t // 2][:, t % 2, :, be * W:(be + 1) * W], lhsT=prow[(g // 4, be)][:, t * P:(t + 1) * P],
+                                out=ctxs[g][part][:, t % 2, :, be * W:(be + 1) * W], lhsT=prow[(g // 4, be)][:, t * P:(t + 1) * P],
                                 rhs=bnd[g // 4][:, be * 2:be * 2 + 2, :], start=(t % 2 == 0 and be == 0), stop=False,
                             )
-                for k in range(n * part // parts, n * (part + 1) // parts):
-                    pt, dc = prods[k]
-                    for t in range(4):
+                for pt, dc in mine:
+                    for t in quarters:
                         if band:
-                            dst, last = ctxs[g][t // 2][:, t % 2, j, :], j == 1 and k == n - 1 and t % 2 == 1
+                            dst, last = ctxs[g][t // 2][:, t % 2, j, :], j == 1 and pt is prods[-1][0] and t % 2 == 1
                         else:
-                            dst, last = ctxs[g][0][:, t, :], k == n - 1 and t == 3
+                            dst, last = ctxs[g][0][:, t, :], pt is prods[-1][0] and t == 3
                         nc.tensor.matmul(
                             out=dst, lhsT=pt[:, t * P:(t + 1) * P], rhs=perm[dc],
-                            start=(k == 0 and t == 0 and not band), stop=last, is_transpose=True,
+                            start=(pt is prods[0][0] and t == 0 and not band), stop=last, is_transpose=True,
                         )
 
         def evac(g):

from contextlib import ExitStack

import concourse.mybir as mybir
from concourse.masks import make_identity

FP8X4 = mybir.dt.float8_e4m3fn_x4
BF16 = mybir.dt.bfloat16
F32 = mybir.dt.float32
U32 = mybir.dt.uint32
U8 = mybir.dt.uint8
I32 = mybir.dt.int32
ALU = mybir.AluOpType
ACT = mybir.ActivationFunctionType
AX = mybir.AxisListType

B, CIN, CV, COUT, H, W = 4, 512, 512, 128, 64, 64
P = 128
DILS = (1, 2, 4)
BLOCKS = [(0, 0, 4), (0, 4, 8), (0, 12, 4), (1, 0, 8), (1, 8, 8)]
PREP = 6
GL = 3
ON_S = lambda i, t: True
NN = 27
PLAIN = {0: ((-1, -2), (2, 4), (), (-4,)), 1: ((-2, -4), (2, 4), (1,), ()), 2: ((-1, -2), (1, 2), (0, 4), (-4,)), 3: ((-2, -4), (1, 2), (-1, 0, 4), ())}
BAND_DUE = {1: 3, 2: 1, 4: 3}
PADA = 16
IMG_ROW = H * W
SLOT = 72
FLOPS = 2 * B * H * W * (CIN * CV + CV * COUT + 27 * CV)


def banded(g):
    return g % 4 < 2 and g >= 4


def columns_for(g):
    band, r = banded(g), g % H
    cols = []
    for l, d in enumerate(DILS):
        rows = [i for i in (0, 1, 2) if 0 <= r + (i - 1) * d < H and not (band and (i == 1 or d == 1 and i == (2, 0)[r % 4]))]
        for j in (0, 2) if rows else ():
            cols.append(((j - 1) * d, [((i - 1) * d, 9 * l + 3 * i + j) for i in rows], BAND_DUE[d] if band else -1))
    return cols


def plain_for(g):
    r = g % H
    term = {0: (0, 4)}
    for l, d in enumerate(DILS):
        term[-d], term[d] = (-d, 9 * l + 1), (d, 9 * l + 7)
    summed, added, by_scalar, by_gpsimd = PLAIN[g % 4 if banded(g) else 2 + g % 2]
    return [[term[s] for s in shifts if 0 <= r + s < H] for shifts in (summed, added, by_scalar, by_gpsimd)]


def tile_selfattentionmodulev2_pb_t_kernel(tc, x, attn, v_w, v_b, w_w, w_b, out):
    nc = tc.nc
    out_flat = out.rearrange("b o r c -> (b o r c)")

    def scratch(pitch, first, width, rows):
        base = 2 * P * IMG_ROW + 48 * W + first
        return out_flat[base:base + rows * pitch].rearrange("(q w) -> q w", w=pitch)[:, 0:width]

    with ExitStack() as ctx:
        const = ctx.enter_context(tc.tile_pool(name="const", bufs=1))
        ps_o = ctx.enter_context(tc.psum_pool(name="ps_o", bufs=2))
        ps_v = ctx.enter_context(tc.psum_pool(name="ps_v", bufs=4))
        ps_p = ctx.enter_context(tc.psum_pool(name="ps_p", bufs=1))

        xraw = ctx.enter_context(tc.tile_pool(name="xraw", bufs=2))
        qin = ctx.enter_context(tc.tile_pool(name="qin", bufs=2))
        qout = ctx.enter_context(tc.tile_pool(name="qout", bufs=2))
        vpool = ctx.enter_context(tc.tile_pool(name="vpool", bufs=10))
        gacc = ctx.enter_context(tc.tile_pool(name="gacc", bufs=5))
        gtmp = ctx.enter_context(tc.tile_pool(name="gtmp", bufs=2))
        raws = {}

        def load_x(kk):
            bp, k4 = kk // 16, kk % 16
            raw = xraw.tile([P, 4, 4, 2, W], BF16)
            for be in range(2):
                nc.sync.dma_start(
                    out=raw[:, :, :, be, :],
                    in_=x[2 * bp + be].rearrange("(p j) r c -> p j r c", j=4)[:, :, 4 * k4:4 * k4 + 4, :],
                )
            raws[kk] = raw

        with tc.tile_pool(name="setup", bufs=1) as setup:
            a_src = attn.rearrange("b n (s q) c -> (b n s) (q c)", s=4)
            a_ld = setup.tile([P, 2, 16, W], BF16)
            a_raw = []
            for bp in range(2):
                raw = const.tile([P, PADA + 2048 + PADA], BF16, name="a_raw%d" % bp)
                nc.vector.memset(raw[:, 0:PADA], 0.0)
                nc.vector.memset(raw[:, PADA + 2048:], 0.0)
                a_raw.append(raw)

            def side_by_side(bp):
                return a_raw[bp][:, PADA:PADA + 2048].rearrange("p (q b c) -> p b q c", q=16, b=2)

            def load_weights(b, dst, eng):
                first = b * 4 * NN
                n = min(P, B * 4 * NN - first)
                eng.dma_start(out=dst[0:n], in_=a_src[first:first + n, :].rearrange("p (q c) -> p q c", c=W))
                if n < P:
                    eng.dma_start(out=dst[n:P], in_=a_src[0:P - n, :].rearrange("p (q c) -> p q c", c=W))

            load_weights(0, a_ld[:, 0], nc.scalar)
            load_weights(1, a_ld[:, 1], nc.sync)
            vw_sb = setup.tile([P, 4, CIN], BF16)
            nc.scalar.dma_start(out=vw_sb[:], in_=v_w.rearrange("(p t) k -> p t k", t=4))
            load_x(0)
            vb_raw = setup.tile([P, CV], BF16)
            nc.sync.dma_start(out=vb_raw[:], in_=v_b.partition_broadcast(P))
            w_sb = const.tile([P, CV], BF16)
            nc.sync.dma_start(out=w_sb[:], in_=w_w)
            wb_raw = const.tile([P, 1], BF16)
            with nc.allow_non_contiguous_dma(reason="one bias value to a partition"):
                nc.sync.dma_start(out=wb_raw[:], in_=w_b.rearrange("(p o) -> p o", o=1))
            zero = setup.tile([P, 1024], F32)
            nc.gpsimd.memset(zero[:], 0.0)
            nc.sync.dma_start(out=scratch(IMG_ROW, 0, 1024, P), in_=zero[:])
            load_weights(2, side_by_side(1)[:, 0], nc.sync)
            load_weights(3, side_by_side(1)[:, 1], nc.sync)

            ident_f = const.tile([P, P], F32)
            make_identity(nc, ident_f[:])
            ident_b = const.tile([P, P], BF16)
            nc.vector.tensor_copy(out=ident_b[:], in_=ident_f[:])
            nc.vector.tensor_copy(out=side_by_side(0), in_=a_ld[:])
            i3 = ident_f[:].rearrange("p (b c) -> p b c", b=2)
            msk = const.tile([P, 16], F32)
            perm = {0: ident_f[:]}
            for dc in (-4, -2, -1, 1, 2, 4):
                pm = const.tile([P, 2, W], F32, name="perm%d" % (dc + 4))
                e = abs(dc)
                if dc > 0:
                    nc.vector.tensor_copy(out=pm[:, :, 0:W - e], in_=i3[:, :, e:W])
                    nc.vector.tensor_copy(out=pm[:, :, W - e:W], in_=i3[:, :, 0:e])
                    nc.vector.tensor_reduce(out=msk[:, dc + 4:dc + 5], in_=i3[:, :, e:W], axis=AX.XY, op=ALU.add)
                else:
                    nc.vector.tensor_copy(out=pm[:, :, e:W], in_=i3[:, :, 0:W - e])
                    nc.vector.tensor_copy(out=pm[:, :, 0:e], in_=i3[:, :, W - e:W])
                    nc.vector.tensor_reduce(out=msk[:, dc + 4:dc + 5], in_=i3[:, :, 0:W - e], axis=AX.XY, op=ALU.add)
                perm[dc] = pm[:].rearrange("p b c -> p (b c)")

            scale_tiles = []
            for k in range(2):
                sc = const.tile([P, 2, 512], U8, align_bytes=64, name="scales%d" % k)
                nc.gpsimd.memset(sc[:].rearrange("p h w -> p (h w)").bitcast(I32), 0)
                scale_tiles.append(sc)

            s_tmp = const.tile([P, NN, 4, 8], F32)
            a_t, s_all, strip = [], [], []
            for k, (bp, q0, nq) in enumerate(BLOCKS):
                a_blk = const.tile([P, NN, 4, nq], F32, name="a_t%d" % k)
                s_blk = const.tile([P, 4, nq], F32, name="s_all%d" % k)
                p_blk = const.tile([P, 4, nq // 4, 2, 2, 9], F32, name="strip%d" % k)
                nc.gpsimd.memset(p_blk[:], 0.0)
                a_t.append(a_blk)
                s_all.append(s_blk)
                strip.append(p_blk)

            def place(g):
                bp, s, q = g // H, g % H // 16, g % 16
                for k, (b, q0, nq) in enumerate(BLOCKS):
                    if b == bp and q0 <= q < q0 + nq:
                        return k, q - q0, s

            def weight(g, n):
                k, q, s = place(g)
                return a_t[k][:, n, s, q:q + 1]

            def bias_weight(g):
                k, q, s = place(g)
                return s_all[k][:, s, q:q + 1]

            classes = [(0, 1, 9)]
            for l, d in enumerate(DILS):
                for j in (0, 2):
                    classes.append(((j - 1) * d, 9 * l + j, 3))

            def masked(on_scalar, dst, src, dc):
                if on_scalar and dc == 0:
                    nc.scalar.copy(out=dst, in_=src)
                elif on_scalar:
                    nc.scalar.activation(out=dst, in_=src, func=ACT.Copy, scale=msk[:, dc + 4:dc + 5])
                elif dc == 0:
                    nc.vector.tensor_copy(out=dst, in_=src)
                else:
                    nc.vector.tensor_scalar_mul(out=dst, in0=src, scalar1=msk[:, dc + 4:dc + 5])

            def prep_class(block, k, on_scalar):
                bp, q0, nq = BLOCKS[block]
                a_blk = a_t[block]
                if k == len(classes):
                    nc.vector.tensor_tensor(out=a_blk[:, 4], in0=a_blk[:, 4], in1=a_blk[:, 13], op=ALU.add)
                    nc.vector.tensor_tensor(out=a_blk[:, 4], in0=a_blk[:, 4], in1=a_blk[:, 22], op=ALU.add)
                    s_blk = strip[block][:].rearrange("p s k i j e -> p (s k) (i j) e")
                    p_blk = a_blk[:].rearrange("p n s (k i) -> p (s k) i n", i=4)
                    nc.vector.tensor_copy(out=s_blk[:, :, 0:4:3, 0:9:8], in_=p_blk[:, :, 0:2, 23:20:-2])
                    nc.vector.tensor_copy(out=s_blk[:, :, 0:4:3, 2:7:4], in_=p_blk[:, :, 0:2, 14:11:-2])
                    nc.vector.tensor_copy(out=s_blk[:, :, 0:4:3, 3:6], in_=p_blk[:, :, 0:2, 5:2:-1])
                    nc.vector.tensor_copy(out=s_blk[:, :, 2, 3:6], in_=p_blk[:, :, 0, 8:5:-1])
                    nc.vector.tensor_copy(out=s_blk[:, :, 1, 3:6], in_=p_blk[:, :, 1, 2::-1])
                    return
                dc, n0, cnt = classes[k]
                at_ps = ps_o.tile([P, 8, P], BF16, tag="o")
                for q in range(nq):
                    s0 = PADA + (q0 + q) * P - dc
                    nc.tensor.transpose(out=at_ps[:, q, :], in_=a_raw[bp][:, s0:s0 + P], identity=ident_b[:])
                view = at_ps[:, 0:nq].rearrange("p q (n s) -> p n s q", s=4)
                src = view[:, n0:n0 + 3 * cnt - 2:3]
                masked(on_scalar, a_blk[:, n0:n0 + 3 * cnt - 2:3], src, dc)
                if dc != 0:
                    return
                masked(on_scalar, s_tmp[:, n0:n0 + 3 * cnt - 2:3, :, 0:nq], src, 0)
                for odc, m0, ocnt in classes[1:]:
                    masked(on_scalar, s_tmp[:, m0:m0 + 7:3, :, 0:nq], view[:, m0:m0 + 7:3], -odc)
                for l, d in enumerate(DILS):
                    top, end = min(d - q0, nq), min(q0 + nq - (16 - d), nq)
                    if top > 0:
                        nc.vector.memset(s_tmp[:, 9 * l:9 * l + 3, 0, 0:top], 0.0)
                    if end > 0:
                        nc.vector.memset(s_tmp[:, 9 * l + 6:9 * l + 9, 3, nq - end:nq], 0.0)
                nc.vector.tensor_reduce(out=s_all[block][:], in_=s_tmp[:, :, :, 0:nq].rearrange("p n s q -> p s q n"), axis=AX.X, op=ALU.add)

            vw_perm = setup.tile([P, 4, 4, P], BF16)
            nc.vector.tensor_copy(out=vw_perm[:], in_=vw_sb[:].rearrange("a t (p j) -> a t j p", j=4))
            vw_grp = setup.tile([P, 4, P, 4], BF16, align_bytes=64)
            for t in range(4):
                tp = ps_o.tile([P, 8, P], BF16, tag="o")
                for j in range(4):
                    nc.tensor.transpose(out=tp[:, j, :], in_=vw_perm[:, t, j, :], identity=ident_b[:])
                grouped = tp[:, 0:4, :].rearrange("p j a -> p a j")
                if t % 2 == 0:
                    nc.vector.tensor_copy(out=vw_grp[:, t], in_=grouped)
                else:
                    nc.scalar.copy(out=vw_grp[:, t], in_=grouped)
            vwc = const.tile([P, CV], U32, align_bytes=64)
            vws = const.tile([P, CV], U8, align_bytes=64)
            nc.vector.quantize_mx(out=vwc[:].bitcast(FP8X4), scales=vws[:], in_=vw_grp[:].rearrange("p t a j -> p (t a j)"))
            vb_bc = const.tile([P, CV], F32)
            nc.vector.tensor_copy(out=vb_bc[:].rearrange("p (t a) -> p t a", t=4), in_=vb_raw[:].rearrange("p (a t) -> p t a", t=4))

            for k in range(len(classes) + 1):
                prep_class(0, k, k != 0)

        glpool = ctx.enter_context(tc.tile_pool(name="glpool", bufs=GL))
        chpool = ctx.enter_context(tc.tile_pool(name="chpool", bufs=37))
        lopool = ctx.enter_context(tc.tile_pool(name="lopool", bufs=8))
        pair = ctx.enter_context(tc.tile_pool(name="pair", bufs=2))
        pvals = ctx.enter_context(tc.tile_pool(name="pvals", bufs=4))
        bands = ctx.enter_context(tc.tile_pool(name="bands", bufs=3))
        opool = ctx.enter_context(tc.tile_pool(name="opool", bufs=2))

        def prep_w():
            w_perm = const.tile([P, 4, P], BF16)
            nc.vector.tensor_copy(out=w_perm[:], in_=w_sb[:].rearrange("a (p j) -> a j p", j=4))
            w_grp = const.tile([P, P, 4], BF16, align_bytes=64)
            tpw = ps_o.tile([P, 8, P], BF16, tag="o")
            for j in range(4):
                nc.tensor.transpose(out=tpw[:, j, :], in_=w_perm[:, j, :], identity=ident_b[:])
            nc.vector.tensor_copy(out=w_grp[:], in_=tpw[:, 0:4, :].rearrange("p j a -> p a j"))
            wc = const.tile([P, COUT], U32, align_bytes=64)
            ws = const.tile([P, COUT], U8, align_bytes=64)
            nc.vector.quantize_mx(out=wc[:].bitcast(FP8X4), scales=ws[:], in_=w_grp[:].rearrange("p a j -> p (a j)"))
            wb = const.tile([P, 1], F32)
            nc.vector.tensor_copy(out=wb[:], in_=wb_raw[:])
            return wc, ws, wb

        NT = 2 * H
        NG = NT // 4
        stages, codes, vps, vrow = {}, {}, {}, {}
        cht, lot, ctxs, ops = {}, {}, {}, {}
        bnd, pairs, pps, prow = {}, {}, {}, {}
        w_op = []

        def band_write(kk):
            k, q, s = place(4 * kk)
            for be in range(2):
                for i in range(2):
                    dst = scratch(IMG_ROW + 1, i * W * IMG_ROW + ((kk % 3) * 4 + be * 2) * SLOT, 2 * SLOT, W).rearrange("q (s w) -> q s w", w=SLOT)
                    nc.sync.dma_start(out=dst[:, :, 0:9], in_=strip[k][be * W:(be + 1) * W, s, q // 4, i])

        def band_read(kk):
            src = scratch(IMG_ROW, (kk % 3) * 4 * SLOT, 4 * SLOT, P).rearrange("q (s w) -> q s w", w=SLOT)
            bt = bands.tile([P, 4, W], F32)
            nc.sync.dma_start(out=bt[:], in_=src[:, :, 4:4 + W])
            bnd[kk] = bt

        def pair_codes(kk):
            qc, qs = codes[kk - 4]
            pc = pair.tile([P, 256], I32, align_bytes=64)
            ps = pair.tile([P, 256], U8, align_bytes=64)
            for be in range(2):
                nc.sync.dma_start(
                    out=pc[:, be * P:(be + 1) * P].rearrange("p (i c) -> p i c", i=2),
                    in_=qc[:, 0, 0:256].bitcast(I32).rearrange("p (i b c) -> p b i c", i=2, b=2)[:, be],
                )
                nc.sync.dma_start(
                    out=ps[:, be * P:(be + 1) * P].bitcast(I32).rearrange("p (i c) -> p i c", i=2),
                    in_=qs[:, 0, 0:256].bitcast(I32).rearrange("p (i b c) -> p b i c", i=2, b=2)[:, be],
                )
            pairs[kk] = (pc, ps)

        def pair_mx(kk, be, times):
            pc, ps = pairs[kk]
            if (kk, be) not in pps:
                p_ps = ps_o.tile([P, CV], F32, tag="o")
                pps[(kk, be)] = p_ps
            for k in range(times):
                nc.tensor.matmul_mx(
                    out=pps[(kk, be)][:],
                    lhsT=pc[:, be * P:(be + 1) * P].bitcast(FP8X4),
                    lhsT_scale=ps[:, be * P:(be + 1) * P],
                    rhs=vwc[:].bitcast(FP8X4),
                    rhs_scale=vws[:],
                    start=True,
                    stop=True,
                )

        def pair_out(kk, be):
            pv = pvals.tile([P, CV], F32)
            nc.scalar.copy(out=pv[:], in_=pps[(kk, be)][:])
            prow[(kk, be)] = pv

        def has_pair(kk):
            return 0 <= kk < NG and banded(4 * kk)

        def stage(kq):
            if kq not in stages:
                st = qin.tile([P, 2, 4, P, 4], BF16, align_bytes=64)
                stages[kq] = st
            return stages[kq]

        def inter_x(kk):
            nc.gpsimd.tensor_scalar(
                out=stage(kk - 4)[:, 0].rearrange("p i u j -> p (i u) j"),
                in0=raws[kk][:].rearrange("p j i b c -> p (i b c) j"),
                scalar1=1.0, scalar2=0.0, op0=ALU.mult, op1=ALU.add,
            )

        def quant(kq):
            qc = qout.tile([P, 2, 512], U32, align_bytes=64)
            qs = scale_tiles[kq % 2]
            lo, hi = (0 if kq + 4 < NG else 1), (2 if kq >= 0 else 1)
            nc.vector.quantize_mx(
                out=qc[:, lo:hi, :].rearrange("p h w -> p (h w)").bitcast(FP8X4),
                scales=qs[:, lo:hi, :].rearrange("p h w -> p (h w)"),
                in_=stages[kq][:, lo:hi].rearrange("p h i u j -> p (h i u j)"),
            )
            codes[kq] = (qc, qs)

        def value_mx(g, times):
            if not 0 <= g < NT:
                return
            qc, qs = codes[g // 4 - 4]
            i = g % 4
            if g not in vps:
                v_ps = ps_v.tile([P, CV], F32)
                vps[g] = v_ps
            for k in range(times):
                nc.tensor.matmul_mx(
                    out=vps[g][:],
                    lhsT=qc[:, 0, i * P:(i + 1) * P].bitcast(FP8X4),
                    lhsT_scale=qs[:, 0, i * P:(i + 1) * P],
                    rhs=vwc[:].bitcast(FP8X4),
                    rhs_scale=vws[:],
                    start=True,
                    stop=True,
                )

        def value_out(g):
            vp = vpool.tile([P, CV], F32)
            nc.scalar.copy(out=vp[:], in_=vps[g][:])
            vrow[g] = vp

        def product(pool_tile, g, term):
            dr, n = term
            nc.scalar.activation(out=pool_tile[:], in_=vrow[g + dr][:], func=ACT.Copy, scale=weight(g, n))

        def heads(g, after, own_row):
            if not 0 <= g < NT:
                return
            todo = [(dc, terms) for dc, terms, due in columns_for(g) if due == after]
            for dc, terms in todo:
                if (terms[0][0] == 0) == own_row:
                    ch = chpool.tile([P, CV], F32)
                    product(ch, g, terms[0])
                    cht.setdefault(g, []).append((ch[:], dc, terms[1:]))

        def macs_of(t):
            todo = []
            for back in (4, 2, 1, 0):
                for ch, dc, terms in cht.get(t - back, []):
                    todo.extend((ch, t - back, n) for dr, n in terms if dr == back)
            return todo

        def mac(t, ch, g, n):
            nc.vector.scalar_tensor_tensor(
                out=ch, in0=vps[t][:], scalar=weight(g, n), in1=ch,
                op0=ALU.mult, op1=ALU.add,
            )

        def gp_product(dst, src, factor):
            nc.gpsimd.tensor_scalar(out=dst, in0=src, scalar1=factor, scalar2=0.0, op0=ALU.mult, op1=ALU.add)

        def plain_sums(g):
            if not 0 <= g < NT:
                return
            acc = gacc.tile([P, 2, CV], F32)
            summed = [plain_for(g + i)[0] for i in range(2)]
            for i in range(2):
                gp_product(acc[:, i], vb_bc[:], bias_weight(g + i))
                cht.setdefault(g + i, []).append((acc[:, i], 0, plain_for(g + i)[1]))
            more = []
            for k in range(max(len(s) for s in summed)):
                tmp = gtmp.tile([P, 2, CV], F32)
                both = [i for i in range(2) if k < len(summed[i])]
                for i in both:
                    dr, n = summed[i][k]
                    gp_product(tmp[:, i], vrow[g + i + dr][:], weight(g + i, n))
                more.append((tmp, both[0], both[-1] + 1))
            for tmp, lo, hi in more:
                nc.gpsimd.tensor_tensor(out=acc[:, lo:hi], in0=acc[:, lo:hi], in1=tmp[:, lo:hi], op=ALU.add)

        def lones(g):
            for dr, n in plain_for(g)[3]:
                gl = glpool.tile([P, CV], F32)
                gp_product(gl[:], vrow[g + dr][:], weight(g, n))
                lot.setdefault(g, []).append(gl[:])
            for term in plain_for(g)[2]:
                lo = lopool.tile([P, CV], F32)
                product(lo, g, term)
                lot.setdefault(g, []).append(lo[:])

        def flush(g, row, extra):
            band, j = banded(g), g % 4
            if not band:
                ctx_ps = ps_o.tile([P, 4, P], F32, tag="o")
                ctxs[g] = [ctx_ps]
            elif j == 0:
                pair_a = ps_p.tile([P, 2, 2, P], F32)
                pair_b = ps_p.tile([P, 2, 2, P], F32)
                ctxs[g] = ctxs[g + 1] = [pair_a, pair_b]
            prods = [(ch, dc) for ch, dc, terms in cht[g]] + [(lo, 0) for lo in lot.get(g, [])]
            n = len(prods)
            first = band and j == 0
            parts = 2 if band else 3
            for part in range(parts):
                if part == 1 and extra is not None:
                    pair_mx(extra[0], extra[1], 1 if first else 2)
                else:
                    value_mx(row, 1 if first else 2)
                quarters, mine = range(4), prods[n * part // parts:n * (part + 1) // parts]
                if first:
                    quarters, mine = range(2 * part, 2 * part + 2), prods
                    for t in quarters:
                        for be in range(2):
                            nc.tensor.matmul(
                                out=ctxs[g][part][:, t % 2, :, be * W:(be + 1) * W], lhsT=prow[(g // 4, be)][:, t * P:(t + 1) * P],
                                rhs=bnd[g // 4][:, be * 2:be * 2 + 2, :], start=(t % 2 == 0 and be == 0), stop=False,
                            )
                for pt, dc in mine:
                    for t in quarters:
                        if band:
                            dst, last = ctxs[g][t // 2][:, t % 2, j, :], j == 1 and pt is prods[-1][0] and t % 2 == 1
                        else:
                            dst, last = ctxs[g][0][:, t, :], pt is prods[-1][0] and t == 3
                        nc.tensor.matmul(
                            out=dst, lhsT=pt[:, t * P:(t + 1) * P], rhs=perm[dc],
                            start=(pt is prods[0][0] and t == 0 and not band), stop=last, is_transpose=True,
                        )

        def evac(g):
            j = g % 4
            st = stage(g // 4)
            if not banded(g):
                nc.scalar.copy(out=st[:, 1, j], in_=ctxs[g][0][:].rearrange("p t u -> p u t"))
            elif j == 1:
                for half in range(2):
                    nc.scalar.copy(out=st[:, 1, 0:2, :, 2 * half:2 * half + 2], in_=ctxs[g][half][:].rearrange("p t j u -> p j u t"))

        def out_mx(kk):
            qc, qs = codes[kk]
            o_ps = ps_o.tile([P, 512], F32, tag="o")
            nc.tensor.matmul_mx(
                out=o_ps[:], lhsT=w_op[0][0][:].bitcast(FP8X4), lhsT_scale=w_op[0][1][:], rhs=qc[:, 1, :].bitcast(FP8X4), rhs_scale=qs[:, 1, :],
                start=True, stop=True,
            )
            ops[kk] = o_ps

        def out_store(kk):
            bp, r0 = kk // 16, (kk % 16) * 4
            o_sb = opool.tile([P, 2, 4, W], F32)
            nc.scalar.activation(
                out=o_sb[:].rearrange("p b r c -> p r b c"),
                in_=ops[kk][:].rearrange("p (r b c) -> p r b c", r=4, b=2),
                func=ACT.Identity, bias=w_op[0][2][:, 0:1],
            )
            nc.sync.dma_start(
                out=out[2 * bp:2 * bp + 2, :, r0:r0 + 4, :].rearrange("b o r c -> o b (r c)"),
                in_=o_sb[:].rearrange("p b r c -> p b (r c)"),
            )

        def slot(t):
            if t % 4 == 2 and 1 <= (t + 14) // 4 < NG:
                load_x((t + 14) // 4)
            if t % 4 == 0 and 0 <= (t + 8) // 4 < NG:
                inter_x((t + 8) // 4)
            if t % 4 == 3 and has_pair((t + 1) // 4):
                band_write((t + 1) // 4)
            if t % 4 == 1 and has_pair((t - 1) // 4):
                band_read((t - 1) // 4)
            heads(t + 1, -1, False)
            if t % 2 == 1:
                plain_sums(t + 1)
            if 0 <= t + 1 < NT:
                value_out(t + 1)
                heads(t + 1, -1, True)
            heads(t - 1, 1, False)
            if 0 <= t - 6 < NT:
                evac(t - 6)
            if t % 4 in (2, 3) and has_pair(t // 4):
                pair_out(t // 4, t % 4 - 2)
            heads(t - 3, 3, False)
            if 0 <= t - 3 < NT:
                lones(t - 3)
            if t % 4 == 1 and 0 <= (t - 13) // 4 < NG:
                out_store((t - 13) // 4)
            todo = macs_of(t) if 0 <= t < NT else []
            for ch, g, n in todo[:6]:
                mac(t, ch, g, n)
            if t % 4 == 2 and -4 <= (t - 10) // 4 < NG:
                quant((t - 10) // 4)
                if has_pair((t + 2) // 4):
                    pair_codes((t + 2) // 4)
            for ch, g, n in todo[6:]:
                mac(t, ch, g, n)
            extra = None
            if t % 4 in (1, 2) and has_pair(t // 4):
                extra = (t // 4, t % 4 - 1)
            if 0 <= t - 5 < NT:
                flush(t - 5, t + 2, extra)
            else:
                value_mx(t + 2, 1)
                if extra is not None:
                    pair_mx(extra[0], extra[1], 1)
            if t % 4 == 0 and 0 <= (t - 12) // 4 < NG:
                out_mx((t - 12) // 4)
            if t == 2:
                w_op.append(prep_w())
            if -1 <= t < 6:
                for i in range(PREP * (t + 1), min(PREP * (t + 2), 8 * len(BLOCKS) - 8)):
                    prep_class(1 + i // 8, i % 8, ON_S(i, t))

        with tc.manual_schedule(engines={mybir.EngineType.Pool}):
            for t in range(-14, 6):
                slot(t)
        with tc.manual_schedule(engines={mybir.EngineType.PE, mybir.EngineType.DVE, mybir.EngineType.Activation, mybir.EngineType.Pool}):
            for t in range(6, NT + 10):
                slot(t)
